import numpy as np
import ml_dtypes


def mxq(x, axis, fmt="e4m3"):
    dtype, down = {"e4m3": (ml_dtypes.float8_e4m3fn, 7), "e5m2": (ml_dtypes.float8_e5m2, 14)}[fmt]
    v = np.moveaxis(np.asarray(x, np.float32).astype(ml_dtypes.bfloat16).astype(np.float64), axis, -1)
    blocks = v.reshape(v.shape[:-1] + (-1, 32))
    amax = np.abs(blocks).max(-1, keepdims=True)
    byte = np.maximum(np.where(amax > 0, np.frexp(amax)[1] - 1 + 127, 0) - down, 1)
    scale = np.exp2(byte - 127.0)
    codes = (blocks / scale).astype(np.float32).astype(dtype).astype(np.float64)
    return np.moveaxis((codes * scale).reshape(v.shape), -1, axis)


WIDE = False


def mx_kscale(k):
    if not WIDE:
        return np.ones(k)
    levels = np.array([10, -10, 5, -5, 0])
    a = np.random.permutation(np.resize(levels, k // 512 * 4)).reshape(k // 512, 4)
    idx = np.arange(k)
    return np.exp2(a[idx // 512, idx % 128 // 32])


BF16 = ml_dtypes.bfloat16


def bf(x):
    return np.asarray(x, np.float32).astype(BF16)


def f64(x):
    return np.asarray(x).astype(np.float64)


E2M1 = np.array([0.0, 0.5, 1.0, 1.5, 2.0, 3.0, 4.0, 6.0, -0.0, -0.5, -1.0, -1.5, -2.0, -3.0, -4.0, -6.0])


def pack_weight(w, fmt):
    k, n = w.shape
    w = f64(bf(w)).reshape(k // 32, 32, n)
    amax = np.abs(w).max(1)
    if fmt == "e4m3":
        byte = np.frexp(amax)[1] - 1 + 127 - 7
    else:
        mant, ex = np.frexp(amax / 6.0)
        byte = np.where(mant > 0.5, ex, ex - 1) + 127
    byte = np.clip(np.where(amax > 0, byte, 1), 1, 254)
    scaled = (w * np.exp2(127.0 - byte)[:, None, :]).reshape(k, n).astype(np.float32)
    by_word = np.ascontiguousarray(scaled.reshape(k // 512, 128, 4, n).transpose(0, 1, 3, 2))
    if fmt == "e4m3":
        words = by_word.astype(ml_dtypes.float8_e4m3fn).view(np.uint8)
    else:
        c = by_word.astype(ml_dtypes.float4_e2m1fn).view(np.uint8) & 0xF
        words = c[..., 0::2] | (c[..., 1::2] << 4)
    return np.ascontiguousarray(words), np.ascontiguousarray(byte.astype(np.uint8).reshape(k // 512, 16, n))


def unpack_weight(words, scales, fmt):
    g, p, n, _ = words.shape
    if fmt == "e4m3":
        vals = np.ascontiguousarray(words).view(ml_dtypes.float8_e4m3fn).astype(np.float64)
    else:
        nib = np.empty((g, p, n, 4), np.uint8)
        nib[..., 0::2] = words & 0xF
        nib[..., 1::2] = words >> 4
        vals = E2M1[nib]
    vals = vals * np.repeat(np.exp2(scales.astype(np.float64) - 127.0), 8, axis=1)[..., None]
    return vals.transpose(0, 1, 3, 2).reshape(g * 512, n)


B, S, D, H = 1, 128, 2048, 4096
NS = int(round(np.log2(H)))


def erf(z):
    z = np.clip(z, -6.0, 6.0)
    z2 = 2.0 * z * z
    term = z.copy()
    tot = z.copy()
    for n in range(1, 130):
        term = term * (z2 / (2 * n + 1))
        tot = tot + term
    return 2.0 / np.sqrt(np.pi) * np.exp(-z * z) * tot


def gelu_exact(v):
    return 0.5 * v * (1.0 + erf(v / np.sqrt(2.0)))


def butterfly(y, weights, dim):
    lead = y.shape[:-1]
    for stage in range(weights.shape[0]):
        s = 2 ** stage
        nb = dim // (2 * s)
        yr = y.reshape(*lead, nb, 2, s)
        a = yr[..., 0, :]
        b = yr[..., 1, :]
        w = weights[stage].reshape(nb, s, 2, 2)
        na = w[..., 0, 0] * a + w[..., 0, 1] * b
        nb2 = w[..., 1, 0] * a + w[..., 1, 1] * b
        y = np.stack([na, nb2], axis=-2).reshape(*lead, dim)
    return y


def bfly_draw():
    g = np.random.standard_normal((NS, H // 2, 2, 2))
    return np.sign(g) * 0.58 + 0.15 * g


def setup_inputs():
    s, t = mx_kscale(D), mx_kscale(H)
    x = np.random.standard_normal((B, S, D)) * s
    W_exp = np.random.standard_normal((D, H)) / np.sqrt(D) / s[:, None]
    b_exp = np.random.standard_normal(H) * 0.1
    up_weights = bfly_draw()
    up_bias = np.random.standard_normal(H) * 0.1
    down_weights = bfly_draw()
    down_weights[NS - 1] = down_weights[NS - 1] * t.reshape(2, H // 2).T[:, :, None]
    W_con = np.random.standard_normal((H, D)) * 1.5 / np.sqrt(H) / t[:, None]
    b_con = np.random.standard_normal(D) * 0.1
    down_bias = np.random.standard_normal(D) * 0.1
    W_exp_words, W_exp_scales = pack_weight(W_exp, "e4m3")
    W_con_words, W_con_scales = pack_weight(W_con, "e4m3")
    return {"x": bf(x), "W_exp_words": W_exp_words, "W_exp_scales": W_exp_scales, "b_exp": bf(b_exp), "up_weights": bf(up_weights), "up_bias": bf(up_bias),
            "down_weights": bf(down_weights), "W_con_words": W_con_words, "W_con_scales": W_con_scales, "b_con": bf(b_con), "down_bias": bf(down_bias)}


def reference(x, W_exp_words, W_exp_scales, b_exp, up_weights, up_bias, down_weights, W_con_words, W_con_scales, b_con, down_bias):
    h = (mxq(f64(x), 2, "e4m3") @ unpack_weight(W_exp_words, W_exp_scales, "e4m3")) + f64(b_exp)
    h = butterfly(h, f64(up_weights), H)
    h = gelu_exact(h + f64(up_bias))
    h = butterfly(h, f64(down_weights), H)
    y = (mxq(h, 2, "e4m3") @ unpack_weight(W_con_words, W_con_scales, "e4m3")) + f64(b_con)
    return y + f64(down_bias)

@@ -1,0 +1,269 @@
+from contextlib import ExitStack
+
+import concourse.bass as bass
+import concourse.mybir as mybir
+import concourse.tile as tile
+from concourse.masks import make_identity
+
+F32 = mybir.dt.float32
+BF16 = mybir.dt.bfloat16
+I32 = mybir.dt.int32
+U32 = mybir.dt.uint32
+U8 = mybir.dt.uint8
+FP8X4 = mybir.dt.float8_e4m3fn_x4
+ALU = mybir.AluOpType
+ACT = mybir.ActivationFunctionType
+
+P = 128
+TOK = 128
+D_IN = 2048
+H = 4096
+NT = H // P
+FLOPS = 2 * 2 * TOK * D_IN * H + 24 * (H // 2) * 6 * TOK
+
+
+def tile_butterflymlp_w_kernel(
+    tc, x, W_exp_words, W_exp_scales, b_exp, up_weights, up_bias, down_weights, W_con_words, W_con_scales, b_con, down_bias, out
+):
+    nc = tc.nc
+    with ExitStack() as ctx:
+        const = ctx.enter_context(tc.tile_pool(name="const", bufs=1))
+        wpool = ctx.enter_context(tc.tile_pool(name="wpool", bufs=8))
+        dpool = ctx.enter_context(tc.tile_pool(name="dpool", bufs=3))
+
+        ident_f = const.tile([P, P], F32, name="ident_f")
+        make_identity(nc, ident_f[:])
+        ident_b = const.tile([P, P], BF16, name="ident_b")
+        make_identity(nc, ident_b[:])
+
+        pl_exp = const.tile([P, H], U8, name="pl_exp", align_bytes=64)
+        nc.vector.memset(pl_exp[:].bitcast(I32), 0)
+        pl_con = const.tile([P, 2, D_IN], U8, name="pl_con", align_bytes=64)
+        nc.vector.memset(pl_con[:].rearrange("p h n -> p (h n)").bitcast(I32), 0)
+
+        g_mats = [const.tile([P, NT, P], F32, name="g_up"), const.tile([P, NT, P], F32, name="g_down")]
+        wh32 = [const.tile([P, 80, 2, 2], F32, name="wh_up"), const.tile([P, 80, 2, 2], F32, name="wh_down")]
+        bias32 = const.tile([P, P], F32, name="bias32")
+        bsum = const.tile([P, D_IN], F32, name="bsum")
+        xq = const.tile([P, 4 * TOK], U32, name="xq", align_bytes=64)
+        xs = const.tile([P, 4 * TOK], U8, name="xs", align_bytes=64)
+        hq = const.tile([P, 8 * TOK], U32, name="hq", align_bytes=64)
+        hs = const.tile([P, 8 * TOK], U8, name="hs", align_bytes=64)
+
+        with ExitStack() as early:
+            tmp = early.enter_context(tc.tile_pool(name="tmp", bufs=1))
+            grp = early.enter_context(tc.tile_pool(name="grp", bufs=3))
+            psA = early.enter_context(tc.psum_pool(name="psA", bufs=2))
+
+            raw = tmp.tile([P, 7, 256], BF16, name="raw")
+            for b, w in enumerate((up_weights, down_weights)):
+                src = w[0:7].rearrange("s (c k) r l -> c s (k r l)", c=NT)
+                for h in range(2):
+                    nc.scalar.dma_start(out=raw[64 * h + 32 * b : 64 * h + 32 * b + 32, :, :], in_=src)
+            x_sb = tmp.tile([P, D_IN], BF16, name="x_sb", align_bytes=64)
+            nc.sync.dma_start(out=x_sb[:], in_=x.flatten_outer_dims())
+            vb = tmp.tile([P, P], BF16, name="vb")
+            nc.vector.memset(vb[64:128, :], 0.0)
+            nc.scalar.dma_start(out=vb[0:32, :], in_=b_exp.rearrange("(c p) -> c p", p=P))
+            nc.scalar.dma_start(out=vb[32:64, :], in_=up_bias.rearrange("(c p) -> c p", p=P))
+            zh = [tmp.tile([P, 512], BF16, name="zh_up"), tmp.tile([P, 512], BF16, name="zh_down")]
+            for b, w in enumerate((up_weights, down_weights)):
+                nc.vector.memset(zh[b][64:128, :], 0.0)
+                nc.scalar.dma_start(out=zh[b][0:80, :], in_=w[7:12].rearrange("s (k p) r l -> (s k) (p r l)", p=P))
+            for q in range(4):
+                nc.sync.dma_start(out=pl_exp[32 * q : 32 * q + 16, :].bitcast(I32), in_=W_exp_scales[:, 4 * q : 4 * q + 4, :].bitcast(I32))
+            bc_b = tmp.tile([P, D_IN], BF16, name="bc_b")
+            db_b = tmp.tile([P, D_IN], BF16, name="db_b")
+            nc.gpsimd.dma_start(out=bc_b[:], in_=b_con.partition_broadcast(P))
+            nc.gpsimd.dma_start(out=db_b[:], in_=down_bias.partition_broadcast(P))
+            nc.gpsimd.tensor_tensor(out=bsum[:], in0=bc_b[:], in1=db_b[:], op=ALU.add)
+
+            wx = []
+            for c8 in range(8):
+                t = wpool.tile([P, 4, 512], U32, name="wx%d" % c8, tag="w", align_bytes=64)
+                nc.sync.dma_start(
+                    out=t[:].bitcast(I32),
+                    in_=W_exp_words[:, :, 512 * c8 : 512 * (c8 + 1), :].rearrange("g p n t -> p g (n t)").bitcast(I32),
+                )
+                wx.append(t)
+
+            xw = x_sb[:].bitcast(F32)
+            xg = tmp.tile([P, 4, TOK, 4], BF16, name="xg", align_bytes=64)
+            for h in range(2):
+                px = psA.tile([P, 2, 2, TOK], F32, name="px", tag="tp")
+                for g2 in range(2):
+                    g = 2 * h + g2
+                    for u in range(2):
+                        nc.tensor.transpose(out=px[:, g2, u, :], in_=xw[:, 256 * g + u : 256 * (g + 1) : 2], identity=ident_f[:])
+                nc.vector.tensor_copy(out=xg[:, 2 * h : 2 * h + 2, :, :].bitcast(F32), in_=px[:].rearrange("p g u q -> p g q u"))
+            nc.vector.quantize_mx(out=xq[:].bitcast(FP8X4), scales=xs[:], in_=xg[:].rearrange("p g q t -> p (g q t)"))
+
+            pb = psA.tile([P, P], BF16, name="pb", tag="tp")
+            nc.tensor.transpose(out=pb[:], in_=vb[:], identity=ident_b[:])
+            nc.vector.tensor_copy(out=bias32[:], in_=pb[:])
+            for b in range(2):
+                pz = psA.tile([P, 2, P], F32, name="pz", tag="tp")
+                zw = zh[b][:].bitcast(F32)
+                for r in range(2):
+                    nc.tensor.transpose(out=pz[:, r, :], in_=zw[:, r:256:2], identity=ident_f[:])
+                nc.vector.tensor_copy(out=wh32[b][:], in_=pz[:].bitcast(BF16).rearrange("p r (w l) -> p w r l", l=2)[:, 0:80, :, :])
+
+            fp = tmp.tile([P, 7, 256], BF16, name="fp")
+            for s in range(6):
+                nc.vector.tensor_copy(
+                    out=fp[:, s, :].rearrange("p (r b a l) -> p r b a l", r=2, b=2**s, a=2 ** (6 - s), l=2),
+                    in_=raw[:, s, :].rearrange("p (a b r l) -> p r b a l", a=2 ** (6 - s), b=2**s, r=2, l=2),
+                )
+            for h in range(2):
+                nc.vector.tensor_copy(
+                    out=fp[64 * h : 64 * h + 64, 6, 0:128].rearrange("p (b l) -> p b l", l=2),
+                    in_=raw[64 * h : 64 * h + 64, 6, :].rearrange("p (b r l) -> p b r l", r=2, l=2)[:, :, h, :],
+                )
+            xprev = fp[:, 0, :]
+            for s in (1, 2):
+                xn = tmp.tile([P, 128 * 2 ** (s + 1)], F32, name="xrec%d" % s)
+                shp = [P, 2, 128, 2**s]
+                nc.vector.tensor_tensor(
+                    out=xn[:].rearrange("p (u m w) -> p u m w", u=2, w=2**s),
+                    in0=xprev.rearrange("p (m w) -> p m w", w=2**s).unsqueeze(1).to_broadcast(shp),
+                    in1=fp[:, s, :].rearrange("p (u m) -> p u m", u=2).unsqueeze(3).to_broadcast(shp),
+                    op=ALU.mult,
+                )
+                xprev = xn[:]
+            yprev = fp[:, 6, 0:128]
+            for s in (5, 4, 3):
+                yn = tmp.tile([P, 64 * 2 ** (7 - s)], F32, name="yrec%d" % s)
+                u = 2 ** (5 - s)
+                shp = [P, u, 128, 2]
+                nc.vector.tensor_tensor(
+                    out=yn[:].rearrange("p (u m w) -> p u m w", u=u, w=2),
+                    in0=yprev.rearrange("p (u m) -> p u m", u=u).unsqueeze(3).to_broadcast(shp),
+                    in1=fp[:, s, :].rearrange("p (m w) -> p m w", w=2).unsqueeze(1).to_broadcast(shp),
+                    op=ALU.mult,
+                )
+                yprev = yn[:]
+            for u in range(8):
+                gr = grp.tile([P, 1024], F32, name="gr", tag="gr")
+                nc.vector.tensor_tensor(
+                    out=gr[:].rearrange("p (m w) -> p m w", w=8),
+                    in0=xprev.rearrange("p (m w) -> p m w", w=8),
+                    in1=yprev[:, 128 * u : 128 * (u + 1)].unsqueeze(2).to_broadcast([P, 128, 8]),
+                    op=ALU.mult,
+                )
+                for vh in range(2):
+                    pt = psA.tile([P, 4, P], F32, name="pt", tag="tp")
+                    for sl in range(4):
+                        v = 4 * vh + sl
+                        nc.tensor.transpose(out=pt[:, sl, :], in_=gr[:, 128 * v : 128 * (v + 1)], identity=ident_f[:])
+                    il0 = 8 * u + 4 * vh
+                    for b in range(2):
+                        dst = g_mats[b][:].rearrange("p c (h i) -> p c h i", h=2)[:, :, :, il0 : il0 + 4]
+                        src = pt[:].rearrange("p s (h b c) -> p b c h s", h=2, b=2)[:, b]
+                        if b == 0:
+                            nc.scalar.copy(out=dst, in_=src)
+                        else:
+                            nc.vector.tensor_copy(out=dst, in_=src)
+
+            h0 = dpool.tile([P, NT, TOK], F32, name="h0", tag="d")
+            pe_banks = []
+            for c8 in range(8):
+                pm = psA.tile([P, 4, TOK], F32, name="pm", tag="mx")
+                for cl in range(4):
+                    c = 4 * c8 + cl
+                    for g in range(4):
+                        nc.tensor.matmul_mx(
+                            out=pm[:, cl, :],
+                            lhsT=wx[c8][:, g, 128 * cl : 128 * (cl + 1)].bitcast(FP8X4),
+                            lhsT_scale=pl_exp[4 * g : 128, 128 * c : 128 * (c + 1)],
+                            rhs=xq[:, 128 * g : 128 * (g + 1)].bitcast(FP8X4),
+                            rhs_scale=xs[:, 128 * g : 128 * (g + 1)],
+                            start=(g == 0),
+                            stop=(g == 3),
+                        )
+                for cl in range(4):
+                    c = 4 * c8 + cl
+                    if cl % 2 == 0:
+                        nc.scalar.activation(out=h0[:, c, :], in_=pm[:, cl, :], func=ACT.Identity, bias=bias32[:, c : c + 1], scale=1.0)
+                    else:
+                        nc.vector.tensor_scalar(out=h0[:, c, :], in0=pm[:, cl, :], scalar1=bias32[:, c : c + 1], scalar2=None, op0=ALU.add)
+
+            def pair_tiles(s5, k):
+                lo = k & (2**s5 - 1)
+                ca = ((k >> s5) << (s5 + 1)) + lo
+                return ca, ca + 2**s5
+
+            def ew_pair(dst, a, b, ca, cb, wh, row):
+                nc.scalar.activation(out=dst[:, ca, :], in_=a, func=ACT.Copy, scale=wh[:, row, 0, 0:1])
+                nc.scalar.activation(out=dst[:, cb, :], in_=b, func=ACT.Copy, scale=wh[:, row, 1, 1:2])
+                nc.vector.scalar_tensor_tensor(out=dst[:, ca, :], in0=b, scalar=wh[:, row, 0, 1:2], in1=dst[:, ca, :], op0=ALU.mult, op1=ALU.add)
+                nc.vector.scalar_tensor_tensor(out=dst[:, cb, :], in0=a, scalar=wh[:, row, 1, 0:1], in1=dst[:, cb, :], op0=ALU.mult, op1=ALU.add)
+
+            def butterfly(src, which):
+                y = dpool.tile([P, NT, TOK], F32, name="y7", tag="d")
+                for c4 in range(8):
+                    pe = psA.tile([P, 4, TOK], F32, name="pe", tag="pe", bufs=3)
+                    for cl in range(4):
+                        c = 4 * c4 + cl
+                        nc.tensor.matmul(out=pe[:, cl, :], lhsT=g_mats[which][:, c, :], rhs=src[:, c, :], start=True, stop=True)
+                    for kk in range(2):
+                        k = 2 * c4 + kk
+                        ca, cb = pair_tiles(0, k)
+                        ew_pair(y, pe[:, ca % 4, :], pe[:, cb % 4, :], ca, cb, wh32[which], k)
+                for s5 in range(1, 5):
+                    yn = dpool.tile([P, NT, TOK], F32, name="yn", tag="d")
+                    for k in range(16):
+                        ca, cb = pair_tiles(s5, k)
+                        ew_pair(yn, y[:, ca, :], y[:, cb, :], ca, cb, wh32[which], 16 * s5 + k)
+                    y = yn
+                return y
+
+            h1 = butterfly(h0, 0)
+            gl = dpool.tile([P, NT, TOK], F32, name="gl", tag="d")
+            for c in range(NT):
+                nc.scalar.activation(out=gl[:, c, :], in_=h1[:, c, :], func=ACT.Gelu, bias=bias32[:, 32 + c : 33 + c], scale=1.0)
+            h2 = butterfly(gl, 1)
+
+        for h in range(2):
+            for q in range(4):
+                nc.sync.dma_start(
+                    out=pl_con[32 * q : 32 * q + 16, h, :].bitcast(I32), in_=W_con_scales[4 * h : 4 * h + 4, 4 * q : 4 * q + 4, :].bitcast(I32)
+                )
+        wc = []
+        for g in range(8):
+            t = wpool.tile([P, D_IN], U32, name="wc%d" % g, tag="w", align_bytes=64)
+            nc.sync.dma_start(out=t[:].bitcast(I32), in_=W_con_words[g].rearrange("p n t -> p (n t)").bitcast(I32))
+            wc.append(t)
+
+        with ExitStack() as late:
+            lpool = late.enter_context(tc.tile_pool(name="lpool", bufs=2))
+            psC = late.enter_context(tc.psum_pool(name="psC", bufs=2))
+            acc = [psC.tile([P, 512], F32, name="acc%d" % n4, tag="acc%d" % n4, bufs=1) for n4 in range(4)]
+            for g in range(8):
+                p1 = psC.tile([P, 4, P], F32, name="p1", tag="p1")
+                for cl in range(4):
+                    nc.tensor.transpose(out=p1[:, cl, :], in_=h2[:, 4 * g + cl, :], identity=ident_f[:])
+                t2 = lpool.tile([P, 4, P], F32, name="t2", tag="t2")
+                nc.scalar.copy(out=t2[:], in_=p1[:].rearrange("q c p -> q (c p)").rearrange("q (m t) -> q t m", t=4))
+                p2 = psC.tile([P, 4, TOK], F32, name="p2", tag="p2")
+                for t in range(4):
+                    nc.tensor.transpose(out=p2[:, t, :], in_=t2[:, t, :], identity=ident_f[:])
+                hb = lpool.tile([P, TOK, 4], BF16, name="hb", tag="hb", align_bytes=64)
+                nc.vector.tensor_copy(out=hb[:], in_=p2[:].rearrange("m t q -> m q t"))
+                nc.vector.quantize_mx(
+                    out=hq[:, 128 * g : 128 * (g + 1)].bitcast(FP8X4), scales=hs[:, 128 * g : 128 * (g + 1)], in_=hb[:].rearrange("m q t -> m (q t)")
+                )
+                for n4 in range(4):
+                    nc.tensor.matmul_mx(
+                        out=acc[n4][:],
+                        lhsT=hq[:, 128 * g : 128 * (g + 1)].bitcast(FP8X4),
+                        lhsT_scale=hs[:, 128 * g : 128 * (g + 1)],
+                        rhs=wc[g][:, 512 * n4 : 512 * (n4 + 1)].bitcast(FP8X4),
+                        rhs_scale=pl_con[4 * (g % 4) : 128, g // 4, 512 * n4 : 512 * (n4 + 1)],
+                        start=(g == 0),
+                        stop=(g == 7),
+                    )
+            out2 = out.flatten_outer_dims()
+            for n4 in range(4):
+                o_sb = lpool.tile([P, 512], F32, name="o_sb", tag="o_sb")
+                nc.vector.tensor_tensor(out=o_sb[:], in0=acc[n4][:], in1=bsum[:, 512 * n4 : 512 * (n4 + 1)], op=ALU.add)
+                nc.sync.dma_start(out=out2[:, 512 * n4 : 512 * (n4 + 1)], in_=o_sb[:])

@@ -29,55 +29,52 @@ def tile_butterflymlp_w_kernel(
     with ExitStack() as ctx:
         const = ctx.enter_context(tc.tile_pool(name="const", bufs=1))
         wpool = ctx.enter_context(tc.tile_pool(name="wpool", bufs=8))
-        dpool = ctx.enter_context(tc.tile_pool(name="dpool", bufs=3))
+        psum = ctx.enter_context(tc.psum_pool(name="psum", bufs=1))
+
+        def bank(i, shape, dtype=F32):
+            return psum.tile(shape, dtype, name="bk%d" % i, tag="bk%d" % i)
 
         ident_f = const.tile([P, P], F32, name="ident_f")
         make_identity(nc, ident_f[:])
         ident_b = const.tile([P, P], BF16, name="ident_b")
         make_identity(nc, ident_b[:])
-
         pl_exp = const.tile([P, H], U8, name="pl_exp", align_bytes=64)
         nc.vector.memset(pl_exp[:].bitcast(I32), 0)
         pl_con = const.tile([P, 2, D_IN], U8, name="pl_con", align_bytes=64)
-        nc.vector.memset(pl_con[:].rearrange("p h n -> p (h n)").bitcast(I32), 0)
-
         g_mats = [const.tile([P, NT, P], F32, name="g_up"), const.tile([P, NT, P], F32, name="g_down")]
+        g3 = const.tile([P, 32, P], F32, name="g3")
         wh32 = [const.tile([P, 80, 2, 2], F32, name="wh_up"), const.tile([P, 80, 2, 2], F32, name="wh_down")]
         bias32 = const.tile([P, P], F32, name="bias32")
-        bsum = const.tile([P, D_IN], F32, name="bsum")
         xq = const.tile([P, 4 * TOK], U32, name="xq", align_bytes=64)
         xs = const.tile([P, 4 * TOK], U8, name="xs", align_bytes=64)
-        hq = const.tile([P, 8 * TOK], U32, name="hq", align_bytes=64)
-        hs = const.tile([P, 8 * TOK], U8, name="hs", align_bytes=64)
+        buf_a = const.tile([P, NT, TOK], F32, name="buf_a")
+        buf_b = const.tile([P, NT, TOK], F32, name="buf_b")
+        buf_c = const.tile([P, NT, TOK], F32, name="buf_c")
+        bsum = const.tile([P, D_IN], F32, name="bsum")
 
-        with ExitStack() as early:
-            tmp = early.enter_context(tc.tile_pool(name="tmp", bufs=1))
-            grp = early.enter_context(tc.tile_pool(name="grp", bufs=3))
-            psA = early.enter_context(tc.psum_pool(name="psA", bufs=2))
+        with tc.tile_pool(name="tmp", bufs=1) as tmp, tc.tile_pool(name="grp", bufs=4) as grp:
+            bw = (up_weights, down_weights)
+            raw = [tmp.tile([P, 7, 256], BF16, name="raw_up"), tmp.tile([P, 7, 256], BF16, name="raw_down")]
 
-            raw = tmp.tile([P, 7, 256], BF16, name="raw")
-            for b, w in enumerate((up_weights, down_weights)):
-                src = w[0:7].rearrange("s (c k) r l -> c s (k r l)", c=NT)
-                for h in range(2):
-                    nc.scalar.dma_start(out=raw[64 * h + 32 * b : 64 * h + 32 * b + 32, :, :], in_=src)
-            x_sb = tmp.tile([P, D_IN], BF16, name="x_sb", align_bytes=64)
+            def load_raw(b):
+                src = bw[b][0:7].rearrange("s (c k) r l -> c s (k r l)", c=NT)
+                for h in range(4):
+                    nc.scalar.dma_start(out=raw[b][32 * h : 32 * h + 32, :, :], in_=src)
+
+            load_raw(0)
+            x_sb = grp.tile([P, D_IN], BF16, name="x_sb", tag="gr", align_bytes=64)
             nc.sync.dma_start(out=x_sb[:], in_=x.flatten_outer_dims())
             vb = tmp.tile([P, P], BF16, name="vb")
             nc.vector.memset(vb[64:128, :], 0.0)
-            nc.scalar.dma_start(out=vb[0:32, :], in_=b_exp.rearrange("(c p) -> c p", p=P))
-            nc.scalar.dma_start(out=vb[32:64, :], in_=up_bias.rearrange("(c p) -> c p", p=P))
             zh = [tmp.tile([P, 512], BF16, name="zh_up"), tmp.tile([P, 512], BF16, name="zh_down")]
-            for b, w in enumerate((up_weights, down_weights)):
+            for b in range(2):
                 nc.vector.memset(zh[b][64:128, :], 0.0)
-                nc.scalar.dma_start(out=zh[b][0:80, :], in_=w[7:12].rearrange("s (k p) r l -> (s k) (p r l)", p=P))
+            nc.vector.memset(pl_con[:].rearrange("p h n -> p (h n)").bitcast(I32), 0)
             for q in range(4):
                 nc.sync.dma_start(out=pl_exp[32 * q : 32 * q + 16, :].bitcast(I32), in_=W_exp_scales[:, 4 * q : 4 * q + 4, :].bitcast(I32))
-            bc_b = tmp.tile([P, D_IN], BF16, name="bc_b")
-            db_b = tmp.tile([P, D_IN], BF16, name="db_b")
-            nc.gpsimd.dma_start(out=bc_b[:], in_=b_con.partition_broadcast(P))
-            nc.gpsimd.dma_start(out=db_b[:], in_=down_bias.partition_broadcast(P))
-            nc.gpsimd.tensor_tensor(out=bsum[:], in0=bc_b[:], in1=db_b[:], op=ALU.add)
-
+            nc.scalar.dma_start(out=vb[0:32, :], in_=b_exp.rearrange("(c p) -> c p", p=P))
+            nc.scalar.dma_start(out=vb[32:64, :], in_=up_bias.rearrange("(c p) -> c p", p=P))
+            nc.scalar.dma_start(out=zh[0][0:80, :], in_=bw[0][7:12].rearrange("s (k p) r l -> (s k) (p r l)", p=P))
             wx = []
             for c8 in range(8):
                 t = wpool.tile([P, 4, 512], U32, name="wx%d" % c8, tag="w", align_bytes=64)
@@ -86,88 +83,129 @@ def tile_butterflymlp_w_kernel(
                     in_=W_exp_words[:, :, 512 * c8 : 512 * (c8 + 1), :].rearrange("g p n t -> p g (n t)").bitcast(I32),
                 )
                 wx.append(t)
+                if c8 == 1:
+                    load_raw(1)
+                    nc.scalar.dma_start(out=zh[1][0:80, :], in_=bw[1][7:12].rearrange("s (k p) r l -> (s k) (p r l)", p=P))
 
-            xw = x_sb[:].bitcast(F32)
-            xg = tmp.tile([P, 4, TOK, 4], BF16, name="xg", align_bytes=64)
-            for h in range(2):
-                px = psA.tile([P, 2, 2, TOK], F32, name="px", tag="tp")
-                for g2 in range(2):
-                    g = 2 * h + g2
-                    for u in range(2):
-                        nc.tensor.transpose(out=px[:, g2, u, :], in_=xw[:, 256 * g + u : 256 * (g + 1) : 2], identity=ident_f[:])
-                nc.vector.tensor_copy(out=xg[:, 2 * h : 2 * h + 2, :, :].bitcast(F32), in_=px[:].rearrange("p g u q -> p g q u"))
-            nc.vector.quantize_mx(out=xq[:].bitcast(FP8X4), scales=xs[:], in_=xg[:].rearrange("p g q t -> p (g q t)"))
+            def copy_on(eng, o, i):
+                if eng == 0:
+                    nc.vector.tensor_copy(out=o, in_=i)
+                else:
+                    nc.scalar.copy(out=o, in_=i)
 
-            pb = psA.tile([P, P], BF16, name="pb", tag="tp")
-            nc.tensor.transpose(out=pb[:], in_=vb[:], identity=ident_b[:])
-            nc.vector.tensor_copy(out=bias32[:], in_=pb[:])
-            for b in range(2):
-                pz = psA.tile([P, 2, P], F32, name="pz", tag="tp")
+            fp = tmp.tile([P, 7, 256], BF16, name="fp")
+
+            def g_copies(b, stages, eng):
+                for s in stages:
+                    if s <= 4:
+                        o = fp[:, s, :].rearrange("p (r b a l) -> p r b a l", r=2, b=2**s, a=2 ** (6 - s), l=2)
+                        i = raw[b][:, s, :].rearrange("p (a b r l) -> p r b a l", a=2 ** (6 - s), b=2**s, r=2, l=2)
+                        if eng == 0:
+                            nc.vector.tensor_copy(out=o, in_=i)
+                        else:
+                            for r in range(2):
+                                nc.scalar.copy(out=o[:, r], in_=i[:, r])
+                    elif s == 5:
+                        for h in range(4):
+                            q = slice(32 * h, 32 * h + 32)
+                            copy_on(
+                                eng,
+                                fp[q, 5, 0:128].rearrange("p (b a l) -> p b a l", b=32, a=2, l=2),
+                                raw[b][q, 5, :].rearrange("p (a b r l) -> p r b a l", a=2, b=32, r=2, l=2)[:, h % 2],
+                            )
+                    else:
+                        for h in range(4):
+                            q = slice(32 * h, 32 * h + 32)
+                            copy_on(
+                                eng,
+                                fp[q, 6, 0:64].rearrange("p (b l) -> p b l", l=2),
+                                raw[b][q, 6, :].rearrange("p (t b r l) -> p t r b l", t=2, b=32, r=2, l=2)[:, h % 2, h // 2],
+                            )
+
+            xrec = [None, tmp.tile([P, 512], F32, name="xrec1"), tmp.tile([P, 1024], F32, name="xrec2")]
+            yrec = {5: tmp.tile([P, 128], F32, name="yrec5"), 4: tmp.tile([P, 256], F32, name="yrec4"), 3: tmp.tile([P, 512], F32, name="yrec3")}
+
+            def g_x(ve):
+                prev = fp[:, 0, :]
+                for s in (1, 2):
+                    shp = [P, 2, 128, 2**s]
+                    ve.tensor_tensor(
+                        out=xrec[s][:].rearrange("p (u m w) -> p u m w", u=2, w=2**s),
+                        in0=prev.rearrange("p (m w) -> p m w", w=2**s).unsqueeze(1).to_broadcast(shp),
+                        in1=fp[:, s, :].rearrange("p (u m) -> p u m", u=2).unsqueeze(3).to_broadcast(shp),
+                        op=ALU.mult,
+                    )
+                    prev = xrec[s][:]
+
+            def g_y(ve):
+                prev = fp[:, 6, 0:64]
+                for s in (5, 4, 3):
+                    u = 2 if s == 3 else 1
+                    m = 64 if s == 5 else 128
+                    shp = [P, u, m, 2]
+                    ve.tensor_tensor(
+                        out=yrec[s][:].rearrange("p (u m w) -> p u m w", u=u, w=2),
+                        in0=prev.rearrange("p (u m) -> p u m", u=u).unsqueeze(3).to_broadcast(shp),
+                        in1=fp[:, s, 0 : 2 * m].rearrange("p (m w) -> p m w", w=2).unsqueeze(1).to_broadcast(shp),
+                        op=ALU.mult,
+                    )
+                    prev = yrec[s][:]
+
+            grs = {}
+
+            def g_prod(u, ve):
+                gr = grp.tile([P, 1024], F32, name="gr", tag="gr", align_bytes=64)
+                ve.tensor_tensor(
+                    out=gr[:].rearrange("p (m w) -> p m w", w=8),
+                    in0=xrec[2][:].rearrange("p (m w) -> p m w", w=8),
+                    in1=yrec[3][:, 128 * u : 128 * (u + 1)].unsqueeze(2).to_broadcast([P, 128, 8]),
+                    op=ALU.mult,
+                )
+                grs[u] = gr
+
+            def g_out(b, u, banks, eng):
+                for vh in range(2):
+                    pt = bank(banks[vh], [P, 4, P])
+                    for sl in range(4):
+                        v = 4 * vh + sl
+                        nc.tensor.transpose(out=pt[:, sl, :], in_=grs[u][:, 128 * v : 128 * (v + 1)], identity=ident_f[:])
+                    il0 = 8 * u + 4 * vh
+                    copy_on(
+                        eng,
+                        g_mats[b][:].rearrange("p c (h i) -> p c h i", h=4)[:, :, :, il0 : il0 + 4],
+                        pt[:].rearrange("p s (h c) -> p c h s", h=4),
+                    )
+
+            def wh_path(b, bk):
+                pz = bank(bk, [P, 2, P])
                 zw = zh[b][:].bitcast(F32)
                 for r in range(2):
                     nc.tensor.transpose(out=pz[:, r, :], in_=zw[:, r:256:2], identity=ident_f[:])
                 nc.vector.tensor_copy(out=wh32[b][:], in_=pz[:].bitcast(BF16).rearrange("p r (w l) -> p w r l", l=2)[:, 0:80, :, :])
 
-            fp = tmp.tile([P, 7, 256], BF16, name="fp")
-            for s in range(6):
-                nc.vector.tensor_copy(
-                    out=fp[:, s, :].rearrange("p (r b a l) -> p r b a l", r=2, b=2**s, a=2 ** (6 - s), l=2),
-                    in_=raw[:, s, :].rearrange("p (a b r l) -> p r b a l", a=2 ** (6 - s), b=2**s, r=2, l=2),
-                )
+            g_copies(0, (0, 1, 2), 0)
+            g_copies(0, (6, 5, 4, 3), 1)
+            g_x(nc.vector)
+            xw = x_sb[:].bitcast(F32)
+            xg = grp.tile([P, 4, TOK, 4], BF16, name="xg", tag="gr", align_bytes=64)
             for h in range(2):
-                nc.vector.tensor_copy(
-                    out=fp[64 * h : 64 * h + 64, 6, 0:128].rearrange("p (b l) -> p b l", l=2),
-                    in_=raw[64 * h : 64 * h + 64, 6, :].rearrange("p (b r l) -> p b r l", r=2, l=2)[:, :, h, :],
-                )
-            xprev = fp[:, 0, :]
-            for s in (1, 2):
-                xn = tmp.tile([P, 128 * 2 ** (s + 1)], F32, name="xrec%d" % s)
-                shp = [P, 2, 128, 2**s]
-                nc.vector.tensor_tensor(
-                    out=xn[:].rearrange("p (u m w) -> p u m w", u=2, w=2**s),
-                    in0=xprev.rearrange("p (m w) -> p m w", w=2**s).unsqueeze(1).to_broadcast(shp),
-                    in1=fp[:, s, :].rearrange("p (u m) -> p u m", u=2).unsqueeze(3).to_broadcast(shp),
-                    op=ALU.mult,
-                )
-                xprev = xn[:]
-            yprev = fp[:, 6, 0:128]
-            for s in (5, 4, 3):
-                yn = tmp.tile([P, 64 * 2 ** (7 - s)], F32, name="yrec%d" % s)
-                u = 2 ** (5 - s)
-                shp = [P, u, 128, 2]
-                nc.vector.tensor_tensor(
-                    out=yn[:].rearrange("p (u m w) -> p u m w", u=u, w=2),
-                    in0=yprev.rearrange("p (u m) -> p u m", u=u).unsqueeze(3).to_broadcast(shp),
-                    in1=fp[:, s, :].rearrange("p (m w) -> p m w", w=2).unsqueeze(1).to_broadcast(shp),
-                    op=ALU.mult,
-                )
-                yprev = yn[:]
-            for u in range(8):
-                gr = grp.tile([P, 1024], F32, name="gr", tag="gr")
-                nc.vector.tensor_tensor(
-                    out=gr[:].rearrange("p (m w) -> p m w", w=8),
-                    in0=xprev.rearrange("p (m w) -> p m w", w=8),
-                    in1=yprev[:, 128 * u : 128 * (u + 1)].unsqueeze(2).to_broadcast([P, 128, 8]),
-                    op=ALU.mult,
-                )
-                for vh in range(2):
-                    pt = psA.tile([P, 4, P], F32, name="pt", tag="tp")
-                    for sl in range(4):
-                        v = 4 * vh + sl
-                        nc.tensor.transpose(out=pt[:, sl, :], in_=gr[:, 128 * v : 128 * (v + 1)], identity=ident_f[:])
-                    il0 = 8 * u + 4 * vh
-                    for b in range(2):
-                        dst = g_mats[b][:].rearrange("p c (h i) -> p c h i", h=2)[:, :, :, il0 : il0 + 4]
-                        src = pt[:].rearrange("p s (h b c) -> p b c h s", h=2, b=2)[:, b]
-                        if b == 0:
-                            nc.scalar.copy(out=dst, in_=src)
-                        else:
-                            nc.vector.tensor_copy(out=dst, in_=src)
+                px = bank(h, [P, 2, 2, TOK])
+                for g2 in range(2):
+                    g = 2 * h + g2
+                    for u in range(2):
+                        nc.tensor.transpose(out=px[:, g2, u, :], in_=xw[:, 256 * g + u : 256 * (g + 1) : 2], identity=ident_f[:])
+                nc.scalar.copy(out=xg[:, 2 * h : 2 * h + 2, :, :].bitcast(F32), in_=px[:].rearrange("p g u q -> p g q u"))
+            g_y(nc.vector)
+            nc.vector.quantize_mx(out=xq[:].bitcast(FP8X4), scales=xs[:], in_=xg[:].rearrange("p g q t -> p (g q t)"))
+            pb = bank(7, [P, P], BF16)
+            nc.tensor.transpose(out=pb[:], in_=vb[:], identity=ident_b[:])
+            nc.scalar.copy(out=bias32[:], in_=pb[:])
+            wh_path(0, 6)
 
-            h0 = dpool.tile([P, NT, TOK], F32, name="h0", tag="d")
-            pe_banks = []
-            for c8 in range(8):
-                pm = psA.tile([P, 4, TOK], F32, name="pm", tag="mx")
+            h0s = {}
+
+            def mx1(c8):
+                pm = bank(2 + c8 % 2, [P, 4, TOK])
                 for cl in range(4):
                     c = 4 * c8 + cl
                     for g in range(4):
@@ -180,75 +218,204 @@ def tile_butterflymlp_w_kernel(
                             start=(g == 0),
                             stop=(g == 3),
                         )
+                h0 = tmp.tile([P, 4, TOK], F32, name="h0", tag="h0", bufs=3)
                 for cl in range(4):
                     c = 4 * c8 + cl
                     if cl % 2 == 0:
-                        nc.scalar.activation(out=h0[:, c, :], in_=pm[:, cl, :], func=ACT.Identity, bias=bias32[:, c : c + 1], scale=1.0)
+                        nc.scalar.activation(out=h0[:, cl, :], in_=pm[:, cl, :], func=ACT.Identity, bias=bias32[:, c : c + 1], scale=1.0)
                     else:
-                        nc.vector.tensor_scalar(out=h0[:, c, :], in0=pm[:, cl, :], scalar1=bias32[:, c : c + 1], scalar2=None, op0=ALU.add)
+                        nc.vector.tensor_scalar(out=h0[:, cl, :], in0=pm[:, cl, :], scalar1=bias32[:, c : c + 1], scalar2=None, op0=ALU.add)
+                h0s[c8] = h0
+
+            pes = {}
+
+            def pe1(c8):
+                pe = bank(4 + c8 % 3, [P, 4, TOK])
+                for cl in range(4):
+                    nc.tensor.matmul(out=pe[:, cl, :], lhsT=g_mats[0][:, 4 * c8 + cl, :], rhs=h0s[c8][:, cl, :], start=True, stop=True)
+                pes[c8] = pe
 
             def pair_tiles(s5, k):
                 lo = k & (2**s5 - 1)
                 ca = ((k >> s5) << (s5 + 1)) + lo
                 return ca, ca + 2**s5
 
-            def ew_pair(dst, a, b, ca, cb, wh, row):
+            ew_bufs = [None, buf_a, buf_b, buf_a, buf_b, buf_a]
+
+            def ew(s5, k):
+                ca, cb = pair_tiles(s5, k)
+                wh = wh32[0]
+                row = 16 * s5 + k
+                dst = ew_bufs[s5 + 1]
+                if s5 == 0:
+                    a, b = pes[ca // 4][:, ca % 4, :], pes[ca // 4][:, cb % 4, :]
+                else:
+                    a, b = ew_bufs[s5][:, ca, :], ew_bufs[s5][:, cb, :]
                 nc.scalar.activation(out=dst[:, ca, :], in_=a, func=ACT.Copy, scale=wh[:, row, 0, 0:1])
                 nc.scalar.activation(out=dst[:, cb, :], in_=b, func=ACT.Copy, scale=wh[:, row, 1, 1:2])
                 nc.vector.scalar_tensor_tensor(out=dst[:, ca, :], in0=b, scalar=wh[:, row, 0, 1:2], in1=dst[:, ca, :], op0=ALU.mult, op1=ALU.add)
                 nc.vector.scalar_tensor_tensor(out=dst[:, cb, :], in0=a, scalar=wh[:, row, 1, 0:1], in1=dst[:, cb, :], op0=ALU.mult, op1=ALU.add)
 
-            def butterfly(src, which):
-                y = dpool.tile([P, NT, TOK], F32, name="y7", tag="d")
-                for c4 in range(8):
-                    pe = psA.tile([P, 4, TOK], F32, name="pe", tag="pe", bufs=3)
-                    for cl in range(4):
-                        c = 4 * c4 + cl
-                        nc.tensor.matmul(out=pe[:, cl, :], lhsT=g_mats[which][:, c, :], rhs=src[:, c, :], start=True, stop=True)
-                    for kk in range(2):
-                        k = 2 * c4 + kk
-                        ca, cb = pair_tiles(0, k)
-                        ew_pair(y, pe[:, ca % 4, :], pe[:, cb % 4, :], ca, cb, wh32[which], k)
-                for s5 in range(1, 5):
-                    yn = dpool.tile([P, NT, TOK], F32, name="yn", tag="d")
-                    for k in range(16):
-                        ca, cb = pair_tiles(s5, k)
-                        ew_pair(yn, y[:, ca, :], y[:, cb, :], ca, cb, wh32[which], 16 * s5 + k)
-                    y = yn
-                return y
+            g_prod(0, nc.vector)
+            g_prod(1, nc.vector)
+            g_out(0, 0, (0, 1), 1)
+            mx1(0)
+            g_prod(2, nc.vector)
+            g_out(0, 1, (7, 0), 1)
+            g_prod(3, nc.vector)
+            g_out(0, 2, (1, 7), 1)
+            mx1(1)
+            g_out(0, 3, (0, 1), 1)
 
-            h1 = butterfly(h0, 0)
-            gl = dpool.tile([P, NT, TOK], F32, name="gl", tag="d")
-            for c in range(NT):
-                nc.scalar.activation(out=gl[:, c, :], in_=h1[:, c, :], func=ACT.Gelu, bias=bias32[:, 32 + c : 33 + c], scale=1.0)
-            h2 = butterfly(gl, 1)
+            qmask = tmp.tile([P, 4], F32, name="qmask")
+            fh = xrec[1][:, 0:320].rearrange("p (s e) -> p s e", s=5)
+            hx = yrec[5]
+            hys = {3: yrec[4][:, 0:128], 2: yrec[3][:, 0:256]}
+            hmat = xrec[2]
 
-        for h in range(2):
-            for q in range(4):
-                nc.sync.dma_start(
-                    out=pl_con[32 * q : 32 * q + 16, h, :].bitcast(I32), in_=W_con_scales[4 * h : 4 * h + 4, 4 * q : 4 * q + 4, :].bitcast(I32)
+            def g3_small():
+                nc.vector.tensor_reduce(out=qmask[:], in_=ident_f[:].rearrange("p (x u) -> p x u", x=4), axis=mybir.AxisListType.X, op=ALU.add)
+                for s in range(5):
+                    nc.gpsimd.tensor_copy(
+                        out=fh[:, s, :].rearrange("p (r b a l) -> p r b a l", r=2, b=2**s, a=2 ** (4 - s), l=2),
+                        in_=wh32[1][:, 16 * s : 16 * (s + 1), :, :].rearrange("p (a b) r l -> p r b a l", a=2 ** (4 - s), b=2**s),
+                    )
+                nc.gpsimd.tensor_tensor(
+                    out=hx[:].rearrange("p (u m w) -> p u m w", u=2, w=2),
+                    in0=fh[:, 0, :].rearrange("p (m w) -> p m w", w=2).unsqueeze(1).to_broadcast([P, 2, 32, 2]),
+                    in1=fh[:, 1, :].rearrange("p (u m) -> p u m", u=2).unsqueeze(3).to_broadcast([P, 2, 32, 2]),
+                    op=ALU.mult,
                 )
-        wc = []
-        for g in range(8):
-            t = wpool.tile([P, D_IN], U32, name="wc%d" % g, tag="w", align_bytes=64)
-            nc.sync.dma_start(out=t[:].bitcast(I32), in_=W_con_words[g].rearrange("p n t -> p (n t)").bitcast(I32))
-            wc.append(t)
+                hyprev = fh[:, 4, :]
+                for s in (3, 2):
+                    hy = hys[s]
+                    u = 2 ** (4 - s)
+                    nc.gpsimd.tensor_tensor(
+                        out=hy[:].rearrange("p (u m w) -> p u m w", u=u, w=2),
+                        in0=hyprev.rearrange("p (u m) -> p u m", u=u).unsqueeze(3).to_broadcast([P, u, 32, 2]),
+                        in1=fh[:, s, :].rearrange("p (m w) -> p m w", w=2).unsqueeze(1).to_broadcast([P, u, 32, 2]),
+                        op=ALU.mult,
+                    )
+                    hyprev = hy[:]
+                nc.gpsimd.tensor_tensor(
+                    out=hmat[:].rearrange("p (u m w) -> p u m w", u=8, w=4),
+                    in0=hx[:].rearrange("p (m w) -> p m w", w=4).unsqueeze(1).to_broadcast([P, 8, 32, 4]),
+                    in1=hyprev.rearrange("p (u m) -> p u m", u=8).unsqueeze(3).to_broadcast([P, 8, 32, 4]),
+                    op=ALU.mult,
+                )
 
-        with ExitStack() as late:
-            lpool = late.enter_context(tc.tile_pool(name="lpool", bufs=2))
-            psC = late.enter_context(tc.psum_pool(name="psC", bufs=2))
-            acc = [psC.tile([P, 512], F32, name="acc%d" % n4, tag="acc%d" % n4, bufs=1) for n4 in range(4)]
+
+            g2_tasks = [
+                lambda: (g_copies(1, (0, 1, 2, 6, 5, 4, 3), 1), wh_path(1, 0)),
+                lambda: (g_x(nc.gpsimd), g_y(nc.gpsimd)),
+                lambda: g_prod(0, nc.gpsimd),
+                lambda: g_prod(1, nc.gpsimd),
+                lambda: (g_prod(2, nc.gpsimd), g_out(1, 0, (0, 1), 0)),
+                lambda: (g_prod(3, nc.gpsimd), g_out(1, 1, (7, 0), 0)),
+                lambda: (g_out(1, 2, (1, 7), 0), g3_small()),
+                lambda: g_out(1, 3, (0, 1), 0),
+            ]
+            for c8 in range(8):
+                if c8 + 2 < 8:
+                    mx1(c8 + 2)
+                pe1(c8)
+                for k in (2 * c8, 2 * c8 + 1):
+                    ew(0, k)
+                for k in (2 * c8, 2 * c8 + 1):
+                    ew(1, k)
+                if c8 % 2 == 1:
+                    for k in range(2 * c8 - 2, 2 * c8 + 2):
+                        ew(2, k)
+                if c8 % 4 == 3:
+                    for k in range(2 * c8 - 6, 2 * c8 + 2):
+                        ew(3, k)
+                g2_tasks[c8]()
+
+            bc_b = g_mats[0][:, 16:24, :].rearrange("p c i -> p (c i)").bitcast(BF16)
+            db_b = g_mats[0][:, 24:32, :].rearrange("p c i -> p (c i)").bitcast(BF16)
+            nc.gpsimd.dma_start(out=bc_b, in_=b_con.partition_broadcast(P))
+            nc.gpsimd.dma_start(out=db_b, in_=down_bias.partition_broadcast(P))
+            nc.gpsimd.tensor_tensor(out=bsum[:], in0=bc_b, in1=db_b, op=ALU.add)
+
+            for h in range(2):
+                for q in range(4):
+                    nc.sync.dma_start(
+                        out=pl_con[32 * q : 32 * q + 16, h, :].bitcast(I32), in_=W_con_scales[4 * h : 4 * h + 4, 4 * q : 4 * q + 4, :].bitcast(I32)
+                    )
+            wc = []
             for g in range(8):
-                p1 = psC.tile([P, 4, P], F32, name="p1", tag="p1")
-                for cl in range(4):
-                    nc.tensor.transpose(out=p1[:, cl, :], in_=h2[:, 4 * g + cl, :], identity=ident_f[:])
-                t2 = lpool.tile([P, 4, P], F32, name="t2", tag="t2")
-                nc.scalar.copy(out=t2[:], in_=p1[:].rearrange("q c p -> q (c p)").rearrange("q (m t) -> q t m", t=4))
-                p2 = psC.tile([P, 4, TOK], F32, name="p2", tag="p2")
+                t = wpool.tile([P, D_IN], U32, name="wc%d" % g, tag="w", align_bytes=64)
+                nc.sync.dma_start(out=t[:].bitcast(I32), in_=W_con_words[g].rearrange("p n t -> p (n t)").bitcast(I32))
+                wc.append(t)
+
+            gl = buf_b
+            ta = buf_c
+            for q in range(4):
+                pe_lo = bank(4 + 2 * (q % 2), [P, 4, P])
+                pe_hi = bank(5 + 2 * (q % 2), [P, 4, P])
+                for k in range(4 * q, 4 * q + 4):
+                    ew(4, k)
+                    for c, pe in ((k, pe_lo), (k + 16, pe_hi)):
+                        nc.scalar.activation(out=gl[:, c, :], in_=buf_a[:, c, :], func=ACT.Gelu, bias=bias32[:, 32 + c : 33 + c], scale=1.0)
+                        nc.tensor.matmul(out=pe[:, c % 4, :], lhsT=gl[:, c, :], rhs=g_mats[1][:, c, :], start=True, stop=True)
+                for g, pe, eng in ((q, pe_lo, 1), (q + 4, pe_hi, 0)):
+                    copy_on(
+                        eng,
+                        ta[:].rearrange("q u (x c) -> q u x c", x=4)[:, :, :, 4 * g : 4 * g + 4],
+                        pe[:].rearrange("q c (x u) -> q u x c", x=4),
+                    )
+
+            def g3_part(q, bk):
+                ex = tmp.tile([P, 4, 4, 32], F32, name="ex", tag="ex", bufs=2)
+                nc.gpsimd.tensor_tensor(
+                    out=ex[:],
+                    in0=hmat[:, 128 * q : 128 * (q + 1)].rearrange("p (i j) -> p i j", i=4).unsqueeze(2).to_broadcast([P, 4, 4, 32]),
+                    in1=qmask[:].unsqueeze(1).unsqueeze(3).to_broadcast([P, 4, 4, 32]),
+                    op=ALU.mult,
+                )
+                pt = bank(bk, [P, 4, P])
+                for sl in range(4):
+                    nc.tensor.transpose(out=pt[:, sl, :], in_=ex[:, sl, :, :].rearrange("p x j -> p (x j)"), identity=ident_f[:])
+                nc.scalar.copy(
+                    out=g3[:, :, 16 * q : 16 * (q + 1)].rearrange("p u (s x) -> p u s x", s=4),
+                    in_=pt[:].rearrange("p s (x u) -> p u s x", x=4),
+                )
+
+            d2 = buf_a
+
+            def p2_part(u4, bk, eng):
+                pt = bank(bk, [P, 4, TOK])
+                for sl in range(4):
+                    nc.tensor.transpose(out=pt[:, sl, :], in_=ta[:, 4 * u4 + sl, :], identity=ident_f[:])
+                copy_on(eng, d2[:, 4 * u4 : 4 * u4 + 4, :], pt[:])
+
+            for i in range(8):
+                p2_part(i, i % 2, i % 2)
+                g3_part(i, 2 + i % 2)
+
+            t2 = buf_b.rearrange("q (g t) m -> q g t m", t=4)
+            for t in range(4):
+                for f4 in range(2):
+                    pe = bank(4 + (2 * t + f4) % 4, [P, 4, P])
+                    for sl in range(4):
+                        u = 16 * f4 + 4 * sl + t
+                        nc.tensor.matmul(out=pe[:, sl, :], lhsT=d2[:, u, :], rhs=g3[:, u, :], start=True, stop=True)
+                    copy_on(
+                        t % 2,
+                        t2[:, :, t, :].rearrange("q g (a f s) -> q g a f s", a=16, f=2)[:, :, :, f4, :],
+                        pe[:].rearrange("q s (g a) -> q g a s", g=8),
+                    )
+
+        with tc.tile_pool(name="lpool", bufs=2) as lpool:
+            hq = lpool.tile([P, 8 * TOK], U32, name="hq", bufs=1, align_bytes=64)
+            hs = lpool.tile([P, 8 * TOK], U8, name="hs", bufs=1, align_bytes=64)
+            acc = [bank(n4, [P, 512]) for n4 in range(4)]
+            for g in range(8):
+                p2 = bank(4 + g % 4, [P, 4, TOK])
                 for t in range(4):
-                    nc.tensor.transpose(out=p2[:, t, :], in_=t2[:, t, :], identity=ident_f[:])
+                    nc.tensor.transpose(out=p2[:, t, :], in_=t2[:, g, t, :], identity=ident_f[:])
                 hb = lpool.tile([P, TOK, 4], BF16, name="hb", tag="hb", align_bytes=64)
-                nc.vector.tensor_copy(out=hb[:], in_=p2[:].rearrange("m t q -> m q t"))
+                copy_on(g % 2, hb[:], p2[:].rearrange("m t q -> m q t"))
                 nc.vector.quantize_mx(
                     out=hq[:, 128 * g : 128 * (g + 1)].bitcast(FP8X4), scales=hs[:, 128 * g : 128 * (g + 1)], in_=hb[:].rearrange("m q t -> m (q t)")
                 )

@@ -51,6 +51,7 @@ def tile_butterflymlp_w_kernel(
         buf_b = const.tile([P, NT, TOK], F32, name="buf_b")
         buf_c = const.tile([P, NT, TOK], F32, name="buf_c")
         bsum = const.tile([P, D_IN], F32, name="bsum")
+        w7f = const.tile([P, 16, 2, 2], F32, name="w7f")
 
         with tc.tile_pool(name="tmp", bufs=1) as tmp, tc.tile_pool(name="grp", bufs=4) as grp:
             bw = (up_weights, down_weights)
@@ -86,6 +87,12 @@ def tile_butterflymlp_w_kernel(
                 if c8 == 1:
                     load_raw(1)
                     nc.scalar.dma_start(out=zh[1][0:80, :], in_=bw[1][7:12].rearrange("s (k p) r l -> (s k) (p r l)", p=P))
+
+            w7raw = tmp.tile([P, 4, 16], BF16, name="w7raw")
+            w7src = bw[1][7].rearrange("(c h z t) r l -> h c z (t r l)", c=16, h=4, z=8)
+            for h in range(4):
+                nc.scalar.dma_start(out=w7raw[:, h, :], in_=w7src[h])
+            nc.gpsimd.tensor_copy(out=w7f[:].rearrange("p a r l -> p (a r l)"), in_=w7raw[:].rearrange("p h e -> p (h e)"))
 
             def copy_on(eng, o, i):
                 if eng == 0:
@@ -176,12 +183,12 @@ def tile_butterflymlp_w_kernel(
                         pt[:].rearrange("p s (h c) -> p c h s", h=4),
                     )
 
-            def wh_path(b, bk):
+            def wh_path(b, bk, eng):
                 pz = bank(bk, [P, 2, P])
                 zw = zh[b][:].bitcast(F32)
                 for r in range(2):
                     nc.tensor.transpose(out=pz[:, r, :], in_=zw[:, r:256:2], identity=ident_f[:])
-                nc.vector.tensor_copy(out=wh32[b][:], in_=pz[:].bitcast(BF16).rearrange("p r (w l) -> p w r l", l=2)[:, 0:80, :, :])
+                copy_on(eng, wh32[b][:], pz[:].bitcast(BF16).rearrange("p r (w l) -> p w r l", l=2)[:, 0:80, :, :])
 
             g_copies(0, (0, 1, 2), 0)
             g_copies(0, (6, 5, 4, 3), 1)
@@ -200,9 +207,10 @@ def tile_butterflymlp_w_kernel(
             pb = bank(7, [P, P], BF16)
             nc.tensor.transpose(out=pb[:], in_=vb[:], identity=ident_b[:])
             nc.scalar.copy(out=bias32[:], in_=pb[:])
-            wh_path(0, 6)
+            wh_path(0, 6, 1)
 
             h0s = {}
+            pms = {}
 
             def mx1(c8):
                 pm = bank(2 + c8 % 2, [P, 4, TOK])
@@ -218,13 +226,13 @@ def tile_butterflymlp_w_kernel(
                             start=(g == 0),
                             stop=(g == 3),
                         )
+                pms[c8] = pm
+
+            def e1(c8):
                 h0 = tmp.tile([P, 4, TOK], F32, name="h0", tag="h0", bufs=3)
-                for cl in range(4):
-                    c = 4 * c8 + cl
-                    if cl % 2 == 0:
-                        nc.scalar.activation(out=h0[:, cl, :], in_=pm[:, cl, :], func=ACT.Identity, bias=bias32[:, c : c + 1], scale=1.0)
-                    else:
-                        nc.vector.tensor_scalar(out=h0[:, cl, :], in0=pm[:, cl, :], scalar1=bias32[:, c : c + 1], scalar2=None, op0=ALU.add)
+                nc.vector.tensor_tensor(
+                    out=h0[:], in0=pms[c8][:], in1=bias32[:, 4 * c8 : 4 * c8 + 4].unsqueeze(2).to_broadcast([P, 4, TOK]), op=ALU.add
+                )
                 h0s[c8] = h0
 
             pes = {}
@@ -242,19 +250,37 @@ def tile_butterflymlp_w_kernel(
 
             ew_bufs = [None, buf_a, buf_b, buf_a, buf_b, buf_a]
 
-            def ew(s5, k):
-                ca, cb = pair_tiles(s5, k)
-                wh = wh32[0]
-                row = 16 * s5 + k
-                dst = ew_bufs[s5 + 1]
+            def ew_src(s5, c):
                 if s5 == 0:
-                    a, b = pes[ca // 4][:, ca % 4, :], pes[ca // 4][:, cb % 4, :]
+                    return pes[c // 4][:, c % 4, :]
+                return ew_bufs[s5][:, c, :]
+
+            def ew_p(s5, k, side):
+                c = pair_tiles(s5, k)[side]
+                if s5 == 4:
+                    nc.scalar.activation(
+                        out=ew_bufs[5][:, c, :], in_=ew_src(4, c), func=ACT.Identity, scale=wh32[0][:, 64 + k, side, side : side + 1], bias=bias32[:, 32 + c : 33 + c]
+                    )
                 else:
-                    a, b = ew_bufs[s5][:, ca, :], ew_bufs[s5][:, cb, :]
-                nc.scalar.activation(out=dst[:, ca, :], in_=a, func=ACT.Copy, scale=wh[:, row, 0, 0:1])
-                nc.scalar.activation(out=dst[:, cb, :], in_=b, func=ACT.Copy, scale=wh[:, row, 1, 1:2])
-                nc.vector.scalar_tensor_tensor(out=dst[:, ca, :], in0=b, scalar=wh[:, row, 0, 1:2], in1=dst[:, ca, :], op0=ALU.mult, op1=ALU.add)
-                nc.vector.scalar_tensor_tensor(out=dst[:, cb, :], in0=a, scalar=wh[:, row, 1, 0:1], in1=dst[:, cb, :], op0=ALU.mult, op1=ALU.add)
+                    nc.scalar.activation(out=ew_bufs[s5 + 1][:, c, :], in_=ew_src(s5, c), func=ACT.Copy, scale=wh32[0][:, 16 * s5 + k, side, side : side + 1])
+
+            def ew_v(s5, k, side):
+                cs = pair_tiles(s5, k)
+                dst = ew_bufs[s5 + 1][:, cs[side], :]
+                nc.vector.scalar_tensor_tensor(
+                    out=dst, in0=ew_src(s5, cs[1 - side]), scalar=wh32[0][:, 16 * s5 + k, side, 1 - side : 2 - side], in1=dst, op0=ALU.mult, op1=ALU.add
+                )
+
+            def wave(ops, sides=(0, 1)):
+                for s5, k in ops:
+                    for side in sides:
+                        ew_p(s5, k, side)
+                return ops
+
+            def wave_v(ops):
+                for s5, k in ops:
+                    for side in (0, 1):
+                        ew_v(s5, k, side)
 
             g_prod(0, nc.vector)
             g_prod(1, nc.vector)
@@ -262,74 +288,114 @@ def tile_butterflymlp_w_kernel(
             mx1(0)
             g_prod(2, nc.vector)
             g_out(0, 1, (7, 0), 1)
+            mx1(1)
             g_prod(3, nc.vector)
             g_out(0, 2, (1, 7), 1)
-            mx1(1)
+            e1(0)
             g_out(0, 3, (0, 1), 1)
+            e1(1)
 
-            qmask = tmp.tile([P, 4], F32, name="qmask")
-            fh = xrec[1][:, 0:320].rearrange("p (s e) -> p s e", s=5)
-            hx = yrec[5]
-            hys = {3: yrec[4][:, 0:128], 2: yrec[3][:, 0:256]}
-            hmat = xrec[2]
+            zmask = tmp.tile([P, 8], F32, name="zmask")
+            fh = xrec[1][:, 0:256].rearrange("p (s f e) -> p s f e", s=4, f=2)
+            hx = yrec[5][:, 0:128].rearrange("p (f e) -> p f e", f=2)
+            hy = yrec[4][:, 0:128].rearrange("p (f e) -> p f e", f=2)
+            hmat = xrec[2][:, 0:512]
 
             def g3_small():
-                nc.vector.tensor_reduce(out=qmask[:], in_=ident_f[:].rearrange("p (x u) -> p x u", x=4), axis=mybir.AxisListType.X, op=ALU.add)
-                for s in range(5):
-                    nc.gpsimd.tensor_copy(
-                        out=fh[:, s, :].rearrange("p (r b a l) -> p r b a l", r=2, b=2**s, a=2 ** (4 - s), l=2),
-                        in_=wh32[1][:, 16 * s : 16 * (s + 1), :, :].rearrange("p (a b) r l -> p r b a l", a=2 ** (4 - s), b=2**s),
-                    )
-                nc.gpsimd.tensor_tensor(
-                    out=hx[:].rearrange("p (u m w) -> p u m w", u=2, w=2),
-                    in0=fh[:, 0, :].rearrange("p (m w) -> p m w", w=2).unsqueeze(1).to_broadcast([P, 2, 32, 2]),
-                    in1=fh[:, 1, :].rearrange("p (u m) -> p u m", u=2).unsqueeze(3).to_broadcast([P, 2, 32, 2]),
-                    op=ALU.mult,
-                )
-                hyprev = fh[:, 4, :]
-                for s in (3, 2):
-                    hy = hys[s]
-                    u = 2 ** (4 - s)
+                nc.vector.tensor_reduce(out=zmask[:], in_=ident_f[:].rearrange("p (h z t) -> p z h t", h=4, z=8), axis=mybir.AxisListType.XY, op=ALU.add)
+                for s in range(4):
+                    for f in range(2):
+                        nc.gpsimd.tensor_copy(
+                            out=fh[:, s, f, :].rearrange("p (r b a l) -> p r b a l", r=2, b=2**s, a=2 ** (3 - s), l=2),
+                            in_=wh32[1][:, 16 * (s + 1) : 16 * (s + 2), :, :].rearrange("p (a b f) r l -> p f r b a l", a=2 ** (3 - s), b=2**s, f=2)[:, f],
+                        )
+                for f in range(2):
                     nc.gpsimd.tensor_tensor(
-                        out=hy[:].rearrange("p (u m w) -> p u m w", u=u, w=2),
-                        in0=hyprev.rearrange("p (u m) -> p u m", u=u).unsqueeze(3).to_broadcast([P, u, 32, 2]),
-                        in1=fh[:, s, :].rearrange("p (m w) -> p m w", w=2).unsqueeze(1).to_broadcast([P, u, 32, 2]),
+                        out=hx[:, f, :].rearrange("p (u m w) -> p u m w", u=2, w=2),
+                        in0=fh[:, 0, f, :].rearrange("p (m w) -> p m w", w=2).unsqueeze(1).to_broadcast([P, 2, 16, 2]),
+                        in1=fh[:, 1, f, :].rearrange("p (u m) -> p u m", u=2).unsqueeze(3).to_broadcast([P, 2, 16, 2]),
                         op=ALU.mult,
                     )
-                    hyprev = hy[:]
+                    nc.gpsimd.tensor_tensor(
+                        out=hy[:, f, :].rearrange("p (u m w) -> p u m w", u=2, w=2),
+                        in0=fh[:, 3, f, :].rearrange("p (u m) -> p u m", u=2).unsqueeze(3).to_broadcast([P, 2, 16, 2]),
+                        in1=fh[:, 2, f, :].rearrange("p (m w) -> p m w", w=2).unsqueeze(1).to_broadcast([P, 2, 16, 2]),
+                        op=ALU.mult,
+                    )
+                    nc.gpsimd.tensor_tensor(
+                        out=hmat[:, 256 * f : 256 * (f + 1)].rearrange("p (u m w) -> p u m w", u=4, w=4),
+                        in0=hx[:, f, :].rearrange("p (m w) -> p m w", w=4).unsqueeze(1).to_broadcast([P, 4, 16, 4]),
+                        in1=hy[:, f, :].rearrange("p (u m) -> p u m", u=4).unsqueeze(3).to_broadcast([P, 4, 16, 4]),
+                        op=ALU.mult,
+                    )
+
+            exs = {}
+
+            def g3_prod(q):
+                ex = tmp.tile([P, 512], F32, name="ex", tag="ex", bufs=2)
                 nc.gpsimd.tensor_tensor(
-                    out=hmat[:].rearrange("p (u m w) -> p u m w", u=8, w=4),
-                    in0=hx[:].rearrange("p (m w) -> p m w", w=4).unsqueeze(1).to_broadcast([P, 8, 32, 4]),
-                    in1=hyprev.rearrange("p (u m) -> p u m", u=8).unsqueeze(3).to_broadcast([P, 8, 32, 4]),
+                    out=ex[:].rearrange("p (a z) -> p a z", z=8),
+                    in0=hmat[:, 64 * q : 64 * (q + 1)].unsqueeze(2).to_broadcast([P, 64, 8]),
+                    in1=zmask[:].unsqueeze(1).to_broadcast([P, 64, 8]),
                     op=ALU.mult,
                 )
+                exs[q] = ex
 
+            def g3_out(q, bk):
+                pt = bank(bk, [P, 4, P])
+                for sl in range(4):
+                    nc.tensor.transpose(out=pt[:, sl, :], in_=exs[q][:, 128 * sl : 128 * (sl + 1)], identity=ident_f[:])
+                nc.vector.tensor_copy(
+                    out=g3[:].rearrange("p (f h t) (i z) -> p f h t i z", f=2, h=4, z=8)[:, q // 4, :, :, 4 * (q % 4) : 4 * (q % 4) + 4, :],
+                    in_=pt[:].rearrange("p s (h z t) -> p h t s z", h=4, z=8),
+                )
 
-            g2_tasks = [
-                lambda: (g_copies(1, (0, 1, 2, 6, 5, 4, 3), 1), wh_path(1, 0)),
-                lambda: (g_x(nc.gpsimd), g_y(nc.gpsimd)),
-                lambda: g_prod(0, nc.gpsimd),
-                lambda: g_prod(1, nc.gpsimd),
-                lambda: (g_prod(2, nc.gpsimd), g_out(1, 0, (0, 1), 0)),
-                lambda: (g_prod(3, nc.gpsimd), g_out(1, 1, (7, 0), 0)),
-                lambda: (g_out(1, 2, (1, 7), 0), g3_small()),
-                lambda: g_out(1, 3, (0, 1), 0),
-            ]
-            for c8 in range(8):
-                if c8 + 2 < 8:
-                    mx1(c8 + 2)
-                pe1(c8)
-                for k in (2 * c8, 2 * c8 + 1):
-                    ew(0, k)
-                for k in (2 * c8, 2 * c8 + 1):
-                    ew(1, k)
-                if c8 % 2 == 1:
-                    for k in range(2 * c8 - 2, 2 * c8 + 2):
-                        ew(2, k)
-                if c8 % 4 == 3:
-                    for k in range(2 * c8 - 6, 2 * c8 + 2):
-                        ew(3, k)
-                g2_tasks[c8]()
+            def g_out2(i4, t, bk, eng):
+                pt = bank(bk, [P, 4, P])
+                for sl in range(4):
+                    v = 4 * (sl % 2) + t
+                    nc.tensor.transpose(out=pt[:, sl, :], in_=grs[2 * i4 + sl // 2][:, 128 * v : 128 * (v + 1)], identity=ident_f[:])
+                copy_on(
+                    eng,
+                    g_mats[1][:].rearrange("p c (h t z) -> p c h t z", h=4, t=4)[:, :, :, t, 4 * i4 : 4 * i4 + 4],
+                    pt[:].rearrange("p s (h c) -> p c h s", h=4),
+                )
+
+            def ops_in_round(r):
+                ops = []
+                if r in (6, 10):
+                    ops += [(3, k) for k in range(2 * (r - 6), 2 * (r - 6) + 8)]
+                if r in (3, 5, 7, 9):
+                    ops += [(2, k) for k in range(2 * (r - 3), 2 * (r - 3) + 4)]
+                if 1 <= r <= 8:
+                    ops += [(1, 2 * r - 2), (1, 2 * r - 1)]
+                if r <= 7:
+                    ops += [(0, 2 * r), (0, 2 * r + 1)]
+                return ops
+
+            last_ops = [(4, k) for k in range(16)]
+            extra = {
+                0: lambda: g_copies(1, (0, 1, 2, 6, 5, 4, 3), 1),
+                1: lambda: (g_x(nc.gpsimd), g_y(nc.gpsimd), wh_path(1, 0, 0)),
+                2: lambda: (g_prod(0, nc.gpsimd), g_prod(1, nc.gpsimd), g_prod(2, nc.gpsimd), g_prod(3, nc.gpsimd), g3_small(), g3_prod(0), g3_prod(1)),
+                6: lambda: (g_out2(0, 0, 0, 0), g_out2(0, 1, 1, 1)),
+                7: lambda: (g_out2(0, 2, 7, 0), g_out2(0, 3, 0, 1)),
+                8: lambda: (g_out2(1, 0, 1, 0), g_out2(1, 1, 7, 1), g_out2(1, 2, 0, 0), g_out2(1, 3, 1, 1), wave(last_ops, (0,))),
+                9: lambda: (g3_out(0, 7), g3_prod(2), g3_out(1, 0), g3_prod(3), wave([(3, k) for k in range(8, 16)], (0,))),
+                10: lambda: (g3_out(2, 1), g3_prod(4), g3_out(3, 7), g3_prod(5)),
+            }
+            for r in range(11):
+                if r + 2 < 8:
+                    mx1(r + 2)
+                if r < 8:
+                    pe1(r)
+                ops = ops_in_round(r)
+                wave(ops, (1,) if r == 10 else (0, 1))
+                wave_v(ops)
+                if r + 2 < 8:
+                    e1(r + 2)
+                if r in extra:
+                    extra[r]()
 
             bc_b = g_mats[0][:, 16:24, :].rearrange("p c i -> p (c i)").bitcast(BF16)
             db_b = g_mats[0][:, 24:32, :].rearrange("p c i -> p (c i)").bitcast(BF16)
@@ -337,98 +403,104 @@ def tile_butterflymlp_w_kernel(
             nc.gpsimd.dma_start(out=db_b, in_=down_bias.partition_broadcast(P))
             nc.gpsimd.tensor_tensor(out=bsum[:], in0=bc_b, in1=db_b, op=ALU.add)
 
+            sc_view = W_con_scales.rearrange("g (e s) n -> s (g e) n", e=2, s=8)
             for h in range(2):
                 for q in range(4):
-                    nc.sync.dma_start(
-                        out=pl_con[32 * q : 32 * q + 16, h, :].bitcast(I32), in_=W_con_scales[4 * h : 4 * h + 4, 4 * q : 4 * q + 4, :].bitcast(I32)
-                    )
+                    nc.sync.dma_start(out=pl_con[32 * q : 32 * q + 16, h, :].bitcast(I32), in_=sc_view[4 * h : 4 * h + 4, 4 * q : 4 * q + 4, :].bitcast(I32))
+            wc_view = W_con_words.rearrange("g (e s l) n t -> s (g e) l (n t)", e=2, s=8, l=8)
             wc = []
-            for g in range(8):
-                t = wpool.tile([P, D_IN], U32, name="wc%d" % g, tag="w", align_bytes=64)
-                nc.sync.dma_start(out=t[:].bitcast(I32), in_=W_con_words[g].rearrange("p n t -> p (n t)").bitcast(I32))
+            for s in range(8):
+                t = wpool.tile([P, D_IN], U32, name="wc%d" % s, tag="w", align_bytes=64)
+                nc.sync.dma_start(out=t[:].bitcast(I32), in_=wc_view[s].bitcast(I32))
                 wc.append(t)
 
             gl = buf_b
             ta = buf_c
+            wave(last_ops, (1,))
             for q in range(4):
-                pe_lo = bank(4 + 2 * (q % 2), [P, 4, P])
-                pe_hi = bank(5 + 2 * (q % 2), [P, 4, P])
-                for k in range(4 * q, 4 * q + 4):
-                    ew(4, k)
-                    for c, pe in ((k, pe_lo), (k + 16, pe_hi)):
-                        nc.scalar.activation(out=gl[:, c, :], in_=buf_a[:, c, :], func=ACT.Gelu, bias=bias32[:, 32 + c : 33 + c], scale=1.0)
-                        nc.tensor.matmul(out=pe[:, c % 4, :], lhsT=gl[:, c, :], rhs=g_mats[1][:, c, :], start=True, stop=True)
-                for g, pe, eng in ((q, pe_lo, 1), (q + 4, pe_hi, 0)):
+                wave_v(last_ops[4 * q : 4 * q + 4])
+                for hi in range(2):
+                    c0 = 4 * q + 16 * hi
+                    g = q + 4 * hi
+                    nc.scalar.activation(out=gl[:, c0 : c0 + 4, :], in_=buf_a[:, c0 : c0 + 4, :], func=ACT.Gelu)
+                    pe = bank(4 + 2 * (q % 2) + hi, [P, 4, P])
+                    for cl in range(4):
+                        nc.tensor.matmul(out=pe[:, cl, :], lhsT=gl[:, c0 + cl, :], rhs=g_mats[1][:, c0 + cl, :], start=True, stop=True)
                     copy_on(
-                        eng,
-                        ta[:].rearrange("q u (x c) -> q u x c", x=4)[:, :, :, 4 * g : 4 * g + 4],
-                        pe[:].rearrange("q c (x u) -> q u x c", x=4),
+                        1 - hi,
+                        ta[:].rearrange("q b (g e z) -> q b g e z", g=8, e=2)[:, :, g, :, :],
+                        pe[:].rearrange("q (e s) (b z) -> q (s b) e z", e=2, z=8),
                     )
+                if q < 2:
+                    g3_out(4 + 2 * q, 2)
+                    if q == 0:
+                        g3_prod(6)
+                        g3_prod(7)
+                    g3_out(5 + 2 * q, 3)
 
-            def g3_part(q, bk):
-                ex = tmp.tile([P, 4, 4, 32], F32, name="ex", tag="ex", bufs=2)
-                nc.gpsimd.tensor_tensor(
-                    out=ex[:],
-                    in0=hmat[:, 128 * q : 128 * (q + 1)].rearrange("p (i j) -> p i j", i=4).unsqueeze(2).to_broadcast([P, 4, 4, 32]),
-                    in1=qmask[:].unsqueeze(1).unsqueeze(3).to_broadcast([P, 4, 4, 32]),
-                    op=ALU.mult,
-                )
-                pt = bank(bk, [P, 4, P])
-                for sl in range(4):
-                    nc.tensor.transpose(out=pt[:, sl, :], in_=ex[:, sl, :, :].rearrange("p x j -> p (x j)"), identity=ident_f[:])
-                nc.scalar.copy(
-                    out=g3[:, :, 16 * q : 16 * (q + 1)].rearrange("p u (s x) -> p u s x", s=4),
-                    in_=pt[:].rearrange("p s (x u) -> p u s x", x=4),
-                )
-
-            d2 = buf_a
-
-            def p2_part(u4, bk, eng):
-                pt = bank(bk, [P, 4, TOK])
-                for sl in range(4):
-                    nc.tensor.transpose(out=pt[:, sl, :], in_=ta[:, 4 * u4 + sl, :], identity=ident_f[:])
-                copy_on(eng, d2[:, 4 * u4 : 4 * u4 + 4, :], pt[:])
-
-            for i in range(8):
-                p2_part(i, i % 2, i % 2)
-                g3_part(i, 2 + i % 2)
-
-            t2 = buf_b.rearrange("q (g t) m -> q g t m", t=4)
-            for t in range(4):
-                for f4 in range(2):
-                    pe = bank(4 + (2 * t + f4) % 4, [P, 4, P])
-                    for sl in range(4):
-                        u = 16 * f4 + 4 * sl + t
-                        nc.tensor.matmul(out=pe[:, sl, :], lhsT=d2[:, u, :], rhs=g3[:, u, :], start=True, stop=True)
-                    copy_on(
-                        t % 2,
-                        t2[:, :, t, :].rearrange("q g (a f s) -> q g a f s", a=16, f=2)[:, :, :, f4, :],
-                        pe[:].rearrange("q s (g a) -> q g a s", g=8),
-                    )
-
-        with tc.tile_pool(name="lpool", bufs=2) as lpool:
+        with tc.tile_pool(name="lpool", bufs=3) as lpool:
             hq = lpool.tile([P, 8 * TOK], U32, name="hq", bufs=1, align_bytes=64)
             hs = lpool.tile([P, 8 * TOK], U8, name="hs", bufs=1, align_bytes=64)
             acc = [bank(n4, [P, 512]) for n4 in range(4)]
-            for g in range(8):
-                p2 = bank(4 + g % 4, [P, 4, TOK])
+            d2 = buf_a
+            trs = {}
+            outs = {}
+            hbs = {}
+
+            def to_pi(h):
+                for half in range(2):
+                    pt = bank(4 + half, [P, 4, TOK])
+                    for sl in range(4):
+                        blk = 16 * (sl % 2) + 4 * h + 2 * half + sl // 2
+                        nc.tensor.transpose(out=pt[:, sl, :], in_=ta[:, blk, :], identity=ident_f[:])
+                        trs[blk] = pt[:, sl, :]
+
+            def stage7(h):
                 for t in range(4):
-                    nc.tensor.transpose(out=p2[:, t, :], in_=t2[:, g, t, :], identity=ident_f[:])
-                hb = lpool.tile([P, TOK, 4], BF16, name="hb", tag="hb", align_bytes=64)
-                copy_on(g % 2, hb[:], p2[:].rearrange("m t q -> m q t"))
-                nc.vector.quantize_mx(
-                    out=hq[:, 128 * g : 128 * (g + 1)].bitcast(FP8X4), scales=hs[:, 128 * g : 128 * (g + 1)], in_=hb[:].rearrange("m q t -> m (q t)")
-                )
-                for n4 in range(4):
-                    nc.tensor.matmul_mx(
-                        out=acc[n4][:],
-                        lhsT=hq[:, 128 * g : 128 * (g + 1)].bitcast(FP8X4),
-                        lhsT_scale=hs[:, 128 * g : 128 * (g + 1)],
-                        rhs=wc[g][:, 512 * n4 : 512 * (n4 + 1)].bitcast(FP8X4),
-                        rhs_scale=pl_con[4 * (g % 4) : 128, g // 4, 512 * n4 : 512 * (n4 + 1)],
-                        start=(g == 0),
-                        stop=(g == 7),
+                    ba = 4 * h + t
+                    bb = ba + 16
+                    w = w7f[:, 4 * h + t, :, :]
+                    nc.scalar.activation(out=d2[:, ba, :], in_=trs[ba], func=ACT.Copy, scale=w[:, 0, 0:1])
+                    nc.scalar.activation(out=d2[:, bb, :], in_=trs[bb], func=ACT.Copy, scale=w[:, 1, 1:2])
+                    nc.vector.scalar_tensor_tensor(out=d2[:, ba, :], in0=trs[bb], scalar=w[:, 0, 1:2], in1=d2[:, ba, :], op0=ALU.mult, op1=ALU.add)
+                    nc.vector.scalar_tensor_tensor(out=d2[:, bb, :], in0=trs[ba], scalar=w[:, 1, 0:1], in1=d2[:, bb, :], op0=ALU.mult, op1=ALU.add)
+
+            def stages8(h):
+                for f7 in range(2):
+                    po = bank(6 + f7, [P, 4, TOK])
+                    for t in range(4):
+                        blk = 16 * f7 + 4 * h + t
+                        nc.tensor.matmul(out=po[:, t, :], lhsT=g3[:, blk, :], rhs=d2[:, blk, :], start=True, stop=True)
+                    s = 4 * f7 + h
+                    hb = lpool.tile([P, TOK, 4], BF16, name="hb", tag="hb", align_bytes=64)
+                    copy_on(f7, hb[:], po[:].rearrange("m t q -> m q t"))
+                    nc.vector.quantize_mx(
+                        out=hq[:, 128 * s : 128 * (s + 1)].bitcast(FP8X4), scales=hs[:, 128 * s : 128 * (s + 1)], in_=hb[:].rearrange("m q t -> m (q t)")
                     )
+
+            def mx2(h):
+                for f7 in range(2):
+                    s = 4 * f7 + h
+                    for n4 in range(4):
+                        nc.tensor.matmul_mx(
+                            out=acc[n4][:],
+                            lhsT=hq[:, 128 * s : 128 * (s + 1)].bitcast(FP8X4),
+                            lhsT_scale=hs[:, 128 * s : 128 * (s + 1)],
+                            rhs=wc[s][:, 512 * n4 : 512 * (n4 + 1)].bitcast(FP8X4),
+                            rhs_scale=pl_con[4 * (s % 4) : 128, s // 4, 512 * n4 : 512 * (n4 + 1)],
+                            start=(h == 0 and f7 == 0),
+                            stop=(h == 3 and f7 == 1),
+                        )
+
+            to_pi(0)
+            stage7(0)
+            for h in range(4):
+                if h + 1 < 4:
+                    to_pi(h + 1)
+                stages8(h)
+                if h + 1 < 4:
+                    stage7(h + 1)
+                mx2(h)
             out2 = out.flatten_outer_dims()
             for n4 in range(4):
                 o_sb = lpool.tile([P, 512], F32, name="o_sb", tag="o_sb")

@@ -19,6 +19,7 @@ TOK = 128
 D_IN = 2048
 H = 4096
 NT = H // P
+V_SHARE = ()
 FLOPS = 2 * 2 * TOK * D_IN * H + 24 * (H // 2) * 6 * TOK
 
 
@@ -51,7 +52,6 @@ def tile_butterflymlp_w_kernel(
         buf_b = const.tile([P, NT, TOK], F32, name="buf_b")
         buf_c = const.tile([P, NT, TOK], F32, name="buf_c")
         bsum = const.tile([P, D_IN], F32, name="bsum")
-        w7f = const.tile([P, 16, 2, 2], F32, name="w7f")
 
         with tc.tile_pool(name="tmp", bufs=1) as tmp, tc.tile_pool(name="grp", bufs=4) as grp:
             bw = (up_weights, down_weights)
@@ -87,12 +87,6 @@ def tile_butterflymlp_w_kernel(
                 if c8 == 1:
                     load_raw(1)
                     nc.scalar.dma_start(out=zh[1][0:80, :], in_=bw[1][7:12].rearrange("s (k p) r l -> (s k) (p r l)", p=P))
-
-            w7raw = tmp.tile([P, 4, 16], BF16, name="w7raw")
-            w7src = bw[1][7].rearrange("(c h z t) r l -> h c z (t r l)", c=16, h=4, z=8)
-            for h in range(4):
-                nc.scalar.dma_start(out=w7raw[:, h, :], in_=w7src[h])
-            nc.gpsimd.tensor_copy(out=w7f[:].rearrange("p a r l -> p (a r l)"), in_=w7raw[:].rearrange("p h e -> p (h e)"))
 
             def copy_on(eng, o, i):
                 if eng == 0:
@@ -257,7 +251,13 @@ def tile_butterflymlp_w_kernel(
 
             def ew_p(s5, k, side):
                 c = pair_tiles(s5, k)[side]
-                if s5 == 4:
+                if k % 8 in V_SHARE:
+                    w = wh32[0][:, 16 * s5 + k, side, side : side + 1]
+                    if s5 == 4:
+                        nc.vector.tensor_scalar(out=ew_bufs[5][:, c, :], in0=ew_src(4, c), scalar1=w, scalar2=bias32[:, 32 + c : 33 + c], op0=ALU.mult, op1=ALU.add)
+                    else:
+                        nc.vector.tensor_scalar(out=ew_bufs[s5 + 1][:, c, :], in0=ew_src(s5, c), scalar1=w, scalar2=None, op0=ALU.mult)
+                elif s5 == 4:
                     nc.scalar.activation(
                         out=ew_bufs[5][:, c, :], in_=ew_src(4, c), func=ACT.Identity, scale=wh32[0][:, 64 + k, side, side : side + 1], bias=bias32[:, 32 + c : 33 + c]
                     )
@@ -294,72 +294,43 @@ def tile_butterflymlp_w_kernel(
             e1(0)
             g_out(0, 3, (0, 1), 1)
             e1(1)
-
-            zmask = tmp.tile([P, 8], F32, name="zmask")
-            fh = xrec[1][:, 0:256].rearrange("p (s f e) -> p s f e", s=4, f=2)
-            hx = yrec[5][:, 0:128].rearrange("p (f e) -> p f e", f=2)
-            hy = yrec[4][:, 0:128].rearrange("p (f e) -> p f e", f=2)
-            hmat = xrec[2][:, 0:512]
+            qmask = tmp.tile([P, 4], F32, name="qmask")
+            fh = xrec[1][:, 0:320].rearrange("p (s e) -> p s e", s=5)
+            hx = yrec[5]
+            hys = {3: yrec[4][:, 0:128], 2: yrec[3][:, 0:256]}
+            hmat = xrec[2]
 
             def g3_small():
-                nc.vector.tensor_reduce(out=zmask[:], in_=ident_f[:].rearrange("p (h z t) -> p z h t", h=4, z=8), axis=mybir.AxisListType.XY, op=ALU.add)
-                for s in range(4):
-                    for f in range(2):
-                        nc.gpsimd.tensor_copy(
-                            out=fh[:, s, f, :].rearrange("p (r b a l) -> p r b a l", r=2, b=2**s, a=2 ** (3 - s), l=2),
-                            in_=wh32[1][:, 16 * (s + 1) : 16 * (s + 2), :, :].rearrange("p (a b f) r l -> p f r b a l", a=2 ** (3 - s), b=2**s, f=2)[:, f],
-                        )
-                for f in range(2):
-                    nc.gpsimd.tensor_tensor(
-                        out=hx[:, f, :].rearrange("p (u m w) -> p u m w", u=2, w=2),
-                        in0=fh[:, 0, f, :].rearrange("p (m w) -> p m w", w=2).unsqueeze(1).to_broadcast([P, 2, 16, 2]),
-                        in1=fh[:, 1, f, :].rearrange("p (u m) -> p u m", u=2).unsqueeze(3).to_broadcast([P, 2, 16, 2]),
-                        op=ALU.mult,
+                nc.vector.tensor_reduce(out=qmask[:], in_=ident_f[:].rearrange("p (x u) -> p x u", x=4), axis=mybir.AxisListType.X, op=ALU.add)
+                for s in range(5):
+                    nc.vector.tensor_copy(
+                        out=fh[:, s, :].rearrange("p (r b a l) -> p r b a l", r=2, b=2**s, a=2 ** (4 - s), l=2),
+                        in_=wh32[1][:, 16 * s : 16 * (s + 1), :, :].rearrange("p (a b) r l -> p r b a l", a=2 ** (4 - s), b=2**s),
                     )
-                    nc.gpsimd.tensor_tensor(
-                        out=hy[:, f, :].rearrange("p (u m w) -> p u m w", u=2, w=2),
-                        in0=fh[:, 3, f, :].rearrange("p (u m) -> p u m", u=2).unsqueeze(3).to_broadcast([P, 2, 16, 2]),
-                        in1=fh[:, 2, f, :].rearrange("p (m w) -> p m w", w=2).unsqueeze(1).to_broadcast([P, 2, 16, 2]),
-                        op=ALU.mult,
-                    )
-                    nc.gpsimd.tensor_tensor(
-                        out=hmat[:, 256 * f : 256 * (f + 1)].rearrange("p (u m w) -> p u m w", u=4, w=4),
-                        in0=hx[:, f, :].rearrange("p (m w) -> p m w", w=4).unsqueeze(1).to_broadcast([P, 4, 16, 4]),
-                        in1=hy[:, f, :].rearrange("p (u m) -> p u m", u=4).unsqueeze(3).to_broadcast([P, 4, 16, 4]),
-                        op=ALU.mult,
-                    )
-
-            exs = {}
-
-            def g3_prod(q):
-                ex = tmp.tile([P, 512], F32, name="ex", tag="ex", bufs=2)
-                nc.gpsimd.tensor_tensor(
-                    out=ex[:].rearrange("p (a z) -> p a z", z=8),
-                    in0=hmat[:, 64 * q : 64 * (q + 1)].unsqueeze(2).to_broadcast([P, 64, 8]),
-                    in1=zmask[:].unsqueeze(1).to_broadcast([P, 64, 8]),
+                nc.vector.tensor_tensor(
+                    out=hx[:].rearrange("p (u m w) -> p u m w", u=2, w=2),
+                    in0=fh[:, 0, :].rearrange("p (m w) -> p m w", w=2).unsqueeze(1).to_broadcast([P, 2, 32, 2]),
+                    in1=fh[:, 1, :].rearrange("p (u m) -> p u m", u=2).unsqueeze(3).to_broadcast([P, 2, 32, 2]),
                     op=ALU.mult,
                 )
-                exs[q] = ex
-
-            def g3_out(q, bk):
-                pt = bank(bk, [P, 4, P])
-                for sl in range(4):
-                    nc.tensor.transpose(out=pt[:, sl, :], in_=exs[q][:, 128 * sl : 128 * (sl + 1)], identity=ident_f[:])
-                nc.vector.tensor_copy(
-                    out=g3[:].rearrange("p (f h t) (i z) -> p f h t i z", f=2, h=4, z=8)[:, q // 4, :, :, 4 * (q % 4) : 4 * (q % 4) + 4, :],
-                    in_=pt[:].rearrange("p s (h z t) -> p h t s z", h=4, z=8),
+                hyprev = fh[:, 4, :]
+                for s in (3, 2):
+                    hy = hys[s]
+                    u = 2 ** (4 - s)
+                    nc.vector.tensor_tensor(
+                        out=hy[:].rearrange("p (u m w) -> p u m w", u=u, w=2),
+                        in0=hyprev.rearrange("p (u m) -> p u m", u=u).unsqueeze(3).to_broadcast([P, u, 32, 2]),
+                        in1=fh[:, s, :].rearrange("p (m w) -> p m w", w=2).unsqueeze(1).to_broadcast([P, u, 32, 2]),
+                        op=ALU.mult,
+                    )
+                    hyprev = hy[:]
+                nc.vector.tensor_tensor(
+                    out=hmat[:].rearrange("p (u m w) -> p u m w", u=8, w=4),
+                    in0=hx[:].rearrange("p (m w) -> p m w", w=4).unsqueeze(1).to_broadcast([P, 8, 32, 4]),
+                    in1=hyprev.rearrange("p (u m) -> p u m", u=8).unsqueeze(3).to_broadcast([P, 8, 32, 4]),
+                    op=ALU.mult,
                 )
 
-            def g_out2(i4, t, bk, eng):
-                pt = bank(bk, [P, 4, P])
-                for sl in range(4):
-                    v = 4 * (sl % 2) + t
-                    nc.tensor.transpose(out=pt[:, sl, :], in_=grs[2 * i4 + sl // 2][:, 128 * v : 128 * (v + 1)], identity=ident_f[:])
-                copy_on(
-                    eng,
-                    g_mats[1][:].rearrange("p c (h t z) -> p c h t z", h=4, t=4)[:, :, :, t, 4 * i4 : 4 * i4 + 4],
-                    pt[:].rearrange("p s (h c) -> p c h s", h=4),
-                )
 
             def ops_in_round(r):
                 ops = []
@@ -376,13 +347,14 @@ def tile_butterflymlp_w_kernel(
             last_ops = [(4, k) for k in range(16)]
             extra = {
                 0: lambda: g_copies(1, (0, 1, 2, 6, 5, 4, 3), 1),
-                1: lambda: (g_x(nc.gpsimd), g_y(nc.gpsimd), wh_path(1, 0, 0)),
-                2: lambda: (g_prod(0, nc.gpsimd), g_prod(1, nc.gpsimd), g_prod(2, nc.gpsimd), g_prod(3, nc.gpsimd), g3_small(), g3_prod(0), g3_prod(1)),
-                6: lambda: (g_out2(0, 0, 0, 0), g_out2(0, 1, 1, 1)),
-                7: lambda: (g_out2(0, 2, 7, 0), g_out2(0, 3, 0, 1)),
-                8: lambda: (g_out2(1, 0, 1, 0), g_out2(1, 1, 7, 1), g_out2(1, 2, 0, 0), g_out2(1, 3, 1, 1), wave(last_ops, (0,))),
-                9: lambda: (g3_out(0, 7), g3_prod(2), g3_out(1, 0), g3_prod(3), wave([(3, k) for k in range(8, 16)], (0,))),
-                10: lambda: (g3_out(2, 1), g3_prod(4), g3_out(3, 7), g3_prod(5)),
+                1: lambda: (g_x(nc.vector), g_y(nc.vector), wh_path(1, 0, 1)),
+                2: lambda: g_prod(0, nc.vector),
+                3: lambda: g_prod(1, nc.vector),
+                4: lambda: g_prod(2, nc.vector),
+                5: lambda: g_prod(3, nc.vector),
+                7: lambda: g_out(1, 0, (0, 1), 1),
+                8: lambda: (g_out(1, 1, (7, 0), 1), g_out(1, 2, (1, 7), 1), wave(last_ops, (0,))),
+                9: lambda: (g_out(1, 3, (0, 1), 1), wave([(3, k) for k in range(8, 16)], (0,))),
             }
             for r in range(11):
                 if r + 2 < 8:
@@ -401,106 +373,142 @@ def tile_butterflymlp_w_kernel(
             db_b = g_mats[0][:, 24:32, :].rearrange("p c i -> p (c i)").bitcast(BF16)
             nc.gpsimd.dma_start(out=bc_b, in_=b_con.partition_broadcast(P))
             nc.gpsimd.dma_start(out=db_b, in_=down_bias.partition_broadcast(P))
-            nc.gpsimd.tensor_tensor(out=bsum[:], in0=bc_b, in1=db_b, op=ALU.add)
 
-            sc_view = W_con_scales.rearrange("g (e s) n -> s (g e) n", e=2, s=8)
             for h in range(2):
                 for q in range(4):
-                    nc.sync.dma_start(out=pl_con[32 * q : 32 * q + 16, h, :].bitcast(I32), in_=sc_view[4 * h : 4 * h + 4, 4 * q : 4 * q + 4, :].bitcast(I32))
-            wc_view = W_con_words.rearrange("g (e s l) n t -> s (g e) l (n t)", e=2, s=8, l=8)
+                    nc.sync.dma_start(
+                        out=pl_con[32 * q : 32 * q + 16, h, :].bitcast(I32), in_=W_con_scales[4 * h : 4 * h + 4, 4 * q : 4 * q + 4, :].bitcast(I32)
+                    )
             wc = []
-            for s in range(8):
-                t = wpool.tile([P, D_IN], U32, name="wc%d" % s, tag="w", align_bytes=64)
-                nc.sync.dma_start(out=t[:].bitcast(I32), in_=wc_view[s].bitcast(I32))
+            for g in range(8):
+                t = wpool.tile([P, D_IN], U32, name="wc%d" % g, tag="w", align_bytes=64)
+                nc.sync.dma_start(out=t[:].bitcast(I32), in_=W_con_words[g].rearrange("p n t -> p (n t)").bitcast(I32))
                 wc.append(t)
 
             gl = buf_b
             ta = buf_c
             wave(last_ops, (1,))
+            pe2 = {}
             for q in range(4):
                 wave_v(last_ops[4 * q : 4 * q + 4])
                 for hi in range(2):
                     c0 = 4 * q + 16 * hi
-                    g = q + 4 * hi
                     nc.scalar.activation(out=gl[:, c0 : c0 + 4, :], in_=buf_a[:, c0 : c0 + 4, :], func=ACT.Gelu)
                     pe = bank(4 + 2 * (q % 2) + hi, [P, 4, P])
                     for cl in range(4):
                         nc.tensor.matmul(out=pe[:, cl, :], lhsT=gl[:, c0 + cl, :], rhs=g_mats[1][:, c0 + cl, :], start=True, stop=True)
+                    pe2[(q, hi)] = pe
+                if q >= 1:
+                    for hi in range(2):
+                        g = q - 1 + 4 * hi
+                        copy_on(
+                            1 - hi,
+                            ta[:].rearrange("q u (x c) -> q u x c", x=4)[:, :, :, 4 * g : 4 * g + 4],
+                            pe2[(q - 1, hi)][:].rearrange("q c (x u) -> q u x c", x=4),
+                        )
+            for hi in range(2):
+                g = 3 + 4 * hi
+                copy_on(
+                    1 - hi,
+                    ta[:].rearrange("q u (x c) -> q u x c", x=4)[:, :, :, 4 * g : 4 * g + 4],
+                    pe2[(3, hi)][:].rearrange("q c (x u) -> q u x c", x=4),
+                )
+
+            exs = {}
+
+            def g3_prod(q):
+                ex = tmp.tile([P, 4, 4, 32], F32, name="ex", tag="ex", bufs=2)
+                nc.vector.tensor_tensor(
+                    out=ex[:],
+                    in0=hmat[:, 128 * q : 128 * (q + 1)].rearrange("p (i j) -> p i j", i=4).unsqueeze(2).to_broadcast([P, 4, 4, 32]),
+                    in1=qmask[:].unsqueeze(1).unsqueeze(3).to_broadcast([P, 4, 4, 32]),
+                    op=ALU.mult,
+                )
+                exs[q] = ex
+
+            def g3_out(q, bk, eng):
+                pt = bank(bk, [P, 4, P])
+                for sl in range(4):
+                    nc.tensor.transpose(out=pt[:, sl, :], in_=exs[q][:, sl, :, :].rearrange("p x j -> p (x j)"), identity=ident_f[:])
+                copy_on(
+                    eng,
+                    g3[:, :, 16 * q : 16 * (q + 1)].rearrange("p u (s x) -> p u s x", s=4),
+                    pt[:].rearrange("p s (x u) -> p u s x", x=4),
+                )
+
+            d2 = buf_a
+
+            def p2_part(u4, bk, eng):
+                pt = bank(bk, [P, 4, TOK])
+                for sl in range(4):
+                    nc.tensor.transpose(out=pt[:, sl, :], in_=ta[:, 4 * u4 + sl, :], identity=ident_f[:])
+                copy_on(eng, d2[:, 4 * u4 : 4 * u4 + 4, :], pt[:])
+
+            g3_small()
+            g3_prod(0)
+            g3_prod(1)
+            for i in range(8):
+                g3_out(i, 2 + i % 2, i % 2)
+                if i + 2 < 8:
+                    g3_prod(i + 2)
+            for i in range(8):
+                p2_part(i, i % 4, i % 2)
+
+            t2 = buf_b.rearrange("q (g t) m -> q g t m", t=4)
+            for t in range(4):
+                for f4 in range(2):
+                    pe = bank(4 + (2 * t + f4) % 4, [P, 4, P])
+                    for sl in range(4):
+                        u = 16 * f4 + 4 * sl + t
+                        nc.tensor.matmul(out=pe[:, sl, :], lhsT=d2[:, u, :], rhs=g3[:, u, :], start=True, stop=True)
                     copy_on(
-                        1 - hi,
-                        ta[:].rearrange("q b (g e z) -> q b g e z", g=8, e=2)[:, :, g, :, :],
-                        pe[:].rearrange("q (e s) (b z) -> q (s b) e z", e=2, z=8),
+                        t % 2,
+                        t2[:, :, t, :].rearrange("q g (a f s) -> q g a f s", a=16, f=2)[:, :, :, f4, :],
+                        pe[:].rearrange("q s (g a) -> q g a s", g=8),
                     )
-                if q < 2:
-                    g3_out(4 + 2 * q, 2)
-                    if q == 0:
-                        g3_prod(6)
-                        g3_prod(7)
-                    g3_out(5 + 2 * q, 3)
+
+            nc.vector.tensor_tensor(out=bsum[:], in0=bc_b, in1=db_b, op=ALU.add)
 
         with tc.tile_pool(name="lpool", bufs=3) as lpool:
             hq = lpool.tile([P, 8 * TOK], U32, name="hq", bufs=1, align_bytes=64)
             hs = lpool.tile([P, 8 * TOK], U8, name="hs", bufs=1, align_bytes=64)
             acc = [bank(n4, [P, 512]) for n4 in range(4)]
-            d2 = buf_a
-            trs = {}
-            outs = {}
             hbs = {}
 
-            def to_pi(h):
-                for half in range(2):
-                    pt = bank(4 + half, [P, 4, TOK])
-                    for sl in range(4):
-                        blk = 16 * (sl % 2) + 4 * h + 2 * half + sl // 2
-                        nc.tensor.transpose(out=pt[:, sl, :], in_=ta[:, blk, :], identity=ident_f[:])
-                        trs[blk] = pt[:, sl, :]
-
-            def stage7(h):
+            def to_mx(g):
+                p2 = bank(4 + g % 4, [P, 4, TOK])
                 for t in range(4):
-                    ba = 4 * h + t
-                    bb = ba + 16
-                    w = w7f[:, 4 * h + t, :, :]
-                    nc.scalar.activation(out=d2[:, ba, :], in_=trs[ba], func=ACT.Copy, scale=w[:, 0, 0:1])
-                    nc.scalar.activation(out=d2[:, bb, :], in_=trs[bb], func=ACT.Copy, scale=w[:, 1, 1:2])
-                    nc.vector.scalar_tensor_tensor(out=d2[:, ba, :], in0=trs[bb], scalar=w[:, 0, 1:2], in1=d2[:, ba, :], op0=ALU.mult, op1=ALU.add)
-                    nc.vector.scalar_tensor_tensor(out=d2[:, bb, :], in0=trs[ba], scalar=w[:, 1, 0:1], in1=d2[:, bb, :], op0=ALU.mult, op1=ALU.add)
+                    nc.tensor.transpose(out=p2[:, t, :], in_=t2[:, g, t, :], identity=ident_f[:])
+                hb = lpool.tile([P, TOK, 4], BF16, name="hb", tag="hb", align_bytes=64)
+                copy_on(g % 2, hb[:], p2[:].rearrange("m t q -> m q t"))
+                hbs[g] = hb
 
-            def stages8(h):
-                for f7 in range(2):
-                    po = bank(6 + f7, [P, 4, TOK])
-                    for t in range(4):
-                        blk = 16 * f7 + 4 * h + t
-                        nc.tensor.matmul(out=po[:, t, :], lhsT=g3[:, blk, :], rhs=d2[:, blk, :], start=True, stop=True)
-                    s = 4 * f7 + h
-                    hb = lpool.tile([P, TOK, 4], BF16, name="hb", tag="hb", align_bytes=64)
-                    copy_on(f7, hb[:], po[:].rearrange("m t q -> m q t"))
-                    nc.vector.quantize_mx(
-                        out=hq[:, 128 * s : 128 * (s + 1)].bitcast(FP8X4), scales=hs[:, 128 * s : 128 * (s + 1)], in_=hb[:].rearrange("m q t -> m (q t)")
+            def quant(g):
+                nc.vector.quantize_mx(
+                    out=hq[:, 128 * g : 128 * (g + 1)].bitcast(FP8X4), scales=hs[:, 128 * g : 128 * (g + 1)], in_=hbs[g][:].rearrange("m q t -> m (q t)")
+                )
+
+            def mx2(g):
+                for n4 in range(4):
+                    nc.tensor.matmul_mx(
+                        out=acc[n4][:],
+                        lhsT=hq[:, 128 * g : 128 * (g + 1)].bitcast(FP8X4),
+                        lhsT_scale=hs[:, 128 * g : 128 * (g + 1)],
+                        rhs=wc[g][:, 512 * n4 : 512 * (n4 + 1)].bitcast(FP8X4),
+                        rhs_scale=pl_con[4 * (g % 4) : 128, g // 4, 512 * n4 : 512 * (n4 + 1)],
+                        start=(g == 0),
+                        stop=(g == 7),
                     )
 
-            def mx2(h):
-                for f7 in range(2):
-                    s = 4 * f7 + h
-                    for n4 in range(4):
-                        nc.tensor.matmul_mx(
-                            out=acc[n4][:],
-                            lhsT=hq[:, 128 * s : 128 * (s + 1)].bitcast(FP8X4),
-                            lhsT_scale=hs[:, 128 * s : 128 * (s + 1)],
-                            rhs=wc[s][:, 512 * n4 : 512 * (n4 + 1)].bitcast(FP8X4),
-                            rhs_scale=pl_con[4 * (s % 4) : 128, s // 4, 512 * n4 : 512 * (n4 + 1)],
-                            start=(h == 0 and f7 == 0),
-                            stop=(h == 3 and f7 == 1),
-                        )
-
-            to_pi(0)
-            stage7(0)
-            for h in range(4):
-                if h + 1 < 4:
-                    to_pi(h + 1)
-                stages8(h)
-                if h + 1 < 4:
-                    stage7(h + 1)
-                mx2(h)
+            to_mx(0)
+            to_mx(1)
+            quant(0)
+            for g in range(8):
+                if g + 2 < 8:
+                    to_mx(g + 2)
+                if g + 1 < 8:
+                    quant(g + 1)
+                mx2(g)
             out2 = out.flatten_outer_dims()
             for n4 in range(4):
                 o_sb = lpool.tile([P, 512], F32, name="o_sb", tag="o_sb")

@@ -19,15 +19,29 @@ TOK = 128
 D_IN = 2048
 H = 4096
 NT = H // P
-V_SHARE = ()
 FLOPS = 2 * 2 * TOK * D_IN * H + 24 * (H // 2) * 6 * TOK
+KEYS = {('fpv', 0): 2.88, ('fps', 0): 2.88, ('gx', 0): 3.25, ('xt', 0): 3.79, ('xt', 1): 4.31, ('gy', 0): 4.56, ('xe', 0): 4.79, ('vt',): 4.83, ('zt', 0): 4.93, ('xe', 1): 5.31, ('gp', 0, 0): 5.35, ('ve',): 5.75, ('ze', 0): 5.87, ('xq',): 6.22, ('gt', 0, 0, 0): 6.60, ('gp', 0, 1): 6.68, ('gt', 0, 0, 1): 7.12, ('gp', 0, 2): 7.55, ('ge', 0, 0, 0): 7.60, ('mx1', 0): 7.64, ('ge', 0, 0, 1): 8.12, ('gp', 0, 3): 8.41, ('gt', 0, 1, 0): 9.24, ('e1', 0): 9.72, ('gt', 0, 1, 1): 9.76, ('fps', 1): 9.82, ('fpv', 1): 10.16, ('mx1', 1): 10.28, ('gx', 1): 10.52, ('ge', 0, 1, 0): 11.03, ('ge', 0, 1, 1): 11.47, ('gy', 1): 11.83, ('gt', 0, 2, 0): 11.88, ('gt', 0, 2, 1): 12.40, ('e1', 1): 12.62, ('ge', 0, 2, 0): 12.88, ('gt', 0, 3, 0): 12.92, ('gp', 1, 0): 13.07, ('ge', 0, 2, 1): 13.40, ('mx1', 2): 13.44, ('ge', 0, 3, 0): 13.92, ('gp', 1, 1): 13.93, ('gp', 1, 2): 14.80, ('gt', 0, 3, 1): 15.04, ('mx1', 3): 15.56, ('e1', 2): 15.67, ('ge', 0, 3, 1): 16.04, ('gp', 1, 3): 16.11, ('pe1', 0): 17.16, ('pe1', 1): 17.62, ('zt', 1): 18.09, ('e1', 3): 18.10, ('p', 0, 0, 0): 18.10, ('p', 0, 0, 1): 18.22, ('p', 0, 1, 0): 18.34, ('mx1', 4): 18.35, ('p', 0, 1, 1): 18.46, ('p', 0, 2, 0): 18.58, ('p', 0, 2, 1): 18.70, ('p', 0, 3, 0): 18.82, ('p', 0, 3, 1): 18.94, ('v', 0, 0): 18.96, ('ze', 1): 19.05, ('v', 0, 1): 19.20, ('v', 0, 2): 19.45, ('p', 1, 0, 0): 19.58, ('v', 0, 3): 19.69, ('p', 1, 1, 0): 19.70, ('p', 1, 0, 1): 19.83, ('g3s',): 19.93, ('p', 1, 1, 1): 19.94, ('pe1', 2): 19.95, ('p', 1, 2, 0): 20.07, ('p', 1, 3, 0): 20.19, ('wc', 0): 20.25, ('p', 1, 2, 1): 20.31, ('wc', 1): 20.32, ('wc', 2): 20.39, ('mx1', 5): 20.42, ('p', 1, 3, 1): 20.43, ('wc', 3): 20.46, ('wc', 4): 20.53, ('p', 0, 4, 0): 20.90, ('p', 0, 4, 1): 21.02, ('p', 0, 5, 0): 21.14, ('p', 0, 5, 1): 21.26, ('v', 1, 0): 21.65, ('v', 1, 1): 21.89, ('pe1', 3): 22.02, ('v', 1, 2): 22.13, ('p', 2, 0, 0): 22.27, ('v', 1, 3): 22.38, ('p', 2, 2, 0): 22.39, ('gt', 1, 0, 0): 22.49, ('wc', 5): 22.50, ('p', 2, 1, 0): 22.51, ('v', 0, 4): 22.62, ('p', 2, 3, 0): 22.63, ('p', 2, 0, 1): 22.76, ('v', 0, 5): 22.86, ('p', 2, 2, 1): 22.87, ('p', 0, 6, 0): 22.99, ('gt', 1, 0, 1): 23.01, ('e1', 4): 23.11, ('p', 2, 1, 1): 23.11, ('p', 2, 3, 1): 23.23, ('p', 1, 4, 0): 23.35, ('p', 1, 5, 0): 23.47, ('gt', 1, 1, 0): 23.53, ('v', 2, 0): 23.55, ('p', 1, 4, 1): 23.59, ('p', 1, 5, 1): 23.71, ('v', 2, 1): 23.79, ('p', 0, 6, 1): 23.82, ('p', 0, 7, 0): 23.94, ('v', 2, 2): 24.03, ('mx1', 6): 24.05, ('p', 0, 7, 1): 24.06, ('p', 3, 0, 0): 24.18, ('v', 2, 3): 24.28, ('p', 3, 4, 0): 24.30, ('p', 3, 1, 0): 24.42, ('v', 1, 4): 24.52, ('p', 3, 5, 0): 24.54, ('ge', 1, 0, 0): 24.65, ('v', 1, 5): 24.76, ('v', 0, 6): 25.01, ('p', 3, 2, 0): 25.09, ('p', 2, 4, 0): 25.21, ('v', 0, 7): 25.25, ('p', 2, 6, 0): 25.33, ('p', 2, 5, 0): 25.45, ('e1', 5): 25.49, ('p', 2, 7, 0): 25.57, ('pe1', 4): 25.65, ('p', 1, 6, 0): 25.69, ('p', 1, 7, 0): 25.80, ('p', 1, 6, 1): 25.92, ('g3p', 0): 25.94, ('p', 1, 7, 1): 26.04, ('gt', 1, 1, 1): 26.12, ('wc', 6): 26.13, ('p', 3, 3, 0): 26.16, ('p', 3, 6, 0): 26.28, ('e1', 6): 26.38, ('p', 3, 7, 0): 26.40, ('ge', 1, 0, 1): 26.52, ('mx1', 7): 26.64, ('v', 1, 6): 26.82, ('p', 0, 8, 0): 26.95, ('v', 1, 7): 27.06, ('p', 0, 8, 1): 27.07, ('p', 0, 9, 0): 27.19, ('g3p', 1): 27.30, ('p', 0, 9, 1): 27.31, ('ge', 1, 1, 0): 27.43, ('v', 0, 8): 27.81, ('p', 2, 4, 1): 27.87, ('p', 2, 5, 1): 27.99, ('v', 0, 9): 28.05, ('p', 2, 6, 1): 28.11, ('p', 2, 7, 1): 28.22, ('pe1', 5): 28.24, ('ge', 1, 1, 1): 28.34, ('v', 2, 4): 28.37, ('v', 2, 5): 28.61, ('pe1', 6): 28.71, ('wc', 7): 28.72, ('p', 1, 8, 0): 28.78, ('v', 2, 6): 28.85, ('p', 1, 8, 1): 28.90, ('p', 1, 9, 0): 29.02, ('v', 2, 7): 29.10, ('p', 1, 9, 1): 29.14, ('gt', 1, 2, 0): 29.17, ('bl', 0): 29.19, ('p', 0, 10, 0): 29.26, ('e1', 7): 29.34, ('p', 0, 10, 1): 29.37, ('p', 0, 11, 0): 29.49, ('p', 0, 11, 1): 29.61, ('gt', 1, 2, 1): 29.69, ('p', 3, 0, 1): 29.73, ('v', 1, 8): 29.78, ('p', 3, 1, 1): 29.85, ('p', 3, 2, 1): 29.97, ('v', 1, 9): 30.02, ('p', 3, 3, 1): 30.09, ('p', 3, 4, 1): 30.20, ('pe1', 7): 30.21, ('v', 0, 10): 30.27, ('p', 3, 5, 1): 30.32, ('p', 3, 6, 1): 30.44, ('v', 0, 11): 30.51, ('p', 3, 7, 1): 30.56, ('p', 0, 12, 0): 30.68, ('gt', 1, 3, 0): 30.68, ('v', 3, 0): 30.75, ('p', 0, 12, 1): 30.80, ('p', 1, 10, 0): 30.92, ('v', 3, 1): 31.00, ('p', 1, 11, 0): 31.03, ('p', 1, 10, 1): 31.15, ('bl', 1): 31.16, ('g3t', 0): 31.20, ('v', 3, 2): 31.24, ('p', 1, 11, 1): 31.27, ('p', 0, 13, 0): 31.39, ('v', 3, 3): 31.48, ('p', 0, 13, 1): 31.51, ('p', 2, 8, 0): 31.63, ('g3t', 1): 31.72, ('v', 3, 4): 31.73, ('p', 2, 9, 0): 31.75, ('p', 2, 10, 0): 31.87, ('v', 3, 5): 31.97, ('p', 2, 11, 0): 31.98, ('p', 0, 14, 0): 32.10, ('v', 3, 6): 32.21, ('p', 0, 14, 1): 32.22, ('p', 0, 15, 0): 32.34, ('v', 3, 7): 32.46, ('p', 0, 15, 1): 32.46, ('ge', 1, 2, 0): 32.58, ('v', 1, 10): 32.70, ('v', 1, 11): 32.94, ('ge', 1, 2, 1): 33.02, ('v', 0, 12): 33.19, ('gt', 1, 3, 1): 33.40, ('v', 0, 13): 33.43, ('p', 2, 8, 1): 33.45, ('p', 2, 9, 1): 33.57, ('v', 0, 14): 33.67, ('p', 2, 10, 1): 33.69, ('p', 2, 11, 1): 33.81, ('v', 0, 15): 33.92, ('p', 1, 12, 0): 33.93, ('p', 1, 13, 0): 34.05, ('v', 2, 8): 34.16, ('p', 1, 12, 1): 34.17, ('p', 1, 13, 1): 34.28, ('v', 2, 9): 34.40, ('p', 1, 14, 0): 34.40, ('p', 1, 15, 0): 34.52, ('p', 1, 14, 1): 34.64, ('v', 2, 10): 34.65, ('p', 1, 15, 1): 34.76, ('p', 4, 0, 0): 34.88, ('v', 2, 11): 34.89, ('p', 4, 1, 0): 35.00, ('p', 4, 2, 0): 35.11, ('v', 1, 12): 35.13, ('p', 4, 3, 0): 35.23, ('p', 4, 4, 0): 35.35, ('v', 1, 13): 35.38, ('p', 4, 5, 0): 35.47, ('p', 4, 6, 0): 35.59, ('v', 1, 14): 35.62, ('p', 4, 7, 0): 35.71, ('p', 4, 8, 0): 35.83, ('v', 1, 15): 35.86, ('p', 4, 9, 0): 35.94, ('p', 4, 10, 0): 36.06, ('g3p', 2): 36.11, ('p', 4, 11, 0): 36.18, ('p', 4, 12, 0): 36.30, ('p', 4, 13, 0): 36.42, ('p', 4, 14, 0): 36.54, ('g3p', 3): 36.55, ('p', 4, 15, 0): 36.66, ('p', 2, 12, 0): 36.78, ('p', 2, 12, 1): 36.89, ('p', 2, 13, 0): 37.01, ('p', 2, 13, 1): 37.13, ('p', 2, 14, 0): 37.25, ('p', 2, 14, 1): 37.37, ('v', 2, 12): 37.39, ('p', 2, 15, 0): 37.49, ('p', 2, 15, 1): 37.61, ('v', 2, 13): 37.64, ('ge', 1, 3, 0): 37.72, ('v', 2, 14): 37.88, ('v', 2, 15): 38.12, ('ge', 1, 3, 1): 38.16, ('ba',): 38.37, ('p', 3, 8, 0): 38.60, ('p', 3, 9, 0): 38.72, ('p', 3, 10, 0): 38.84, ('p', 3, 11, 0): 38.96, ('p', 3, 12, 0): 39.08, ('p', 3, 13, 0): 39.19, ('p', 3, 14, 0): 39.31, ('p', 3, 15, 0): 39.43, ('p', 3, 8, 1): 39.55, ('p', 3, 9, 1): 39.67, ('p', 3, 10, 1): 39.79, ('p', 3, 11, 1): 39.91, ('p', 3, 12, 1): 40.02, ('v', 3, 8): 40.09, ('p', 3, 13, 1): 40.14, ('p', 3, 14, 1): 40.26, ('v', 3, 9): 40.33, ('p', 3, 15, 1): 40.38, ('g3e', 0): 40.50, ('v', 3, 10): 40.57, ('v', 3, 11): 40.82, ('p', 4, 0, 1): 40.94, ('p', 4, 1, 1): 41.06, ('v', 3, 12): 41.06, ('p', 4, 8, 1): 41.17, ('p', 4, 2, 1): 41.29, ('v', 3, 13): 41.30, ('g3t', 2): 41.32, ('p', 4, 9, 1): 41.41, ('p', 4, 3, 1): 41.53, ('v', 3, 14): 41.55, ('p', 4, 10, 1): 41.65, ('p', 4, 4, 1): 41.77, ('v', 3, 15): 41.79, ('p', 4, 11, 1): 41.89, ('p', 4, 5, 1): 42.01, ('v', 4, 0): 42.03, ('p', 4, 12, 1): 42.12, ('p', 4, 6, 1): 42.24, ('v', 4, 1): 42.28, ('p', 4, 13, 1): 42.36, ('p', 4, 7, 1): 42.48, ('v', 4, 2): 42.52, ('p', 4, 14, 1): 42.60, ('p', 4, 15, 1): 42.72, ('v', 4, 3): 42.76, ('g3e', 1): 42.84, ('v', 4, 4): 43.01, ('v', 4, 5): 43.25, ('g3e', 2): 43.27, ('v', 4, 6): 43.49, ('g3t', 3): 43.65, ('gelu', 0): 43.71, ('v', 4, 7): 43.74, ('v', 4, 8): 43.98, ('gelu', 4): 44.15, ('v', 4, 9): 44.22, ('v', 4, 10): 44.46, ('pe2', 0): 44.53, ('gelu', 1): 44.59, ('v', 4, 11): 44.71, ('v', 4, 12): 44.95, ('pe2', 4): 45.00, ('gelu', 5): 45.03, ('v', 4, 13): 45.19, ('v', 4, 14): 45.44, ('gelu', 2): 45.47, ('pe2', 1): 45.47, ('v', 4, 15): 45.68, ('ea', 0): 45.91, ('g3p', 4): 45.92, ('pe2', 5): 45.94, ('gelu', 6): 46.34, ('ea', 4): 46.37, ('pe2', 2): 46.40, ('ea', 1): 46.78, ('g3p', 5): 46.81, ('g3t', 4): 46.87, ('gelu', 3): 47.22, ('ea', 5): 47.25, ('pe2', 6): 47.39, ('gelu', 7): 47.66, ('g3p', 6): 47.87, ('pe2', 3): 48.04, ('ea', 2): 48.10, ('ea', 6): 48.34, ('pe2', 7): 48.51, ('g3e', 3): 48.54, ('g3e', 4): 48.97, ('g3t', 5): 49.35, ('ea', 3): 49.41, ('ea', 7): 49.46, ('g3t', 6): 49.87, ('g3e', 5): 50.35, ('g3p', 7): 50.35, ('p2t', 0): 50.39, ('g3e', 6): 50.87, ('p2t', 1): 50.91, ('p2e', 0): 51.39, ('g3t', 7): 51.43, ('p2e', 1): 51.91, ('p2t', 2): 51.95, ('g3e', 7): 52.43, ('p2t', 4): 52.47, ('p2e', 2): 52.95, ('p2t', 5): 52.99, ('p2e', 4): 53.47, ('p2t', 3): 53.51, ('p2e', 5): 53.99, ('p2t', 6): 54.03, ('p2e', 3): 54.51, ('p2e', 6): 55.03, ('p2t', 7): 55.33, ('pe3', 0, 0): 55.85, ('pe3', 1, 0): 56.32, ('p2e', 7): 56.33, ('ec', 0, 0): 56.80, ('pe3', 0, 1): 57.15, ('ec', 1, 0): 57.27, ('pe3', 1, 1): 57.62, ('pe3', 2, 0): 58.09, ('ec', 0, 1): 58.10, ('pe3', 3, 0): 58.56, ('ec', 1, 1): 58.57, ('pe3', 2, 1): 59.02, ('ec', 2, 0): 59.04, ('pe3', 3, 1): 59.49, ('ec', 3, 0): 59.50, ('ec', 2, 1): 59.97, ('ec', 3, 1): 60.44, ('lt', 0): 61.26, ('lt', 1): 61.78, ('le', 0): 62.26, ('lt', 2): 62.30, ('lq', 0): 62.70, ('le', 1): 62.78, ('lt', 3): 62.82, ('le', 2): 63.30, ('lt', 4): 63.34, ('lq', 1): 63.74, ('le', 3): 63.82, ('mx2', 0): 63.86, ('lq', 2): 63.87, ('le', 4): 64.34, ('mx2', 1): 64.78, ('lq', 3): 64.78, ('lq', 4): 64.91, ('mx2', 2): 65.69, ('lt', 5): 66.61, ('mx2', 3): 67.13, ('le', 5): 67.61, ('lt', 6): 68.04, ('lq', 5): 68.43, ('mx2', 4): 68.56, ('le', 6): 69.04, ('lt', 7): 69.48, ('lq', 6): 69.49, ('mx2', 5): 70.00, ('le', 7): 70.48, ('mx2', 6): 70.92, ('lq', 7): 71.30, ('mx2', 7): 72.00, ('oa', 0): 73.40, ('oa', 1): 73.84, ('os', 0): 74.22, ('oa', 2): 74.28, ('os', 1): 74.66, ('oa', 3): 74.72, ('os', 2): 75.10, ('os', 3): 75.55}
 
 
 def tile_butterflymlp_w_kernel(
     tc, x, W_exp_words, W_exp_scales, b_exp, up_weights, up_bias, down_weights, W_con_words, W_con_scales, b_con, down_bias, out
 ):
     nc = tc.nc
+    plan = []
+
+    def at(key, fn):
+        plan.append((KEYS.get(key, 1000.0 + len(plan)), len(plan), key, fn))
+
+    done = [0]
+
+    def run_plan():
+        items = sorted(plan[done[0] :])
+        done[0] = len(plan)
+        for item in items:
+            item[3]()
+
     with ExitStack() as ctx:
+        ctx.enter_context(tc.manual_schedule())
         const = ctx.enter_context(tc.tile_pool(name="const", bufs=1))
         wpool = ctx.enter_context(tc.tile_pool(name="wpool", bufs=8))
         psum = ctx.enter_context(tc.psum_pool(name="psum", bufs=1))
@@ -35,10 +49,19 @@ def tile_butterflymlp_w_kernel(
         def bank(i, shape, dtype=F32):
             return psum.tile(shape, dtype, name="bk%d" % i, tag="bk%d" % i)
 
+        def copy_on(eng, o, i):
+            if eng == 0:
+                nc.vector.tensor_copy(out=o, in_=i)
+            else:
+                nc.scalar.copy(out=o, in_=i)
+
         ident_f = const.tile([P, P], F32, name="ident_f")
         make_identity(nc, ident_f[:])
         ident_b = const.tile([P, P], BF16, name="ident_b")
         make_identity(nc, ident_b[:])
+        warm = const.tile([P, 1], F32, name="warm")
+        nc.vector.memset(warm[:], 0.0)
+        nc.scalar.activation(out=warm[:], in_=warm[:], func=ACT.Gelu)
         pl_exp = const.tile([P, H], U8, name="pl_exp", align_bytes=64)
         nc.vector.memset(pl_exp[:].bitcast(I32), 0)
         pl_con = const.tile([P, 2, D_IN], U8, name="pl_con", align_bytes=64)
@@ -52,15 +75,16 @@ def tile_butterflymlp_w_kernel(
         buf_b = const.tile([P, NT, TOK], F32, name="buf_b")
         buf_c = const.tile([P, NT, TOK], F32, name="buf_c")
         bsum = const.tile([P, D_IN], F32, name="bsum")
+        bw = (up_weights, down_weights)
+        wc = {}
 
         with tc.tile_pool(name="tmp", bufs=1) as tmp, tc.tile_pool(name="grp", bufs=4) as grp:
-            bw = (up_weights, down_weights)
             raw = [tmp.tile([P, 7, 256], BF16, name="raw_up"), tmp.tile([P, 7, 256], BF16, name="raw_down")]
 
             def load_raw(b):
                 src = bw[b][0:7].rearrange("s (c k) r l -> c s (k r l)", c=NT)
                 for h in range(4):
-                    nc.scalar.dma_start(out=raw[b][32 * h : 32 * h + 32, :, :], in_=src)
+                    nc.sync.dma_start(out=raw[b][32 * h : 32 * h + 32, :, :], in_=src)
 
             load_raw(0)
             x_sb = grp.tile([P, D_IN], BF16, name="x_sb", tag="gr", align_bytes=64)
@@ -71,11 +95,11 @@ def tile_butterflymlp_w_kernel(
             for b in range(2):
                 nc.vector.memset(zh[b][64:128, :], 0.0)
             nc.vector.memset(pl_con[:].rearrange("p h n -> p (h n)").bitcast(I32), 0)
+            nc.sync.dma_start(out=vb[0:32, :], in_=b_exp.rearrange("(c p) -> c p", p=P))
+            nc.sync.dma_start(out=vb[32:64, :], in_=up_bias.rearrange("(c p) -> c p", p=P))
+            nc.sync.dma_start(out=zh[0][0:80, :], in_=bw[0][7:12].rearrange("s (k p) r l -> (s k) (p r l)", p=P))
             for q in range(4):
                 nc.sync.dma_start(out=pl_exp[32 * q : 32 * q + 16, :].bitcast(I32), in_=W_exp_scales[:, 4 * q : 4 * q + 4, :].bitcast(I32))
-            nc.scalar.dma_start(out=vb[0:32, :], in_=b_exp.rearrange("(c p) -> c p", p=P))
-            nc.scalar.dma_start(out=vb[32:64, :], in_=up_bias.rearrange("(c p) -> c p", p=P))
-            nc.scalar.dma_start(out=zh[0][0:80, :], in_=bw[0][7:12].rearrange("s (k p) r l -> (s k) (p r l)", p=P))
             wx = []
             for c8 in range(8):
                 t = wpool.tile([P, 4, 512], U32, name="wx%d" % c8, tag="w", align_bytes=64)
@@ -86,15 +110,23 @@ def tile_butterflymlp_w_kernel(
                 wx.append(t)
                 if c8 == 1:
                     load_raw(1)
-                    nc.scalar.dma_start(out=zh[1][0:80, :], in_=bw[1][7:12].rearrange("s (k p) r l -> (s k) (p r l)", p=P))
+                    nc.sync.dma_start(out=zh[1][0:80, :], in_=bw[1][7:12].rearrange("s (k p) r l -> (s k) (p r l)", p=P))
+            for h in range(2):
+                for q in range(4):
+                    nc.sync.dma_start(
+                        out=pl_con[32 * q : 32 * q + 16, h, :].bitcast(I32), in_=W_con_scales[4 * h : 4 * h + 4, 4 * q : 4 * q + 4, :].bitcast(I32)
+                    )
 
-            def copy_on(eng, o, i):
-                if eng == 0:
-                    nc.vector.tensor_copy(out=o, in_=i)
-                else:
-                    nc.scalar.copy(out=o, in_=i)
+            def load_wc(g):
+                t = wpool.tile([P, D_IN], U32, name="wc%d" % g, tag="w", align_bytes=64)
+                nc.sync.dma_start(out=t[:].bitcast(I32), in_=W_con_words[g].rearrange("p n t -> p (n t)").bitcast(I32))
+                wc[g] = t
 
             fp = tmp.tile([P, 7, 256], BF16, name="fp")
+            xrec = [None, tmp.tile([P, 512], F32, name="xrec1"), tmp.tile([P, 1024], F32, name="xrec2")]
+            yrec = {5: tmp.tile([P, 128], F32, name="yrec5"), 4: tmp.tile([P, 256], F32, name="yrec4"), 3: tmp.tile([P, 512], F32, name="yrec3")}
+            grs = {}
+            pts = {}
 
             def g_copies(b, stages, eng):
                 for s in stages:
@@ -123,14 +155,11 @@ def tile_butterflymlp_w_kernel(
                                 raw[b][q, 6, :].rearrange("p (t b r l) -> p t r b l", t=2, b=32, r=2, l=2)[:, h % 2, h // 2],
                             )
 
-            xrec = [None, tmp.tile([P, 512], F32, name="xrec1"), tmp.tile([P, 1024], F32, name="xrec2")]
-            yrec = {5: tmp.tile([P, 128], F32, name="yrec5"), 4: tmp.tile([P, 256], F32, name="yrec4"), 3: tmp.tile([P, 512], F32, name="yrec3")}
-
-            def g_x(ve):
+            def g_x():
                 prev = fp[:, 0, :]
                 for s in (1, 2):
                     shp = [P, 2, 128, 2**s]
-                    ve.tensor_tensor(
+                    nc.vector.tensor_tensor(
                         out=xrec[s][:].rearrange("p (u m w) -> p u m w", u=2, w=2**s),
                         in0=prev.rearrange("p (m w) -> p m w", w=2**s).unsqueeze(1).to_broadcast(shp),
                         in1=fp[:, s, :].rearrange("p (u m) -> p u m", u=2).unsqueeze(3).to_broadcast(shp),
@@ -138,13 +167,13 @@ def tile_butterflymlp_w_kernel(
                     )
                     prev = xrec[s][:]
 
-            def g_y(ve):
+            def g_y():
                 prev = fp[:, 6, 0:64]
                 for s in (5, 4, 3):
                     u = 2 if s == 3 else 1
                     m = 64 if s == 5 else 128
                     shp = [P, u, m, 2]
-                    ve.tensor_tensor(
+                    nc.vector.tensor_tensor(
                         out=yrec[s][:].rearrange("p (u m w) -> p u m w", u=u, w=2),
                         in0=prev.rearrange("p (u m) -> p u m", u=u).unsqueeze(3).to_broadcast(shp),
                         in1=fp[:, s, 0 : 2 * m].rearrange("p (m w) -> p m w", w=2).unsqueeze(1).to_broadcast(shp),
@@ -152,59 +181,78 @@ def tile_butterflymlp_w_kernel(
                     )
                     prev = yrec[s][:]
 
-            grs = {}
-
-            def g_prod(u, ve):
+            def g_prod(b, u):
                 gr = grp.tile([P, 1024], F32, name="gr", tag="gr", align_bytes=64)
-                ve.tensor_tensor(
+                nc.vector.tensor_tensor(
                     out=gr[:].rearrange("p (m w) -> p m w", w=8),
                     in0=xrec[2][:].rearrange("p (m w) -> p m w", w=8),
                     in1=yrec[3][:, 128 * u : 128 * (u + 1)].unsqueeze(2).to_broadcast([P, 128, 8]),
                     op=ALU.mult,
                 )
-                grs[u] = gr
+                grs[(b, u)] = gr
 
-            def g_out(b, u, banks, eng):
-                for vh in range(2):
-                    pt = bank(banks[vh], [P, 4, P])
-                    for sl in range(4):
-                        v = 4 * vh + sl
-                        nc.tensor.transpose(out=pt[:, sl, :], in_=grs[u][:, 128 * v : 128 * (v + 1)], identity=ident_f[:])
-                    il0 = 8 * u + 4 * vh
-                    copy_on(
-                        eng,
-                        g_mats[b][:].rearrange("p c (h i) -> p c h i", h=4)[:, :, :, il0 : il0 + 4],
-                        pt[:].rearrange("p s (h c) -> p c h s", h=4),
-                    )
+            def g_tr(b, u, vh, bk):
+                pt = bank(bk, [P, 4, P])
+                for sl in range(4):
+                    v = 4 * vh + sl
+                    nc.tensor.transpose(out=pt[:, sl, :], in_=grs[(b, u)][:, 128 * v : 128 * (v + 1)], identity=ident_f[:])
+                pts[("g", b, u, vh)] = pt
 
-            def wh_path(b, bk, eng):
-                pz = bank(bk, [P, 2, P])
-                zw = zh[b][:].bitcast(F32)
-                for r in range(2):
-                    nc.tensor.transpose(out=pz[:, r, :], in_=zw[:, r:256:2], identity=ident_f[:])
-                copy_on(eng, wh32[b][:], pz[:].bitcast(BF16).rearrange("p r (w l) -> p w r l", l=2)[:, 0:80, :, :])
+            def g_ev(b, u, vh, eng):
+                il0 = 8 * u + 4 * vh
+                copy_on(
+                    eng,
+                    g_mats[b][:].rearrange("p c (h i) -> p c h i", h=4)[:, :, :, il0 : il0 + 4],
+                    pts[("g", b, u, vh)][:].rearrange("p s (h c) -> p c h s", h=4),
+                )
 
-            g_copies(0, (0, 1, 2), 0)
-            g_copies(0, (6, 5, 4, 3), 1)
-            g_x(nc.vector)
+            def build_g(b, banks):
+                at(("fpv", b), lambda: g_copies(b, (0, 1, 2), 0))
+                at(("fps", b), lambda: g_copies(b, (6, 5, 4, 3), 1))
+                at(("gx", b), g_x)
+                at(("gy", b), g_y)
+                for u in range(4):
+                    at(("gp", b, u), lambda u=u: g_prod(b, u))
+                    for vh in range(2):
+                        at(("gt", b, u, vh), lambda u=u, vh=vh: g_tr(b, u, vh, banks[(2 * u + vh) % len(banks)]))
+                        at(("ge", b, u, vh), lambda u=u, vh=vh: g_ev(b, u, vh, 1))
+
             xw = x_sb[:].bitcast(F32)
             xg = grp.tile([P, 4, TOK, 4], BF16, name="xg", tag="gr", align_bytes=64)
-            for h in range(2):
+
+            def x_tr(h):
                 px = bank(h, [P, 2, 2, TOK])
                 for g2 in range(2):
                     g = 2 * h + g2
                     for u in range(2):
                         nc.tensor.transpose(out=px[:, g2, u, :], in_=xw[:, 256 * g + u : 256 * (g + 1) : 2], identity=ident_f[:])
-                nc.scalar.copy(out=xg[:, 2 * h : 2 * h + 2, :, :].bitcast(F32), in_=px[:].rearrange("p g u q -> p g q u"))
-            g_y(nc.vector)
-            nc.vector.quantize_mx(out=xq[:].bitcast(FP8X4), scales=xs[:], in_=xg[:].rearrange("p g q t -> p (g q t)"))
-            pb = bank(7, [P, P], BF16)
-            nc.tensor.transpose(out=pb[:], in_=vb[:], identity=ident_b[:])
-            nc.scalar.copy(out=bias32[:], in_=pb[:])
-            wh_path(0, 6, 1)
+                pts[("x", h)] = px
+
+            for h in range(2):
+                at(("xt", h), lambda h=h: x_tr(h))
+                at(("xe", h), lambda h=h: nc.scalar.copy(out=xg[:, 2 * h : 2 * h + 2, :, :].bitcast(F32), in_=pts[("x", h)][:].rearrange("p g u q -> p g q u")))
+            at(("xq",), lambda: nc.vector.quantize_mx(out=xq[:].bitcast(FP8X4), scales=xs[:], in_=xg[:].rearrange("p g q t -> p (g q t)")))
+
+            def vb_tr():
+                pb = bank(7, [P, P], BF16)
+                nc.tensor.transpose(out=pb[:], in_=vb[:], identity=ident_b[:])
+                pts["vb"] = pb
+
+            at(("vt",), vb_tr)
+            at(("ve",), lambda: nc.scalar.copy(out=bias32[:], in_=pts["vb"][:]))
+
+            def zh_tr(b, bk):
+                pz = bank(bk, [P, 2, P])
+                zw = zh[b][:].bitcast(F32)
+                for r in range(2):
+                    nc.tensor.transpose(out=pz[:, r, :], in_=zw[:, r:256:2], identity=ident_f[:])
+                pts[("z", b)] = pz
+
+            for b in range(2):
+                at(("zt", b), lambda b=b: zh_tr(b, 6 if b == 0 else 7))
+                at(("ze", b), lambda b=b: nc.scalar.copy(out=wh32[b][:], in_=pts[("z", b)][:].bitcast(BF16).rearrange("p r (w l) -> p w r l", l=2)[:, 0:80, :, :]))
 
             h0s = {}
-            pms = {}
 
             def mx1(c8):
                 pm = bank(2 + c8 % 2, [P, 4, TOK])
@@ -220,22 +268,20 @@ def tile_butterflymlp_w_kernel(
                             start=(g == 0),
                             stop=(g == 3),
                         )
-                pms[c8] = pm
+                pts[("m", c8)] = pm
 
             def e1(c8):
                 h0 = tmp.tile([P, 4, TOK], F32, name="h0", tag="h0", bufs=3)
                 nc.vector.tensor_tensor(
-                    out=h0[:], in0=pms[c8][:], in1=bias32[:, 4 * c8 : 4 * c8 + 4].unsqueeze(2).to_broadcast([P, 4, TOK]), op=ALU.add
+                    out=h0[:], in0=pts[("m", c8)][:], in1=bias32[:, 4 * c8 : 4 * c8 + 4].unsqueeze(2).to_broadcast([P, 4, TOK]), op=ALU.add
                 )
                 h0s[c8] = h0
-
-            pes = {}
 
             def pe1(c8):
                 pe = bank(4 + c8 % 3, [P, 4, TOK])
                 for cl in range(4):
                     nc.tensor.matmul(out=pe[:, cl, :], lhsT=g_mats[0][:, 4 * c8 + cl, :], rhs=h0s[c8][:, cl, :], start=True, stop=True)
-                pes[c8] = pe
+                pts[("p", c8)] = pe
 
             def pair_tiles(s5, k):
                 lo = k & (2**s5 - 1)
@@ -246,23 +292,16 @@ def tile_butterflymlp_w_kernel(
 
             def ew_src(s5, c):
                 if s5 == 0:
-                    return pes[c // 4][:, c % 4, :]
+                    return pts[("p", c // 4)][:, c % 4, :]
                 return ew_bufs[s5][:, c, :]
 
             def ew_p(s5, k, side):
                 c = pair_tiles(s5, k)[side]
-                if k % 8 in V_SHARE:
-                    w = wh32[0][:, 16 * s5 + k, side, side : side + 1]
-                    if s5 == 4:
-                        nc.vector.tensor_scalar(out=ew_bufs[5][:, c, :], in0=ew_src(4, c), scalar1=w, scalar2=bias32[:, 32 + c : 33 + c], op0=ALU.mult, op1=ALU.add)
-                    else:
-                        nc.vector.tensor_scalar(out=ew_bufs[s5 + 1][:, c, :], in0=ew_src(s5, c), scalar1=w, scalar2=None, op0=ALU.mult)
-                elif s5 == 4:
-                    nc.scalar.activation(
-                        out=ew_bufs[5][:, c, :], in_=ew_src(4, c), func=ACT.Identity, scale=wh32[0][:, 64 + k, side, side : side + 1], bias=bias32[:, 32 + c : 33 + c]
-                    )
+                w = wh32[0][:, 16 * s5 + k, side, side : side + 1]
+                if s5 == 4:
+                    nc.scalar.activation(out=ew_bufs[5][:, c, :], in_=ew_src(4, c), func=ACT.Identity, scale=w, bias=bias32[:, 32 + c : 33 + c])
                 else:
-                    nc.scalar.activation(out=ew_bufs[s5 + 1][:, c, :], in_=ew_src(s5, c), func=ACT.Copy, scale=wh32[0][:, 16 * s5 + k, side, side : side + 1])
+                    nc.scalar.activation(out=ew_bufs[s5 + 1][:, c, :], in_=ew_src(s5, c), func=ACT.Copy, scale=w)
 
             def ew_v(s5, k, side):
                 cs = pair_tiles(s5, k)
@@ -271,34 +310,47 @@ def tile_butterflymlp_w_kernel(
                     out=dst, in0=ew_src(s5, cs[1 - side]), scalar=wh32[0][:, 16 * s5 + k, side, 1 - side : 2 - side], in1=dst, op0=ALU.mult, op1=ALU.add
                 )
 
-            def wave(ops, sides=(0, 1)):
-                for s5, k in ops:
-                    for side in sides:
-                        ew_p(s5, k, side)
-                return ops
+            build_g(0, (0, 1, 7))
+            for c8 in range(8):
+                at(("mx1", c8), lambda c8=c8: mx1(c8))
+                at(("wc", c8), lambda c8=c8: load_wc(c8))
+                at(("e1", c8), lambda c8=c8: e1(c8))
+                at(("pe1", c8), lambda c8=c8: pe1(c8))
+            build_g(1, (0, 1, 7))
+            for s5 in range(5):
+                for k in range(16):
+                    for side in range(2):
+                        at(("p", s5, k, side), lambda s5=s5, k=k, side=side: ew_p(s5, k, side))
+                    at(("v", s5, k), lambda s5=s5, k=k: (ew_v(s5, k, 0), ew_v(s5, k, 1)))
 
-            def wave_v(ops):
-                for s5, k in ops:
-                    for side in (0, 1):
-                        ew_v(s5, k, side)
+            gl = buf_b
+            ta = buf_c
 
-            g_prod(0, nc.vector)
-            g_prod(1, nc.vector)
-            g_out(0, 0, (0, 1), 1)
-            mx1(0)
-            g_prod(2, nc.vector)
-            g_out(0, 1, (7, 0), 1)
-            mx1(1)
-            g_prod(3, nc.vector)
-            g_out(0, 2, (1, 7), 1)
-            e1(0)
-            g_out(0, 3, (0, 1), 1)
-            e1(1)
+            def pe2(g):
+                pe = bank(4 + g % 4, [P, 4, P])
+                for cl in range(4):
+                    c = 4 * g + cl
+                    nc.tensor.matmul(out=pe[:, cl, :], lhsT=gl[:, c, :], rhs=g_mats[1][:, c, :], start=True, stop=True)
+                pts[("q", g)] = pe
+
+            for g in range(8):
+                at(("gelu", g), lambda g=g: nc.scalar.activation(out=gl[:, 4 * g : 4 * g + 4, :], in_=buf_a[:, 4 * g : 4 * g + 4, :], func=ACT.Gelu))
+                at(("pe2", g), lambda g=g: pe2(g))
+                at(
+                    ("ea", g),
+                    lambda g=g: copy_on(
+                        1 - g // 4,
+                        ta[:].rearrange("q u (x c) -> q u x c", x=4)[:, :, :, 4 * g : 4 * g + 4],
+                        pts[("q", g)][:].rearrange("q c (x u) -> q u x c", x=4),
+                    ),
+                )
+
             qmask = tmp.tile([P, 4], F32, name="qmask")
             fh = xrec[1][:, 0:320].rearrange("p (s e) -> p s e", s=5)
             hx = yrec[5]
             hys = {3: yrec[4][:, 0:128], 2: yrec[3][:, 0:256]}
             hmat = xrec[2]
+            exs = {}
 
             def g3_small():
                 nc.vector.tensor_reduce(out=qmask[:], in_=ident_f[:].rearrange("p (x u) -> p x u", x=4), axis=mybir.AxisListType.X, op=ALU.add)
@@ -313,108 +365,22 @@ def tile_butterflymlp_w_kernel(
                     in1=fh[:, 1, :].rearrange("p (u m) -> p u m", u=2).unsqueeze(3).to_broadcast([P, 2, 32, 2]),
                     op=ALU.mult,
                 )
-                hyprev = fh[:, 4, :]
+                prev = fh[:, 4, :]
                 for s in (3, 2):
-                    hy = hys[s]
                     u = 2 ** (4 - s)
                     nc.vector.tensor_tensor(
-                        out=hy[:].rearrange("p (u m w) -> p u m w", u=u, w=2),
-                        in0=hyprev.rearrange("p (u m) -> p u m", u=u).unsqueeze(3).to_broadcast([P, u, 32, 2]),
+                        out=hys[s].rearrange("p (u m w) -> p u m w", u=u, w=2),
+                        in0=prev.rearrange("p (u m) -> p u m", u=u).unsqueeze(3).to_broadcast([P, u, 32, 2]),
                         in1=fh[:, s, :].rearrange("p (m w) -> p m w", w=2).unsqueeze(1).to_broadcast([P, u, 32, 2]),
                         op=ALU.mult,
                     )
-                    hyprev = hy[:]
+                    prev = hys[s]
                 nc.vector.tensor_tensor(
                     out=hmat[:].rearrange("p (u m w) -> p u m w", u=8, w=4),
                     in0=hx[:].rearrange("p (m w) -> p m w", w=4).unsqueeze(1).to_broadcast([P, 8, 32, 4]),
-                    in1=hyprev.rearrange("p (u m) -> p u m", u=8).unsqueeze(3).to_broadcast([P, 8, 32, 4]),
+                    in1=prev.rearrange("p (u m) -> p u m", u=8).unsqueeze(3).to_broadcast([P, 8, 32, 4]),
                     op=ALU.mult,
                 )
-
-
-            def ops_in_round(r):
-                ops = []
-                if r in (6, 10):
-                    ops += [(3, k) for k in range(2 * (r - 6), 2 * (r - 6) + 8)]
-                if r in (3, 5, 7, 9):
-                    ops += [(2, k) for k in range(2 * (r - 3), 2 * (r - 3) + 4)]
-                if 1 <= r <= 8:
-                    ops += [(1, 2 * r - 2), (1, 2 * r - 1)]
-                if r <= 7:
-                    ops += [(0, 2 * r), (0, 2 * r + 1)]
-                return ops
-
-            last_ops = [(4, k) for k in range(16)]
-            extra = {
-                0: lambda: g_copies(1, (0, 1, 2, 6, 5, 4, 3), 1),
-                1: lambda: (g_x(nc.vector), g_y(nc.vector), wh_path(1, 0, 1)),
-                2: lambda: g_prod(0, nc.vector),
-                3: lambda: g_prod(1, nc.vector),
-                4: lambda: g_prod(2, nc.vector),
-                5: lambda: g_prod(3, nc.vector),
-                7: lambda: g_out(1, 0, (0, 1), 1),
-                8: lambda: (g_out(1, 1, (7, 0), 1), g_out(1, 2, (1, 7), 1), wave(last_ops, (0,))),
-                9: lambda: (g_out(1, 3, (0, 1), 1), wave([(3, k) for k in range(8, 16)], (0,))),
-            }
-            for r in range(11):
-                if r + 2 < 8:
-                    mx1(r + 2)
-                if r < 8:
-                    pe1(r)
-                ops = ops_in_round(r)
-                wave(ops, (1,) if r == 10 else (0, 1))
-                wave_v(ops)
-                if r + 2 < 8:
-                    e1(r + 2)
-                if r in extra:
-                    extra[r]()
-
-            bc_b = g_mats[0][:, 16:24, :].rearrange("p c i -> p (c i)").bitcast(BF16)
-            db_b = g_mats[0][:, 24:32, :].rearrange("p c i -> p (c i)").bitcast(BF16)
-            nc.gpsimd.dma_start(out=bc_b, in_=b_con.partition_broadcast(P))
-            nc.gpsimd.dma_start(out=db_b, in_=down_bias.partition_broadcast(P))
-
-            for h in range(2):
-                for q in range(4):
-                    nc.sync.dma_start(
-                        out=pl_con[32 * q : 32 * q + 16, h, :].bitcast(I32), in_=W_con_scales[4 * h : 4 * h + 4, 4 * q : 4 * q + 4, :].bitcast(I32)
-                    )
-            wc = []
-            for g in range(8):
-                t = wpool.tile([P, D_IN], U32, name="wc%d" % g, tag="w", align_bytes=64)
-                nc.sync.dma_start(out=t[:].bitcast(I32), in_=W_con_words[g].rearrange("p n t -> p (n t)").bitcast(I32))
-                wc.append(t)
-
-            gl = buf_b
-            ta = buf_c
-            wave(last_ops, (1,))
-            pe2 = {}
-            for q in range(4):
-                wave_v(last_ops[4 * q : 4 * q + 4])
-                for hi in range(2):
-                    c0 = 4 * q + 16 * hi
-                    nc.scalar.activation(out=gl[:, c0 : c0 + 4, :], in_=buf_a[:, c0 : c0 + 4, :], func=ACT.Gelu)
-                    pe = bank(4 + 2 * (q % 2) + hi, [P, 4, P])
-                    for cl in range(4):
-                        nc.tensor.matmul(out=pe[:, cl, :], lhsT=gl[:, c0 + cl, :], rhs=g_mats[1][:, c0 + cl, :], start=True, stop=True)
-                    pe2[(q, hi)] = pe
-                if q >= 1:
-                    for hi in range(2):
-                        g = q - 1 + 4 * hi
-                        copy_on(
-                            1 - hi,
-                            ta[:].rearrange("q u (x c) -> q u x c", x=4)[:, :, :, 4 * g : 4 * g + 4],
-                            pe2[(q - 1, hi)][:].rearrange("q c (x u) -> q u x c", x=4),
-                        )
-            for hi in range(2):
-                g = 3 + 4 * hi
-                copy_on(
-                    1 - hi,
-                    ta[:].rearrange("q u (x c) -> q u x c", x=4)[:, :, :, 4 * g : 4 * g + 4],
-                    pe2[(3, hi)][:].rearrange("q c (x u) -> q u x c", x=4),
-                )
-
-            exs = {}
 
             def g3_prod(q):
                 ex = tmp.tile([P, 4, 4, 32], F32, name="ex", tag="ex", bufs=2)
@@ -426,61 +392,78 @@ def tile_butterflymlp_w_kernel(
                 )
                 exs[q] = ex
 
-            def g3_out(q, bk, eng):
-                pt = bank(bk, [P, 4, P])
+            def g3_tr(q):
+                pt = bank(2 + q % 2, [P, 4, P])
                 for sl in range(4):
                     nc.tensor.transpose(out=pt[:, sl, :], in_=exs[q][:, sl, :, :].rearrange("p x j -> p (x j)"), identity=ident_f[:])
-                copy_on(
-                    eng,
-                    g3[:, :, 16 * q : 16 * (q + 1)].rearrange("p u (s x) -> p u s x", s=4),
-                    pt[:].rearrange("p s (x u) -> p u s x", x=4),
+                pts[("h", q)] = pt
+
+            at(("g3s",), g3_small)
+            for q in range(8):
+                at(("g3p", q), lambda q=q: g3_prod(q))
+                at(("g3t", q), lambda q=q: g3_tr(q))
+                at(
+                    ("g3e", q),
+                    lambda q=q: nc.scalar.copy(
+                        out=g3[:, :, 16 * q : 16 * (q + 1)].rearrange("p u (s x) -> p u s x", s=4), in_=pts[("h", q)][:].rearrange("p s (x u) -> p u s x", x=4)
+                    ),
                 )
 
             d2 = buf_a
+            t2 = buf_b.rearrange("q (g t) m -> q g t m", t=4)
 
-            def p2_part(u4, bk, eng):
-                pt = bank(bk, [P, 4, TOK])
+            def p2_tr(u4):
+                pt = bank(u4 % 4, [P, 4, TOK])
                 for sl in range(4):
                     nc.tensor.transpose(out=pt[:, sl, :], in_=ta[:, 4 * u4 + sl, :], identity=ident_f[:])
-                copy_on(eng, d2[:, 4 * u4 : 4 * u4 + 4, :], pt[:])
+                pts[("t", u4)] = pt
 
-            g3_small()
-            g3_prod(0)
-            g3_prod(1)
-            for i in range(8):
-                g3_out(i, 2 + i % 2, i % 2)
-                if i + 2 < 8:
-                    g3_prod(i + 2)
-            for i in range(8):
-                p2_part(i, i % 4, i % 2)
+            def pe3(t, f4):
+                pe = bank(4 + (2 * t + f4) % 4, [P, 4, P])
+                for sl in range(4):
+                    u = 16 * f4 + 4 * sl + t
+                    nc.tensor.matmul(out=pe[:, sl, :], lhsT=d2[:, u, :], rhs=g3[:, u, :], start=True, stop=True)
+                pts[("r", t, f4)] = pe
 
-            t2 = buf_b.rearrange("q (g t) m -> q g t m", t=4)
+            for u4 in range(8):
+                at(("p2t", u4), lambda u4=u4: p2_tr(u4))
+                at(("p2e", u4), lambda u4=u4: copy_on(u4 % 2, d2[:, 4 * u4 : 4 * u4 + 4, :], pts[("t", u4)][:]))
             for t in range(4):
                 for f4 in range(2):
-                    pe = bank(4 + (2 * t + f4) % 4, [P, 4, P])
-                    for sl in range(4):
-                        u = 16 * f4 + 4 * sl + t
-                        nc.tensor.matmul(out=pe[:, sl, :], lhsT=d2[:, u, :], rhs=g3[:, u, :], start=True, stop=True)
-                    copy_on(
-                        t % 2,
-                        t2[:, :, t, :].rearrange("q g (a f s) -> q g a f s", a=16, f=2)[:, :, :, f4, :],
-                        pe[:].rearrange("q s (g a) -> q g a s", g=8),
+                    at(("pe3", t, f4), lambda t=t, f4=f4: pe3(t, f4))
+                    at(
+                        ("ec", t, f4),
+                        lambda t=t, f4=f4: copy_on(
+                            t % 2,
+                            t2[:, :, t, :].rearrange("q g (a f s) -> q g a f s", a=16, f=2)[:, :, :, f4, :],
+                            pts[("r", t, f4)][:].rearrange("q s (g a) -> q g a s", g=8),
+                        ),
                     )
 
-            nc.vector.tensor_tensor(out=bsum[:], in0=bc_b, in1=db_b, op=ALU.add)
+            bc_b = g_mats[0][:, 16:24, :].rearrange("p c i -> p (c i)").bitcast(BF16)
+            db_b = g_mats[0][:, 24:32, :].rearrange("p c i -> p (c i)").bitcast(BF16)
+            at(("bl", 0), lambda: nc.gpsimd.dma_start(out=bc_b, in_=b_con.partition_broadcast(P)))
+            at(("bl", 1), lambda: nc.gpsimd.dma_start(out=db_b, in_=down_bias.partition_broadcast(P)))
+            at(("ba",), lambda: nc.vector.tensor_tensor(out=bsum[:], in0=bc_b, in1=db_b, op=ALU.add))
+            run_plan()
 
         with tc.tile_pool(name="lpool", bufs=3) as lpool:
             hq = lpool.tile([P, 8 * TOK], U32, name="hq", bufs=1, align_bytes=64)
             hs = lpool.tile([P, 8 * TOK], U8, name="hs", bufs=1, align_bytes=64)
             acc = [bank(n4, [P, 512]) for n4 in range(4)]
             hbs = {}
+            obs = {}
+            out2 = out.flatten_outer_dims()
 
-            def to_mx(g):
+            def l2_tr(g):
                 p2 = bank(4 + g % 4, [P, 4, TOK])
                 for t in range(4):
                     nc.tensor.transpose(out=p2[:, t, :], in_=t2[:, g, t, :], identity=ident_f[:])
+                pts[("l", g)] = p2
+
+            def l2_ev(g):
                 hb = lpool.tile([P, TOK, 4], BF16, name="hb", tag="hb", align_bytes=64)
-                copy_on(g % 2, hb[:], p2[:].rearrange("m t q -> m q t"))
+                copy_on(g % 2, hb[:], pts[("l", g)][:].rearrange("m t q -> m q t"))
                 hbs[g] = hb
 
             def quant(g):
@@ -500,17 +483,17 @@ def tile_butterflymlp_w_kernel(
                         stop=(g == 7),
                     )
 
-            to_mx(0)
-            to_mx(1)
-            quant(0)
-            for g in range(8):
-                if g + 2 < 8:
-                    to_mx(g + 2)
-                if g + 1 < 8:
-                    quant(g + 1)
-                mx2(g)
-            out2 = out.flatten_outer_dims()
-            for n4 in range(4):
-                o_sb = lpool.tile([P, 512], F32, name="o_sb", tag="o_sb")
+            def out_add(n4):
+                o_sb = lpool.tile([P, 512], F32, name="o_sb", tag="o_sb", bufs=4)
                 nc.vector.tensor_tensor(out=o_sb[:], in0=acc[n4][:], in1=bsum[:, 512 * n4 : 512 * (n4 + 1)], op=ALU.add)
-                nc.sync.dma_start(out=out2[:, 512 * n4 : 512 * (n4 + 1)], in_=o_sb[:])
+                obs[n4] = o_sb
+
+            for g in range(8):
+                at(("lt", g), lambda g=g: l2_tr(g))
+                at(("le", g), lambda g=g: l2_ev(g))
+                at(("lq", g), lambda g=g: quant(g))
+                at(("mx2", g), lambda g=g: mx2(g))
+            for n4 in range(4):
+                at(("oa", n4), lambda n4=n4: out_add(n4))
+                at(("os", n4), lambda n4=n4: nc.sync.dma_start(out=out2[:, 512 * n4 : 512 * (n4 + 1)], in_=obs[n4][:]))
+            run_plan()

@@ -20,7 +20,9 @@ D_IN = 2048
 H = 4096
 NT = H // P
 FLOPS = 2 * 2 * TOK * D_IN * H + 24 * (H // 2) * 6 * TOK
-KEYS = {('fpv', 0): 2.88, ('fps', 0): 2.88, ('gx', 0): 3.25, ('xt', 0): 3.79, ('xt', 1): 4.31, ('gy', 0): 4.56, ('xe', 0): 4.79, ('vt',): 4.83, ('zt', 0): 4.93, ('xe', 1): 5.31, ('gp', 0, 0): 5.35, ('ve',): 5.75, ('ze', 0): 5.87, ('xq',): 6.22, ('gt', 0, 0, 0): 6.60, ('gp', 0, 1): 6.68, ('gt', 0, 0, 1): 7.12, ('gp', 0, 2): 7.55, ('ge', 0, 0, 0): 7.60, ('mx1', 0): 7.64, ('ge', 0, 0, 1): 8.12, ('gp', 0, 3): 8.41, ('gt', 0, 1, 0): 9.24, ('e1', 0): 9.72, ('gt', 0, 1, 1): 9.76, ('fps', 1): 9.82, ('fpv', 1): 10.16, ('mx1', 1): 10.28, ('gx', 1): 10.52, ('ge', 0, 1, 0): 11.03, ('ge', 0, 1, 1): 11.47, ('gy', 1): 11.83, ('gt', 0, 2, 0): 11.88, ('gt', 0, 2, 1): 12.40, ('e1', 1): 12.62, ('ge', 0, 2, 0): 12.88, ('gt', 0, 3, 0): 12.92, ('gp', 1, 0): 13.07, ('ge', 0, 2, 1): 13.40, ('mx1', 2): 13.44, ('ge', 0, 3, 0): 13.92, ('gp', 1, 1): 13.93, ('gp', 1, 2): 14.80, ('gt', 0, 3, 1): 15.04, ('mx1', 3): 15.56, ('e1', 2): 15.67, ('ge', 0, 3, 1): 16.04, ('gp', 1, 3): 16.11, ('pe1', 0): 17.16, ('pe1', 1): 17.62, ('zt', 1): 18.09, ('e1', 3): 18.10, ('p', 0, 0, 0): 18.10, ('p', 0, 0, 1): 18.22, ('p', 0, 1, 0): 18.34, ('mx1', 4): 18.35, ('p', 0, 1, 1): 18.46, ('p', 0, 2, 0): 18.58, ('p', 0, 2, 1): 18.70, ('p', 0, 3, 0): 18.82, ('p', 0, 3, 1): 18.94, ('v', 0, 0): 18.96, ('ze', 1): 19.05, ('v', 0, 1): 19.20, ('v', 0, 2): 19.45, ('p', 1, 0, 0): 19.58, ('v', 0, 3): 19.69, ('p', 1, 1, 0): 19.70, ('p', 1, 0, 1): 19.83, ('g3s',): 19.93, ('p', 1, 1, 1): 19.94, ('pe1', 2): 19.95, ('p', 1, 2, 0): 20.07, ('p', 1, 3, 0): 20.19, ('wc', 0): 20.25, ('p', 1, 2, 1): 20.31, ('wc', 1): 20.32, ('wc', 2): 20.39, ('mx1', 5): 20.42, ('p', 1, 3, 1): 20.43, ('wc', 3): 20.46, ('wc', 4): 20.53, ('p', 0, 4, 0): 20.90, ('p', 0, 4, 1): 21.02, ('p', 0, 5, 0): 21.14, ('p', 0, 5, 1): 21.26, ('v', 1, 0): 21.65, ('v', 1, 1): 21.89, ('pe1', 3): 22.02, ('v', 1, 2): 22.13, ('p', 2, 0, 0): 22.27, ('v', 1, 3): 22.38, ('p', 2, 2, 0): 22.39, ('gt', 1, 0, 0): 22.49, ('wc', 5): 22.50, ('p', 2, 1, 0): 22.51, ('v', 0, 4): 22.62, ('p', 2, 3, 0): 22.63, ('p', 2, 0, 1): 22.76, ('v', 0, 5): 22.86, ('p', 2, 2, 1): 22.87, ('p', 0, 6, 0): 22.99, ('gt', 1, 0, 1): 23.01, ('e1', 4): 23.11, ('p', 2, 1, 1): 23.11, ('p', 2, 3, 1): 23.23, ('p', 1, 4, 0): 23.35, ('p', 1, 5, 0): 23.47, ('gt', 1, 1, 0): 23.53, ('v', 2, 0): 23.55, ('p', 1, 4, 1): 23.59, ('p', 1, 5, 1): 23.71, ('v', 2, 1): 23.79, ('p', 0, 6, 1): 23.82, ('p', 0, 7, 0): 23.94, ('v', 2, 2): 24.03, ('mx1', 6): 24.05, ('p', 0, 7, 1): 24.06, ('p', 3, 0, 0): 24.18, ('v', 2, 3): 24.28, ('p', 3, 4, 0): 24.30, ('p', 3, 1, 0): 24.42, ('v', 1, 4): 24.52, ('p', 3, 5, 0): 24.54, ('ge', 1, 0, 0): 24.65, ('v', 1, 5): 24.76, ('v', 0, 6): 25.01, ('p', 3, 2, 0): 25.09, ('p', 2, 4, 0): 25.21, ('v', 0, 7): 25.25, ('p', 2, 6, 0): 25.33, ('p', 2, 5, 0): 25.45, ('e1', 5): 25.49, ('p', 2, 7, 0): 25.57, ('pe1', 4): 25.65, ('p', 1, 6, 0): 25.69, ('p', 1, 7, 0): 25.80, ('p', 1, 6, 1): 25.92, ('g3p', 0): 25.94, ('p', 1, 7, 1): 26.04, ('gt', 1, 1, 1): 26.12, ('wc', 6): 26.13, ('p', 3, 3, 0): 26.16, ('p', 3, 6, 0): 26.28, ('e1', 6): 26.38, ('p', 3, 7, 0): 26.40, ('ge', 1, 0, 1): 26.52, ('mx1', 7): 26.64, ('v', 1, 6): 26.82, ('p', 0, 8, 0): 26.95, ('v', 1, 7): 27.06, ('p', 0, 8, 1): 27.07, ('p', 0, 9, 0): 27.19, ('g3p', 1): 27.30, ('p', 0, 9, 1): 27.31, ('ge', 1, 1, 0): 27.43, ('v', 0, 8): 27.81, ('p', 2, 4, 1): 27.87, ('p', 2, 5, 1): 27.99, ('v', 0, 9): 28.05, ('p', 2, 6, 1): 28.11, ('p', 2, 7, 1): 28.22, ('pe1', 5): 28.24, ('ge', 1, 1, 1): 28.34, ('v', 2, 4): 28.37, ('v', 2, 5): 28.61, ('pe1', 6): 28.71, ('wc', 7): 28.72, ('p', 1, 8, 0): 28.78, ('v', 2, 6): 28.85, ('p', 1, 8, 1): 28.90, ('p', 1, 9, 0): 29.02, ('v', 2, 7): 29.10, ('p', 1, 9, 1): 29.14, ('gt', 1, 2, 0): 29.17, ('bl', 0): 29.19, ('p', 0, 10, 0): 29.26, ('e1', 7): 29.34, ('p', 0, 10, 1): 29.37, ('p', 0, 11, 0): 29.49, ('p', 0, 11, 1): 29.61, ('gt', 1, 2, 1): 29.69, ('p', 3, 0, 1): 29.73, ('v', 1, 8): 29.78, ('p', 3, 1, 1): 29.85, ('p', 3, 2, 1): 29.97, ('v', 1, 9): 30.02, ('p', 3, 3, 1): 30.09, ('p', 3, 4, 1): 30.20, ('pe1', 7): 30.21, ('v', 0, 10): 30.27, ('p', 3, 5, 1): 30.32, ('p', 3, 6, 1): 30.44, ('v', 0, 11): 30.51, ('p', 3, 7, 1): 30.56, ('p', 0, 12, 0): 30.68, ('gt', 1, 3, 0): 30.68, ('v', 3, 0): 30.75, ('p', 0, 12, 1): 30.80, ('p', 1, 10, 0): 30.92, ('v', 3, 1): 31.00, ('p', 1, 11, 0): 31.03, ('p', 1, 10, 1): 31.15, ('bl', 1): 31.16, ('g3t', 0): 31.20, ('v', 3, 2): 31.24, ('p', 1, 11, 1): 31.27, ('p', 0, 13, 0): 31.39, ('v', 3, 3): 31.48, ('p', 0, 13, 1): 31.51, ('p', 2, 8, 0): 31.63, ('g3t', 1): 31.72, ('v', 3, 4): 31.73, ('p', 2, 9, 0): 31.75, ('p', 2, 10, 0): 31.87, ('v', 3, 5): 31.97, ('p', 2, 11, 0): 31.98, ('p', 0, 14, 0): 32.10, ('v', 3, 6): 32.21, ('p', 0, 14, 1): 32.22, ('p', 0, 15, 0): 32.34, ('v', 3, 7): 32.46, ('p', 0, 15, 1): 32.46, ('ge', 1, 2, 0): 32.58, ('v', 1, 10): 32.70, ('v', 1, 11): 32.94, ('ge', 1, 2, 1): 33.02, ('v', 0, 12): 33.19, ('gt', 1, 3, 1): 33.40, ('v', 0, 13): 33.43, ('p', 2, 8, 1): 33.45, ('p', 2, 9, 1): 33.57, ('v', 0, 14): 33.67, ('p', 2, 10, 1): 33.69, ('p', 2, 11, 1): 33.81, ('v', 0, 15): 33.92, ('p', 1, 12, 0): 33.93, ('p', 1, 13, 0): 34.05, ('v', 2, 8): 34.16, ('p', 1, 12, 1): 34.17, ('p', 1, 13, 1): 34.28, ('v', 2, 9): 34.40, ('p', 1, 14, 0): 34.40, ('p', 1, 15, 0): 34.52, ('p', 1, 14, 1): 34.64, ('v', 2, 10): 34.65, ('p', 1, 15, 1): 34.76, ('p', 4, 0, 0): 34.88, ('v', 2, 11): 34.89, ('p', 4, 1, 0): 35.00, ('p', 4, 2, 0): 35.11, ('v', 1, 12): 35.13, ('p', 4, 3, 0): 35.23, ('p', 4, 4, 0): 35.35, ('v', 1, 13): 35.38, ('p', 4, 5, 0): 35.47, ('p', 4, 6, 0): 35.59, ('v', 1, 14): 35.62, ('p', 4, 7, 0): 35.71, ('p', 4, 8, 0): 35.83, ('v', 1, 15): 35.86, ('p', 4, 9, 0): 35.94, ('p', 4, 10, 0): 36.06, ('g3p', 2): 36.11, ('p', 4, 11, 0): 36.18, ('p', 4, 12, 0): 36.30, ('p', 4, 13, 0): 36.42, ('p', 4, 14, 0): 36.54, ('g3p', 3): 36.55, ('p', 4, 15, 0): 36.66, ('p', 2, 12, 0): 36.78, ('p', 2, 12, 1): 36.89, ('p', 2, 13, 0): 37.01, ('p', 2, 13, 1): 37.13, ('p', 2, 14, 0): 37.25, ('p', 2, 14, 1): 37.37, ('v', 2, 12): 37.39, ('p', 2, 15, 0): 37.49, ('p', 2, 15, 1): 37.61, ('v', 2, 13): 37.64, ('ge', 1, 3, 0): 37.72, ('v', 2, 14): 37.88, ('v', 2, 15): 38.12, ('ge', 1, 3, 1): 38.16, ('ba',): 38.37, ('p', 3, 8, 0): 38.60, ('p', 3, 9, 0): 38.72, ('p', 3, 10, 0): 38.84, ('p', 3, 11, 0): 38.96, ('p', 3, 12, 0): 39.08, ('p', 3, 13, 0): 39.19, ('p', 3, 14, 0): 39.31, ('p', 3, 15, 0): 39.43, ('p', 3, 8, 1): 39.55, ('p', 3, 9, 1): 39.67, ('p', 3, 10, 1): 39.79, ('p', 3, 11, 1): 39.91, ('p', 3, 12, 1): 40.02, ('v', 3, 8): 40.09, ('p', 3, 13, 1): 40.14, ('p', 3, 14, 1): 40.26, ('v', 3, 9): 40.33, ('p', 3, 15, 1): 40.38, ('g3e', 0): 40.50, ('v', 3, 10): 40.57, ('v', 3, 11): 40.82, ('p', 4, 0, 1): 40.94, ('p', 4, 1, 1): 41.06, ('v', 3, 12): 41.06, ('p', 4, 8, 1): 41.17, ('p', 4, 2, 1): 41.29, ('v', 3, 13): 41.30, ('g3t', 2): 41.32, ('p', 4, 9, 1): 41.41, ('p', 4, 3, 1): 41.53, ('v', 3, 14): 41.55, ('p', 4, 10, 1): 41.65, ('p', 4, 4, 1): 41.77, ('v', 3, 15): 41.79, ('p', 4, 11, 1): 41.89, ('p', 4, 5, 1): 42.01, ('v', 4, 0): 42.03, ('p', 4, 12, 1): 42.12, ('p', 4, 6, 1): 42.24, ('v', 4, 1): 42.28, ('p', 4, 13, 1): 42.36, ('p', 4, 7, 1): 42.48, ('v', 4, 2): 42.52, ('p', 4, 14, 1): 42.60, ('p', 4, 15, 1): 42.72, ('v', 4, 3): 42.76, ('g3e', 1): 42.84, ('v', 4, 4): 43.01, ('v', 4, 5): 43.25, ('g3e', 2): 43.27, ('v', 4, 6): 43.49, ('g3t', 3): 43.65, ('gelu', 0): 43.71, ('v', 4, 7): 43.74, ('v', 4, 8): 43.98, ('gelu', 4): 44.15, ('v', 4, 9): 44.22, ('v', 4, 10): 44.46, ('pe2', 0): 44.53, ('gelu', 1): 44.59, ('v', 4, 11): 44.71, ('v', 4, 12): 44.95, ('pe2', 4): 45.00, ('gelu', 5): 45.03, ('v', 4, 13): 45.19, ('v', 4, 14): 45.44, ('gelu', 2): 45.47, ('pe2', 1): 45.47, ('v', 4, 15): 45.68, ('ea', 0): 45.91, ('g3p', 4): 45.92, ('pe2', 5): 45.94, ('gelu', 6): 46.34, ('ea', 4): 46.37, ('pe2', 2): 46.40, ('ea', 1): 46.78, ('g3p', 5): 46.81, ('g3t', 4): 46.87, ('gelu', 3): 47.22, ('ea', 5): 47.25, ('pe2', 6): 47.39, ('gelu', 7): 47.66, ('g3p', 6): 47.87, ('pe2', 3): 48.04, ('ea', 2): 48.10, ('ea', 6): 48.34, ('pe2', 7): 48.51, ('g3e', 3): 48.54, ('g3e', 4): 48.97, ('g3t', 5): 49.35, ('ea', 3): 49.41, ('ea', 7): 49.46, ('g3t', 6): 49.87, ('g3e', 5): 50.35, ('g3p', 7): 50.35, ('p2t', 0): 50.39, ('g3e', 6): 50.87, ('p2t', 1): 50.91, ('p2e', 0): 51.39, ('g3t', 7): 51.43, ('p2e', 1): 51.91, ('p2t', 2): 51.95, ('g3e', 7): 52.43, ('p2t', 4): 52.47, ('p2e', 2): 52.95, ('p2t', 5): 52.99, ('p2e', 4): 53.47, ('p2t', 3): 53.51, ('p2e', 5): 53.99, ('p2t', 6): 54.03, ('p2e', 3): 54.51, ('p2e', 6): 55.03, ('p2t', 7): 55.33, ('pe3', 0, 0): 55.85, ('pe3', 1, 0): 56.32, ('p2e', 7): 56.33, ('ec', 0, 0): 56.80, ('pe3', 0, 1): 57.15, ('ec', 1, 0): 57.27, ('pe3', 1, 1): 57.62, ('pe3', 2, 0): 58.09, ('ec', 0, 1): 58.10, ('pe3', 3, 0): 58.56, ('ec', 1, 1): 58.57, ('pe3', 2, 1): 59.02, ('ec', 2, 0): 59.04, ('pe3', 3, 1): 59.49, ('ec', 3, 0): 59.50, ('ec', 2, 1): 59.97, ('ec', 3, 1): 60.44, ('lt', 0): 61.26, ('lt', 1): 61.78, ('le', 0): 62.26, ('lt', 2): 62.30, ('lq', 0): 62.70, ('le', 1): 62.78, ('lt', 3): 62.82, ('le', 2): 63.30, ('lt', 4): 63.34, ('lq', 1): 63.74, ('le', 3): 63.82, ('mx2', 0): 63.86, ('lq', 2): 63.87, ('le', 4): 64.34, ('mx2', 1): 64.78, ('lq', 3): 64.78, ('lq', 4): 64.91, ('mx2', 2): 65.69, ('lt', 5): 66.61, ('mx2', 3): 67.13, ('le', 5): 67.61, ('lt', 6): 68.04, ('lq', 5): 68.43, ('mx2', 4): 68.56, ('le', 6): 69.04, ('lt', 7): 69.48, ('lq', 6): 69.49, ('mx2', 5): 70.00, ('le', 7): 70.48, ('mx2', 6): 70.92, ('lq', 7): 71.30, ('mx2', 7): 72.00, ('oa', 0): 73.40, ('oa', 1): 73.84, ('os', 0): 74.22, ('oa', 2): 74.28, ('os', 1): 74.66, ('oa', 3): 74.72, ('os', 2): 75.10, ('os', 3): 75.55}
+V_SHARE = (1,)
+GE_ENG = ((1, 1, 1, 1), (1, 1, 1, 1))
+KEYS = {('fpv', 0): 3.00, ('fps', 0): 3.00, ('gx', 0): 3.44, ('xt', 0): 3.91, ('xt', 1): 4.33, ('vt',): 4.74, ('zt', 0): 4.80, ('xe', 0): 4.93, ('gy', 0): 4.93, ('xe', 1): 5.38, ('gp', 0, 0): 5.80, ('ve',): 5.84, ('ze', 0): 5.98, ('xq',): 6.69, ('gp', 0, 1): 7.15, ('gt', 0, 0, 0): 7.19, ('gt', 0, 0, 1): 7.45, ('mx1', 0): 7.85, ('gp', 0, 2): 8.04, ('ge', 0, 0, 0): 8.05, ('ge', 0, 0, 1): 8.50, ('gt', 0, 1, 0): 8.93, ('gp', 0, 3): 8.94, ('gt', 0, 1, 1): 9.27, ('mx1', 1): 9.53, ('e1', 0): 9.83, ('ge', 0, 1, 0): 9.87, ('fpv', 1): 10.30, ('ge', 0, 1, 1): 10.33, ('gt', 0, 2, 0): 10.61, ('gx', 1): 10.74, ('fps', 1): 10.78, ('gt', 0, 2, 1): 10.95, ('gt', 0, 3, 0): 11.28, ('e1', 1): 12.10, ('ge', 0, 2, 0): 12.21, ('ge', 0, 2, 1): 12.67, ('gy', 1): 12.71, ('mx1', 2): 13.00, ('ge', 0, 3, 0): 13.12, ('gp', 1, 0): 13.58, ('w7',): 13.58, ('gt', 0, 3, 1): 14.08, ('zt', 1): 14.42, ('gp', 1, 1): 14.47, ('mx1', 3): 14.76, ('ge', 0, 3, 1): 15.02, ('e1', 2): 15.36, ('ze', 1): 15.48, ('gp', 1, 2): 15.83, ('gt', 1, 0, 0): 15.86, ('pe1', 0): 16.21, ('gp', 1, 3): 16.72, ('ge', 1, 0, 0): 16.81, ('pe1', 1): 17.09, ('g3s',): 17.61, ('p', 0, 0, 0): 17.69, ('p', 0, 0, 1): 17.86, ('mx1', 4): 17.97, ('p', 0, 2, 0): 18.57, ('p', 0, 2, 1): 18.74, ('p', 0, 3, 0): 18.91, ('pe1', 2): 19.05, ('p', 0, 3, 1): 19.07, ('p', 0, 1, 0): 19.09, ('p', 0, 1, 1): 19.23, ('v', 0, 0): 19.38, ('v', 0, 1): 19.67, ('p', 1, 1, 0): 19.97, ('gt', 1, 0, 1): 20.02, ('p', 1, 1, 1): 20.06, ('v', 1, 1): 20.15, ('p', 1, 0, 0): 20.17, ('gt', 1, 0, 2): 20.28, ('v', 0, 2): 20.45, ('p', 1, 0, 1): 20.47, ('gt', 1, 0, 3): 20.54, ('p', 0, 4, 0): 20.63, ('v', 0, 3): 20.74, ('p', 0, 4, 1): 20.80, ('p', 0, 5, 0): 20.97, ('e1', 3): 21.03, ('p', 0, 5, 1): 21.13, ('p', 1, 2, 0): 21.30, ('wc', 0): 21.38, ('wc', 1): 21.45, ('p', 1, 3, 0): 21.47, ('v', 1, 0): 21.50, ('wc', 2): 21.52, ('wc', 3): 21.59, ('p', 1, 2, 1): 21.63, ('wc', 4): 21.66, ('e1', 4): 21.79, ('p', 1, 3, 1): 21.80, ('p', 2, 3, 0): 21.97, ('mx1', 5): 22.00, ('ge', 1, 0, 1): 22.13, ('v', 0, 4): 22.26, ('v', 1, 2): 22.55, ('p', 2, 0, 0): 22.59, ('p', 2, 2, 0): 22.76, ('v', 1, 3): 22.85, ('ge', 1, 0, 2): 22.92, ('pe1', 3): 23.08, ('v', 0, 5): 23.14, ('p', 2, 0, 1): 23.38, ('p', 2, 1, 0): 23.43, ('p', 2, 1, 1): 23.53, ('p', 2, 2, 1): 23.55, ('v', 2, 1): 23.62, ('wc', 5): 23.68, ('p', 2, 3, 1): 23.71, ('p', 1, 4, 0): 23.88, ('e1', 5): 23.91, ('mx1', 6): 24.04, ('p', 1, 4, 1): 24.05, ('p', 1, 5, 0): 24.21, ('v', 2, 0): 24.38, ('p', 1, 5, 1): 24.38, ('p', 3, 5, 0): 24.55, ('v', 2, 2): 24.67, ('p', 0, 6, 0): 24.71, ('p', 0, 6, 1): 24.88, ('v', 2, 3): 24.97, ('p', 0, 7, 0): 25.05, ('pe1', 4): 25.12, ('p', 0, 7, 1): 25.21, ('v', 1, 4): 25.26, ('p', 3, 0, 0): 25.38, ('p', 3, 2, 0): 25.55, ('v', 1, 5): 25.55, ('p', 3, 4, 0): 25.71, ('wc', 6): 25.72, ('e1', 6): 25.85, ('p', 3, 3, 0): 25.88, ('p', 3, 6, 0): 26.05, ('mx1', 7): 26.09, ('p', 2, 4, 0): 26.21, ('v', 0, 6): 26.31, ('p', 2, 6, 0): 26.38, ('p', 2, 5, 0): 26.55, ('v', 0, 7): 26.61, ('p', 2, 7, 0): 26.71, ('p', 0, 8, 0): 26.88, ('p', 3, 1, 0): 26.90, ('g3p', 0): 26.99, ('p', 0, 8, 1): 27.05, ('pe1', 5): 27.16, ('p', 1, 6, 0): 27.21, ('p', 1, 7, 0): 27.38, ('g3p', 1): 27.46, ('p', 1, 6, 1): 27.55, ('p', 1, 7, 1): 27.71, ('wc', 7): 27.76, ('p', 3, 7, 0): 27.88, ('p', 0, 9, 0): 27.93, ('ge', 1, 0, 3): 28.05, ('p', 0, 9, 1): 28.07, ('pe1', 6): 28.13, ('v', 1, 6): 28.22, ('v', 1, 7): 28.51, ('p', 0, 10, 0): 28.73, ('bl', 0): 28.73, ('v', 0, 8): 28.80, ('p', 0, 10, 1): 28.90, ('gt', 1, 1, 0): 29.01, ('p', 2, 4, 1): 29.06, ('v', 0, 9): 29.10, ('p', 2, 6, 1): 29.23, ('gt', 1, 1, 1): 29.27, ('p', 1, 9, 0): 29.39, ('p', 2, 5, 1): 29.40, ('p', 1, 9, 1): 29.48, ('gt', 1, 1, 2): 29.53, ('p', 2, 7, 1): 29.56, ('v', 1, 9): 29.58, ('p', 1, 8, 0): 29.73, ('g3t', 0): 29.79, ('v', 2, 4): 29.87, ('p', 1, 8, 1): 29.90, ('p', 0, 11, 0): 30.06, ('v', 2, 5): 30.16, ('p', 0, 11, 1): 30.23, ('p', 0, 12, 0): 30.40, ('v', 2, 6): 30.46, ('p', 0, 12, 1): 30.56, ('p', 3, 0, 1): 30.73, ('v', 2, 7): 30.75, ('p', 3, 4, 1): 30.90, ('v', 1, 8): 31.04, ('p', 3, 5, 1): 31.06, ('p', 0, 13, 0): 31.23, ('v', 0, 10): 31.34, ('p', 3, 2, 1): 31.40, ('p', 3, 3, 1): 31.56, ('v', 0, 11): 31.63, ('p', 3, 6, 1): 31.73, ('p', 3, 7, 1): 31.90, ('e1', 7): 31.92, ('p', 0, 13, 1): 32.06, ('p', 1, 10, 0): 32.23, ('p', 3, 1, 1): 32.39, ('p', 1, 11, 0): 32.40, ('v', 3, 0): 32.48, ('p', 1, 10, 1): 32.56, ('p', 1, 11, 1): 32.73, ('v', 3, 1): 32.78, ('pe1', 7): 32.89, ('p', 2, 8, 0): 32.90, ('p', 2, 10, 0): 33.06, ('v', 3, 2): 33.07, ('p', 2, 11, 0): 33.23, ('v', 3, 3): 33.36, ('ge', 1, 1, 0): 33.40, ('v', 3, 4): 33.66, ('g3t', 1): 33.77, ('ge', 1, 1, 1): 33.85, ('v', 3, 5): 33.95, ('v', 3, 6): 34.24, ('ge', 1, 1, 2): 34.31, ('gt', 1, 1, 3): 34.35, ('bl', 1): 34.37, ('v', 3, 7): 34.54, ('p', 0, 14, 0): 34.76, ('v', 1, 10): 34.83, ('p', 0, 14, 1): 34.93, ('p', 0, 15, 0): 35.10, ('v', 1, 11): 35.12, ('p', 0, 15, 1): 35.26, ('v', 0, 12): 35.42, ('ge', 1, 1, 3): 35.43, ('v', 0, 13): 35.71, ('p', 2, 8, 1): 35.89, ('p', 2, 9, 0): 36.00, ('p', 2, 10, 1): 36.05, ('p', 2, 9, 1): 36.10, ('v', 2, 9): 36.19, ('p', 2, 11, 1): 36.22, ('p', 1, 12, 0): 36.39, ('v', 0, 14): 36.48, ('p', 1, 12, 1): 36.55, ('p', 1, 13, 0): 36.72, ('v', 2, 8): 36.78, ('p', 1, 13, 1): 36.89, ('p', 4, 0, 0): 37.05, ('v', 2, 10): 37.07, ('p', 4, 2, 0): 37.25, ('v', 2, 11): 37.36, ('p', 1, 14, 0): 37.45, ('p', 1, 15, 0): 37.61, ('v', 1, 12): 37.66, ('p', 4, 3, 0): 37.78, ('v', 1, 13): 37.95, ('p', 4, 4, 0): 37.98, ('p', 4, 5, 0): 38.17, ('v', 0, 15): 38.24, ('p', 4, 6, 0): 38.37, ('p', 4, 1, 0): 38.54, ('p', 4, 7, 0): 38.57, ('p', 4, 9, 0): 38.63, ('p', 3, 9, 0): 38.72, ('p', 4, 8, 0): 38.76, ('g3e', 0): 38.82, ('p', 4, 10, 0): 38.96, ('p', 1, 14, 1): 39.16, ('g3p', 2): 39.28, ('p', 1, 15, 1): 39.32, ('p', 4, 11, 0): 39.49, ('p', 4, 12, 0): 39.69, ('g3e', 1): 39.75, ('p', 4, 13, 0): 39.88, ('p', 4, 14, 0): 40.08, ('v', 1, 14): 40.21, ('g3t', 2): 40.25, ('p', 4, 15, 0): 40.28, ('p', 2, 12, 0): 40.47, ('v', 1, 15): 40.51, ('p', 2, 13, 0): 40.64, ('g3p', 3): 40.80, ('p', 2, 14, 0): 40.81, ('p', 2, 15, 0): 40.97, ('p', 2, 12, 1): 41.14, ('g3e', 2): 41.27, ('p', 2, 13, 1): 41.31, ('p', 2, 14, 1): 41.47, ('p', 2, 15, 1): 41.64, ('g3p', 4): 41.73, ('g3t', 3): 41.77, ('p', 3, 8, 0): 41.81, ('p', 3, 10, 0): 41.97, ('p', 3, 11, 0): 42.14, ('v', 2, 12): 42.20, ('p', 3, 12, 0): 42.31, ('p', 3, 13, 0): 42.47, ('v', 2, 13): 42.49, ('p', 3, 14, 0): 42.64, ('g3t', 4): 42.70, ('v', 2, 14): 42.79, ('p', 3, 15, 0): 42.81, ('p', 3, 8, 1): 42.99, ('v', 2, 15): 43.08, ('p', 3, 12, 1): 43.16, ('p', 3, 13, 1): 43.33, ('p', 3, 9, 1): 43.37, ('v', 3, 9): 43.47, ('p', 3, 10, 1): 43.58, ('p', 3, 14, 1): 43.75, ('v', 3, 8): 43.76, ('p', 3, 11, 1): 43.91, ('v', 3, 12): 44.05, ('p', 3, 15, 1): 44.08, ('v', 3, 10): 44.35, ('p', 4, 0, 1): 44.55, ('v', 3, 11): 44.64, ('p', 4, 8, 1): 44.75, ('v', 3, 13): 44.93, ('p', 4, 4, 1): 44.95, ('p', 4, 2, 1): 45.14, ('v', 3, 14): 45.23, ('p', 4, 10, 1): 45.34, ('v', 3, 15): 45.52, ('p', 4, 3, 1): 45.54, ('p', 4, 5, 1): 45.73, ('p', 4, 1, 1): 45.81, ('p', 4, 9, 1): 45.91, ('p', 4, 11, 1): 45.93, ('v', 4, 0): 46.00, ('p', 4, 6, 1): 46.13, ('v', 4, 1): 46.29, ('p', 4, 7, 1): 46.32, ('p', 4, 12, 1): 46.52, ('v', 4, 2): 46.59, ('p', 4, 13, 1): 46.72, ('v', 4, 3): 46.88, ('p', 4, 14, 1): 46.91, ('p', 4, 15, 1): 47.11, ('v', 4, 4): 47.17, ('v', 4, 5): 47.47, ('gelu', 0): 47.67, ('v', 4, 6): 47.76, ('v', 4, 7): 48.05, ('gelu', 4): 48.13, ('v', 4, 8): 48.35, ('pe2', 0): 48.63, ('v', 4, 9): 48.64, ('gelu', 1): 48.85, ('v', 4, 10): 48.93, ('v', 4, 11): 49.23, ('gelu', 5): 49.30, ('pe2', 4): 49.51, ('v', 4, 12): 49.52, ('v', 4, 13): 49.81, ('gelu', 2): 50.02, ('v', 4, 14): 50.11, ('pe2', 1): 50.40, ('ea', 0): 50.40, ('gelu', 6): 50.48, ('v', 4, 15): 50.86, ('ea', 4): 51.16, ('pe2', 5): 51.28, ('g3e', 3): 51.62, ('gelu', 3): 51.66, ('g3p', 5): 52.09, ('ea', 1): 52.11, ('pe2', 2): 52.16, ('g3e', 4): 52.56, ('gelu', 7): 52.57, ('g3p', 6): 53.02, ('ea', 5): 53.03, ('pe2', 6): 53.04, ('ba',): 53.49, ('pe2', 3): 53.93, ('pe2', 7): 54.81, ('ea', 2): 55.24, ('ea', 3): 55.41, ('g3t', 5): 55.69, ('ea', 6): 55.70, ('g3t', 6): 55.95, ('ea', 7): 56.29, ('g3e', 5): 56.55, ('g3p', 7): 57.02, ('tp', 0, 0): 57.25, ('g3e', 6): 57.49, ('tp', 0, 1): 57.51, ('g3t', 7): 57.99, ('s7', 0, 0): 58.11, ('g3e', 7): 59.28, ('s7', 0, 1): 59.75, ('tp', 1, 0): 59.78, ('s7', 1, 0): 60.92, ('tp', 1, 1): 61.42, ('m8', 0, 0): 61.68, ('s7', 1, 1): 62.28, ('m8', 0, 1): 62.57, ('le', 0, 0): 63.17, ('tp', 2, 0): 63.45, ('tp', 2, 1): 63.96, ('le', 0, 1): 64.05, ('lq', 0, 0): 64.12, ('m8', 1, 0): 64.22, ('s7', 2, 0): 64.31, ('mx2', 0, 0): 65.10, ('lq', 0, 1): 65.48, ('s7', 2, 1): 65.61, ('le', 1, 0): 65.70, ('m8', 1, 1): 66.06, ('lq', 1, 0): 66.78, ('mx2', 0, 1): 67.03, ('le', 1, 1): 67.63, ('mx2', 1, 0): 67.99, ('lq', 1, 1): 68.59, ('tp', 3, 0): 68.87, ('tp', 3, 1): 69.22, ('mx2', 1, 1): 69.48, ('s7', 3, 0): 69.82, ('m8', 2, 0): 70.44, ('s7', 3, 1): 70.99, ('m8', 2, 1): 71.41, ('le', 2, 0): 72.01, ('le', 2, 1): 72.89, ('lq', 2, 0): 72.97, ('m8', 3, 0): 72.97, ('lq', 2, 1): 73.85, ('mx2', 2, 0): 73.85, ('le', 3, 0): 74.45, ('mx2', 2, 1): 74.81, ('lq', 3, 0): 75.40, ('m8', 3, 1): 75.69, ('mx2', 3, 0): 76.66, ('le', 3, 1): 77.26, ('lq', 3, 1): 78.22, ('mx2', 3, 1): 79.04, ('oa', 0): 80.52, ('oa', 1): 80.99, ('oa', 2): 81.45, ('os', 0): 81.49, ('oa', 3): 81.92, ('os', 1): 81.95, ('os', 2): 82.42, ('os', 3): 82.89}
 
 
 def tile_butterflymlp_w_kernel(
@@ -75,6 +77,7 @@ def tile_butterflymlp_w_kernel(
         buf_b = const.tile([P, NT, TOK], F32, name="buf_b")
         buf_c = const.tile([P, NT, TOK], F32, name="buf_c")
         bsum = const.tile([P, D_IN], F32, name="bsum")
+        w7f = const.tile([P, 16, 2, 2], F32, name="w7f")
         bw = (up_weights, down_weights)
         wc = {}
 
@@ -100,6 +103,8 @@ def tile_butterflymlp_w_kernel(
             nc.sync.dma_start(out=zh[0][0:80, :], in_=bw[0][7:12].rearrange("s (k p) r l -> (s k) (p r l)", p=P))
             for q in range(4):
                 nc.sync.dma_start(out=pl_exp[32 * q : 32 * q + 16, :].bitcast(I32), in_=W_exp_scales[:, 4 * q : 4 * q + 4, :].bitcast(I32))
+            w7raw = tmp.tile([P, 4, 16], BF16, name="w7raw")
+            w7src = bw[1][7].rearrange("(c h z t) r l -> h c z (t r l)", c=16, h=4, z=8)
             wx = []
             for c8 in range(8):
                 t = wpool.tile([P, 4, 512], U32, name="wx%d" % c8, tag="w", align_bytes=64)
@@ -111,15 +116,17 @@ def tile_butterflymlp_w_kernel(
                 if c8 == 1:
                     load_raw(1)
                     nc.sync.dma_start(out=zh[1][0:80, :], in_=bw[1][7:12].rearrange("s (k p) r l -> (s k) (p r l)", p=P))
+                    for h in range(4):
+                        nc.sync.dma_start(out=w7raw[:, h, :], in_=w7src[h])
+            sc_view = W_con_scales.rearrange("g (e s) n -> s (g e) n", e=2, s=8)
+            wc_view = W_con_words.rearrange("g (e s l) n t -> s (g e) l (n t)", e=2, s=8, l=8)
             for h in range(2):
                 for q in range(4):
-                    nc.sync.dma_start(
-                        out=pl_con[32 * q : 32 * q + 16, h, :].bitcast(I32), in_=W_con_scales[4 * h : 4 * h + 4, 4 * q : 4 * q + 4, :].bitcast(I32)
-                    )
+                    nc.sync.dma_start(out=pl_con[32 * q : 32 * q + 16, h, :].bitcast(I32), in_=sc_view[4 * h : 4 * h + 4, 4 * q : 4 * q + 4, :].bitcast(I32))
 
             def load_wc(g):
                 t = wpool.tile([P, D_IN], U32, name="wc%d" % g, tag="w", align_bytes=64)
-                nc.sync.dma_start(out=t[:].bitcast(I32), in_=W_con_words[g].rearrange("p n t -> p (n t)").bitcast(I32))
+                nc.sync.dma_start(out=t[:].bitcast(I32), in_=wc_view[g].bitcast(I32))
                 wc[g] = t
 
             fp = tmp.tile([P, 7, 256], BF16, name="fp")
@@ -215,7 +222,7 @@ def tile_butterflymlp_w_kernel(
                     at(("gp", b, u), lambda u=u: g_prod(b, u))
                     for vh in range(2):
                         at(("gt", b, u, vh), lambda u=u, vh=vh: g_tr(b, u, vh, banks[(2 * u + vh) % len(banks)]))
-                        at(("ge", b, u, vh), lambda u=u, vh=vh: g_ev(b, u, vh, 1))
+                        at(("ge", b, u, vh), lambda u=u, vh=vh: g_ev(b, u, vh, GE_ENG[b][u]))
 
             xw = x_sb[:].bitcast(F32)
             xg = grp.tile([P, 4, TOK, 4], BF16, name="xg", tag="gr", align_bytes=64)
@@ -251,6 +258,32 @@ def tile_butterflymlp_w_kernel(
             for b in range(2):
                 at(("zt", b), lambda b=b: zh_tr(b, 6 if b == 0 else 7))
                 at(("ze", b), lambda b=b: nc.scalar.copy(out=wh32[b][:], in_=pts[("z", b)][:].bitcast(BF16).rearrange("p r (w l) -> p w r l", l=2)[:, 0:80, :, :]))
+
+            def g_tr2(i4, t, bk):
+                pt = bank(bk, [P, 4, P])
+                for sl in range(4):
+                    v = 4 * (sl % 2) + t
+                    nc.tensor.transpose(out=pt[:, sl, :], in_=grs[(1, 2 * i4 + sl // 2)][:, 128 * v : 128 * (v + 1)], identity=ident_f[:])
+                pts[("g2", i4, t)] = pt
+
+            def g_ev2(i4, t):
+                copy_on(
+                    GE_ENG[1][t],
+                    g_mats[1][:].rearrange("p c (h t z) -> p c h t z", h=4, t=4)[:, :, :, t, 4 * i4 : 4 * i4 + 4],
+                    pts[("g2", i4, t)][:].rearrange("p s (h c) -> p c h s", h=4),
+                )
+
+            def build_g2(banks):
+                at(("fpv", 1), lambda: g_copies(1, (0, 1, 2), 0))
+                at(("fps", 1), lambda: g_copies(1, (6, 5, 4, 3), 1))
+                at(("gx", 1), g_x)
+                at(("gy", 1), g_y)
+                for u in range(4):
+                    at(("gp", 1, u), lambda u=u: g_prod(1, u))
+                for i4 in range(2):
+                    for t in range(4):
+                        at(("gt", 1, i4, t), lambda i4=i4, t=t: g_tr2(i4, t, banks[(4 * i4 + t) % len(banks)]))
+                        at(("ge", 1, i4, t), lambda i4=i4, t=t: g_ev2(i4, t))
 
             h0s = {}
 
@@ -298,7 +331,12 @@ def tile_butterflymlp_w_kernel(
             def ew_p(s5, k, side):
                 c = pair_tiles(s5, k)[side]
                 w = wh32[0][:, 16 * s5 + k, side, side : side + 1]
-                if s5 == 4:
+                if k % 8 in V_SHARE:
+                    if s5 == 4:
+                        nc.vector.tensor_scalar(out=ew_bufs[5][:, c, :], in0=ew_src(4, c), scalar1=w, scalar2=bias32[:, 32 + c : 33 + c], op0=ALU.mult, op1=ALU.add)
+                    else:
+                        nc.vector.tensor_scalar(out=ew_bufs[s5 + 1][:, c, :], in0=ew_src(s5, c), scalar1=w, scalar2=None, op0=ALU.mult)
+                elif s5 == 4:
                     nc.scalar.activation(out=ew_bufs[5][:, c, :], in_=ew_src(4, c), func=ACT.Identity, scale=w, bias=bias32[:, 32 + c : 33 + c])
                 else:
                     nc.scalar.activation(out=ew_bufs[s5 + 1][:, c, :], in_=ew_src(s5, c), func=ACT.Copy, scale=w)
@@ -316,12 +354,13 @@ def tile_butterflymlp_w_kernel(
                 at(("wc", c8), lambda c8=c8: load_wc(c8))
                 at(("e1", c8), lambda c8=c8: e1(c8))
                 at(("pe1", c8), lambda c8=c8: pe1(c8))
-            build_g(1, (0, 1, 7))
+            build_g2((0, 1, 7))
             for s5 in range(5):
                 for k in range(16):
                     for side in range(2):
                         at(("p", s5, k, side), lambda s5=s5, k=k, side=side: ew_p(s5, k, side))
                     at(("v", s5, k), lambda s5=s5, k=k: (ew_v(s5, k, 0), ew_v(s5, k, 1)))
+
 
             gl = buf_b
             ta = buf_c
@@ -339,55 +378,55 @@ def tile_butterflymlp_w_kernel(
                 at(
                     ("ea", g),
                     lambda g=g: copy_on(
-                        1 - g // 4,
-                        ta[:].rearrange("q u (x c) -> q u x c", x=4)[:, :, :, 4 * g : 4 * g + 4],
-                        pts[("q", g)][:].rearrange("q c (x u) -> q u x c", x=4),
+                        g % 2,
+                        ta[:].rearrange("q b (g e z) -> q b g e z", g=8, e=2)[:, :, g, :, :],
+                        pts[("q", g)][:].rearrange("q (e s) (b z) -> q (s b) e z", e=2, z=8),
                     ),
                 )
 
-            qmask = tmp.tile([P, 4], F32, name="qmask")
-            fh = xrec[1][:, 0:320].rearrange("p (s e) -> p s e", s=5)
-            hx = yrec[5]
-            hys = {3: yrec[4][:, 0:128], 2: yrec[3][:, 0:256]}
-            hmat = xrec[2]
+            at(("w7",), lambda: nc.scalar.copy(out=w7f[:].rearrange("p a r l -> p (a r l)"), in_=w7raw[:].rearrange("p h e -> p (h e)")))
+            zmask = tmp.tile([P, 8], F32, name="zmask")
+            fh = xrec[1][:, 0:256].rearrange("p (s f e) -> p s f e", s=4, f=2)
+            hx = yrec[5][:, 0:128].rearrange("p (f e) -> p f e", f=2)
+            hy = yrec[4][:, 0:128].rearrange("p (f e) -> p f e", f=2)
+            hmat = xrec[2][:, 0:512]
             exs = {}
 
             def g3_small():
-                nc.vector.tensor_reduce(out=qmask[:], in_=ident_f[:].rearrange("p (x u) -> p x u", x=4), axis=mybir.AxisListType.X, op=ALU.add)
-                for s in range(5):
-                    nc.vector.tensor_copy(
-                        out=fh[:, s, :].rearrange("p (r b a l) -> p r b a l", r=2, b=2**s, a=2 ** (4 - s), l=2),
-                        in_=wh32[1][:, 16 * s : 16 * (s + 1), :, :].rearrange("p (a b) r l -> p r b a l", a=2 ** (4 - s), b=2**s),
-                    )
-                nc.vector.tensor_tensor(
-                    out=hx[:].rearrange("p (u m w) -> p u m w", u=2, w=2),
-                    in0=fh[:, 0, :].rearrange("p (m w) -> p m w", w=2).unsqueeze(1).to_broadcast([P, 2, 32, 2]),
-                    in1=fh[:, 1, :].rearrange("p (u m) -> p u m", u=2).unsqueeze(3).to_broadcast([P, 2, 32, 2]),
-                    op=ALU.mult,
-                )
-                prev = fh[:, 4, :]
-                for s in (3, 2):
-                    u = 2 ** (4 - s)
+                nc.vector.tensor_reduce(out=zmask[:], in_=ident_f[:].rearrange("p (h z t) -> p z h t", h=4, z=8), axis=mybir.AxisListType.XY, op=ALU.add)
+                for s in range(4):
+                    for f in range(2):
+                        nc.vector.tensor_copy(
+                            out=fh[:, s, f, :].rearrange("p (r b a l) -> p r b a l", r=2, b=2**s, a=2 ** (3 - s), l=2),
+                            in_=wh32[1][:, 16 * (s + 1) : 16 * (s + 2), :, :].rearrange("p (a b f) r l -> p f r b a l", a=2 ** (3 - s), b=2**s, f=2)[:, f],
+                        )
+                for f in range(2):
                     nc.vector.tensor_tensor(
-                        out=hys[s].rearrange("p (u m w) -> p u m w", u=u, w=2),
-                        in0=prev.rearrange("p (u m) -> p u m", u=u).unsqueeze(3).to_broadcast([P, u, 32, 2]),
-                        in1=fh[:, s, :].rearrange("p (m w) -> p m w", w=2).unsqueeze(1).to_broadcast([P, u, 32, 2]),
+                        out=hx[:, f, :].rearrange("p (u m w) -> p u m w", u=2, w=2),
+                        in0=fh[:, 0, f, :].rearrange("p (m w) -> p m w", w=2).unsqueeze(1).to_broadcast([P, 2, 16, 2]),
+                        in1=fh[:, 1, f, :].rearrange("p (u m) -> p u m", u=2).unsqueeze(3).to_broadcast([P, 2, 16, 2]),
                         op=ALU.mult,
                     )
-                    prev = hys[s]
-                nc.vector.tensor_tensor(
-                    out=hmat[:].rearrange("p (u m w) -> p u m w", u=8, w=4),
-                    in0=hx[:].rearrange("p (m w) -> p m w", w=4).unsqueeze(1).to_broadcast([P, 8, 32, 4]),
-                    in1=prev.rearrange("p (u m) -> p u m", u=8).unsqueeze(3).to_broadcast([P, 8, 32, 4]),
-                    op=ALU.mult,
-                )
+                    nc.vector.tensor_tensor(
+                        out=hy[:, f, :].rearrange("p (u m w) -> p u m w", u=2, w=2),
+                        in0=fh[:, 3, f, :].rearrange("p (u m) -> p u m", u=2).unsqueeze(3).to_broadcast([P, 2, 16, 2]),
+                        in1=fh[:, 2, f, :].rearrange("p (m w) -> p m w", w=2).unsqueeze(1).to_broadcast([P, 2, 16, 2]),
+                        op=ALU.mult,
+                    )
+                for f in range(2):
+                    nc.vector.tensor_tensor(
+                        out=hmat[:, 256 * f : 256 * (f + 1)].rearrange("p (u m w) -> p u m w", u=4, w=4),
+                        in0=hx[:, f, :].rearrange("p (m w) -> p m w", w=4).unsqueeze(1).to_broadcast([P, 4, 16, 4]),
+                        in1=hy[:, f, :].rearrange("p (u m) -> p u m", u=4).unsqueeze(3).to_broadcast([P, 4, 16, 4]),
+                        op=ALU.mult,
+                    )
 
             def g3_prod(q):
-                ex = tmp.tile([P, 4, 4, 32], F32, name="ex", tag="ex", bufs=2)
+                ex = tmp.tile([P, 512], F32, name="ex", tag="ex", bufs=2)
                 nc.vector.tensor_tensor(
-                    out=ex[:],
-                    in0=hmat[:, 128 * q : 128 * (q + 1)].rearrange("p (i j) -> p i j", i=4).unsqueeze(2).to_broadcast([P, 4, 4, 32]),
-                    in1=qmask[:].unsqueeze(1).unsqueeze(3).to_broadcast([P, 4, 4, 32]),
+                    out=ex[:].rearrange("p (a z) -> p a z", z=8),
+                    in0=hmat[:, 64 * q : 64 * (q + 1)].unsqueeze(2).to_broadcast([P, 64, 8]),
+                    in1=zmask[:].unsqueeze(1).to_broadcast([P, 64, 8]),
                     op=ALU.mult,
                 )
                 exs[q] = ex
@@ -395,7 +434,7 @@ def tile_butterflymlp_w_kernel(
             def g3_tr(q):
                 pt = bank(2 + q % 2, [P, 4, P])
                 for sl in range(4):
-                    nc.tensor.transpose(out=pt[:, sl, :], in_=exs[q][:, sl, :, :].rearrange("p x j -> p (x j)"), identity=ident_f[:])
+                    nc.tensor.transpose(out=pt[:, sl, :], in_=exs[q][:, 128 * sl : 128 * (sl + 1)], identity=ident_f[:])
                 pts[("h", q)] = pt
 
             at(("g3s",), g3_small)
@@ -404,41 +443,11 @@ def tile_butterflymlp_w_kernel(
                 at(("g3t", q), lambda q=q: g3_tr(q))
                 at(
                     ("g3e", q),
-                    lambda q=q: nc.scalar.copy(
-                        out=g3[:, :, 16 * q : 16 * (q + 1)].rearrange("p u (s x) -> p u s x", s=4), in_=pts[("h", q)][:].rearrange("p s (x u) -> p u s x", x=4)
+                    lambda q=q: nc.vector.tensor_copy(
+                        out=g3[:].rearrange("p (f h t) (i z) -> p f h t i z", f=2, h=4, z=8)[:, q // 4, :, :, 4 * (q % 4) : 4 * (q % 4) + 4, :],
+                        in_=pts[("h", q)][:].rearrange("p s (h z t) -> p h t s z", h=4, z=8),
                     ),
                 )
-
-            d2 = buf_a
-            t2 = buf_b.rearrange("q (g t) m -> q g t m", t=4)
-
-            def p2_tr(u4):
-                pt = bank(u4 % 4, [P, 4, TOK])
-                for sl in range(4):
-                    nc.tensor.transpose(out=pt[:, sl, :], in_=ta[:, 4 * u4 + sl, :], identity=ident_f[:])
-                pts[("t", u4)] = pt
-
-            def pe3(t, f4):
-                pe = bank(4 + (2 * t + f4) % 4, [P, 4, P])
-                for sl in range(4):
-                    u = 16 * f4 + 4 * sl + t
-                    nc.tensor.matmul(out=pe[:, sl, :], lhsT=d2[:, u, :], rhs=g3[:, u, :], start=True, stop=True)
-                pts[("r", t, f4)] = pe
-
-            for u4 in range(8):
-                at(("p2t", u4), lambda u4=u4: p2_tr(u4))
-                at(("p2e", u4), lambda u4=u4: copy_on(u4 % 2, d2[:, 4 * u4 : 4 * u4 + 4, :], pts[("t", u4)][:]))
-            for t in range(4):
-                for f4 in range(2):
-                    at(("pe3", t, f4), lambda t=t, f4=f4: pe3(t, f4))
-                    at(
-                        ("ec", t, f4),
-                        lambda t=t, f4=f4: copy_on(
-                            t % 2,
-                            t2[:, :, t, :].rearrange("q g (a f s) -> q g a f s", a=16, f=2)[:, :, :, f4, :],
-                            pts[("r", t, f4)][:].rearrange("q s (g a) -> q g a s", g=8),
-                        ),
-                    )
 
             bc_b = g_mats[0][:, 16:24, :].rearrange("p c i -> p (c i)").bitcast(BF16)
             db_b = g_mats[0][:, 24:32, :].rearrange("p c i -> p (c i)").bitcast(BF16)
@@ -451,36 +460,59 @@ def tile_butterflymlp_w_kernel(
             hq = lpool.tile([P, 8 * TOK], U32, name="hq", bufs=1, align_bytes=64)
             hs = lpool.tile([P, 8 * TOK], U8, name="hs", bufs=1, align_bytes=64)
             acc = [bank(n4, [P, 512]) for n4 in range(4)]
+            d2 = buf_a
             hbs = {}
             obs = {}
             out2 = out.flatten_outer_dims()
 
-            def l2_tr(g):
-                p2 = bank(4 + g % 4, [P, 4, TOK])
+            def to_pi(h, half):
+                pt = bank(4 + half, [P, 4, TOK])
+                for sl in range(4):
+                    blk = 16 * (sl % 2) + 4 * h + 2 * half + sl // 2
+                    nc.tensor.transpose(out=pt[:, sl, :], in_=ta[:, blk, :], identity=ident_f[:])
+                    pts[("b", blk)] = pt[:, sl, :]
+
+            def stage7(h, half):
+                for t in (2 * half, 2 * half + 1):
+                    for f7 in range(2):
+                        blk = 16 * f7 + 4 * h + t
+                        nc.vector.tensor_scalar(out=d2[:, blk, :], in0=pts[("b", blk)], scalar1=w7f[:, 4 * h + t, f7, f7 : f7 + 1], scalar2=None, op0=ALU.mult)
+                for t in (2 * half, 2 * half + 1):
+                    for f7 in range(2):
+                        blk = 16 * f7 + 4 * h + t
+                        nc.vector.scalar_tensor_tensor(
+                            out=d2[:, blk, :], in0=pts[("b", 16 * (1 - f7) + 4 * h + t)], scalar=w7f[:, 4 * h + t, f7, 1 - f7 : 2 - f7], in1=d2[:, blk, :], op0=ALU.mult, op1=ALU.add
+                        )
+
+            def stages8(h, f7):
+                po = bank(6 + f7, [P, 4, TOK])
                 for t in range(4):
-                    nc.tensor.transpose(out=p2[:, t, :], in_=t2[:, g, t, :], identity=ident_f[:])
-                pts[("l", g)] = p2
+                    blk = 16 * f7 + 4 * h + t
+                    nc.tensor.matmul(out=po[:, t, :], lhsT=g3[:, blk, :], rhs=d2[:, blk, :], start=True, stop=True)
+                pts[("o", h, f7)] = po
 
-            def l2_ev(g):
+            def l2_ev(h, f7):
                 hb = lpool.tile([P, TOK, 4], BF16, name="hb", tag="hb", align_bytes=64)
-                copy_on(g % 2, hb[:], pts[("l", g)][:].rearrange("m t q -> m q t"))
-                hbs[g] = hb
+                nc.scalar.copy(out=hb[:], in_=pts[("o", h, f7)][:].rearrange("m t q -> m q t"))
+                hbs[(h, f7)] = hb
 
-            def quant(g):
+            def quant(h, f7):
+                s = 4 * f7 + h
                 nc.vector.quantize_mx(
-                    out=hq[:, 128 * g : 128 * (g + 1)].bitcast(FP8X4), scales=hs[:, 128 * g : 128 * (g + 1)], in_=hbs[g][:].rearrange("m q t -> m (q t)")
+                    out=hq[:, 128 * s : 128 * (s + 1)].bitcast(FP8X4), scales=hs[:, 128 * s : 128 * (s + 1)], in_=hbs[(h, f7)][:].rearrange("m q t -> m (q t)")
                 )
 
-            def mx2(g):
+            def mx2(h, f7):
+                s = 4 * f7 + h
                 for n4 in range(4):
                     nc.tensor.matmul_mx(
                         out=acc[n4][:],
-                        lhsT=hq[:, 128 * g : 128 * (g + 1)].bitcast(FP8X4),
-                        lhsT_scale=hs[:, 128 * g : 128 * (g + 1)],
-                        rhs=wc[g][:, 512 * n4 : 512 * (n4 + 1)].bitcast(FP8X4),
-                        rhs_scale=pl_con[4 * (g % 4) : 128, g // 4, 512 * n4 : 512 * (n4 + 1)],
-                        start=(g == 0),
-                        stop=(g == 7),
+                        lhsT=hq[:, 128 * s : 128 * (s + 1)].bitcast(FP8X4),
+                        lhsT_scale=hs[:, 128 * s : 128 * (s + 1)],
+                        rhs=wc[s][:, 512 * n4 : 512 * (n4 + 1)].bitcast(FP8X4),
+                        rhs_scale=pl_con[4 * (s % 4) : 128, s // 4, 512 * n4 : 512 * (n4 + 1)],
+                        start=(h == 0 and f7 == 0),
+                        stop=(h == 3 and f7 == 1),
                     )
 
             def out_add(n4):
@@ -488,11 +520,15 @@ def tile_butterflymlp_w_kernel(
                 nc.vector.tensor_tensor(out=o_sb[:], in0=acc[n4][:], in1=bsum[:, 512 * n4 : 512 * (n4 + 1)], op=ALU.add)
                 obs[n4] = o_sb
 
-            for g in range(8):
-                at(("lt", g), lambda g=g: l2_tr(g))
-                at(("le", g), lambda g=g: l2_ev(g))
-                at(("lq", g), lambda g=g: quant(g))
-                at(("mx2", g), lambda g=g: mx2(g))
+            for h in range(4):
+                for half in range(2):
+                    at(("tp", h, half), lambda h=h, half=half: to_pi(h, half))
+                    at(("s7", h, half), lambda h=h, half=half: stage7(h, half))
+                for f7 in range(2):
+                    at(("m8", h, f7), lambda h=h, f7=f7: stages8(h, f7))
+                    at(("le", h, f7), lambda h=h, f7=f7: l2_ev(h, f7))
+                    at(("lq", h, f7), lambda h=h, f7=f7: quant(h, f7))
+                    at(("mx2", h, f7), lambda h=h, f7=f7: mx2(h, f7))
             for n4 in range(4):
                 at(("oa", n4), lambda n4=n4: out_add(n4))
                 at(("os", n4), lambda n4=n4: nc.sync.dma_start(out=out2[:, 512 * n4 : 512 * (n4 + 1)], in_=obs[n4][:]))

@@ -19,43 +19,21 @@ TOK = 128
 D_IN = 2048
 H = 4096
 NT = H // P
-FLOPS = 2 * 2 * TOK * D_IN * H + 24 * (H // 2) * 6 * TOK
 V_SHARE = (1,)
-GE_ENG = ((1, 1, 1, 1), (1, 1, 1, 1))
-KEYS = {('fpv', 0): 3.00, ('fps', 0): 3.00, ('gx', 0): 3.44, ('xt', 0): 3.91, ('xt', 1): 4.33, ('vt',): 4.74, ('zt', 0): 4.80, ('xe', 0): 4.93, ('gy', 0): 4.93, ('xe', 1): 5.38, ('gp', 0, 0): 5.80, ('ve',): 5.84, ('ze', 0): 5.98, ('xq',): 6.69, ('gp', 0, 1): 7.15, ('gt', 0, 0, 0): 7.19, ('gt', 0, 0, 1): 7.45, ('mx1', 0): 7.85, ('gp', 0, 2): 8.04, ('ge', 0, 0, 0): 8.05, ('ge', 0, 0, 1): 8.50, ('gt', 0, 1, 0): 8.93, ('gp', 0, 3): 8.94, ('gt', 0, 1, 1): 9.27, ('mx1', 1): 9.53, ('e1', 0): 9.83, ('ge', 0, 1, 0): 9.87, ('fpv', 1): 10.30, ('ge', 0, 1, 1): 10.33, ('gt', 0, 2, 0): 10.61, ('gx', 1): 10.74, ('fps', 1): 10.78, ('gt', 0, 2, 1): 10.95, ('gt', 0, 3, 0): 11.28, ('e1', 1): 12.10, ('ge', 0, 2, 0): 12.21, ('ge', 0, 2, 1): 12.67, ('gy', 1): 12.71, ('mx1', 2): 13.00, ('ge', 0, 3, 0): 13.12, ('gp', 1, 0): 13.58, ('w7',): 13.58, ('gt', 0, 3, 1): 14.08, ('zt', 1): 14.42, ('gp', 1, 1): 14.47, ('mx1', 3): 14.76, ('ge', 0, 3, 1): 15.02, ('e1', 2): 15.36, ('ze', 1): 15.48, ('gp', 1, 2): 15.83, ('gt', 1, 0, 0): 15.86, ('pe1', 0): 16.21, ('gp', 1, 3): 16.72, ('ge', 1, 0, 0): 16.81, ('pe1', 1): 17.09, ('g3s',): 17.61, ('p', 0, 0, 0): 17.69, ('p', 0, 0, 1): 17.86, ('mx1', 4): 17.97, ('p', 0, 2, 0): 18.57, ('p', 0, 2, 1): 18.74, ('p', 0, 3, 0): 18.91, ('pe1', 2): 19.05, ('p', 0, 3, 1): 19.07, ('p', 0, 1, 0): 19.09, ('p', 0, 1, 1): 19.23, ('v', 0, 0): 19.38, ('v', 0, 1): 19.67, ('p', 1, 1, 0): 19.97, ('gt', 1, 0, 1): 20.02, ('p', 1, 1, 1): 20.06, ('v', 1, 1): 20.15, ('p', 1, 0, 0): 20.17, ('gt', 1, 0, 2): 20.28, ('v', 0, 2): 20.45, ('p', 1, 0, 1): 20.47, ('gt', 1, 0, 3): 20.54, ('p', 0, 4, 0): 20.63, ('v', 0, 3): 20.74, ('p', 0, 4, 1): 20.80, ('p', 0, 5, 0): 20.97, ('e1', 3): 21.03, ('p', 0, 5, 1): 21.13, ('p', 1, 2, 0): 21.30, ('wc', 0): 21.38, ('wc', 1): 21.45, ('p', 1, 3, 0): 21.47, ('v', 1, 0): 21.50, ('wc', 2): 21.52, ('wc', 3): 21.59, ('p', 1, 2, 1): 21.63, ('wc', 4): 21.66, ('e1', 4): 21.79, ('p', 1, 3, 1): 21.80, ('p', 2, 3, 0): 21.97, ('mx1', 5): 22.00, ('ge', 1, 0, 1): 22.13, ('v', 0, 4): 22.26, ('v', 1, 2): 22.55, ('p', 2, 0, 0): 22.59, ('p', 2, 2, 0): 22.76, ('v', 1, 3): 22.85, ('ge', 1, 0, 2): 22.92, ('pe1', 3): 23.08, ('v', 0, 5): 23.14, ('p', 2, 0, 1): 23.38, ('p', 2, 1, 0): 23.43, ('p', 2, 1, 1): 23.53, ('p', 2, 2, 1): 23.55, ('v', 2, 1): 23.62, ('wc', 5): 23.68, ('p', 2, 3, 1): 23.71, ('p', 1, 4, 0): 23.88, ('e1', 5): 23.91, ('mx1', 6): 24.04, ('p', 1, 4, 1): 24.05, ('p', 1, 5, 0): 24.21, ('v', 2, 0): 24.38, ('p', 1, 5, 1): 24.38, ('p', 3, 5, 0): 24.55, ('v', 2, 2): 24.67, ('p', 0, 6, 0): 24.71, ('p', 0, 6, 1): 24.88, ('v', 2, 3): 24.97, ('p', 0, 7, 0): 25.05, ('pe1', 4): 25.12, ('p', 0, 7, 1): 25.21, ('v', 1, 4): 25.26, ('p', 3, 0, 0): 25.38, ('p', 3, 2, 0): 25.55, ('v', 1, 5): 25.55, ('p', 3, 4, 0): 25.71, ('wc', 6): 25.72, ('e1', 6): 25.85, ('p', 3, 3, 0): 25.88, ('p', 3, 6, 0): 26.05, ('mx1', 7): 26.09, ('p', 2, 4, 0): 26.21, ('v', 0, 6): 26.31, ('p', 2, 6, 0): 26.38, ('p', 2, 5, 0): 26.55, ('v', 0, 7): 26.61, ('p', 2, 7, 0): 26.71, ('p', 0, 8, 0): 26.88, ('p', 3, 1, 0): 26.90, ('g3p', 0): 26.99, ('p', 0, 8, 1): 27.05, ('pe1', 5): 27.16, ('p', 1, 6, 0): 27.21, ('p', 1, 7, 0): 27.38, ('g3p', 1): 27.46, ('p', 1, 6, 1): 27.55, ('p', 1, 7, 1): 27.71, ('wc', 7): 27.76, ('p', 3, 7, 0): 27.88, ('p', 0, 9, 0): 27.93, ('ge', 1, 0, 3): 28.05, ('p', 0, 9, 1): 28.07, ('pe1', 6): 28.13, ('v', 1, 6): 28.22, ('v', 1, 7): 28.51, ('p', 0, 10, 0): 28.73, ('bl', 0): 28.73, ('v', 0, 8): 28.80, ('p', 0, 10, 1): 28.90, ('gt', 1, 1, 0): 29.01, ('p', 2, 4, 1): 29.06, ('v', 0, 9): 29.10, ('p', 2, 6, 1): 29.23, ('gt', 1, 1, 1): 29.27, ('p', 1, 9, 0): 29.39, ('p', 2, 5, 1): 29.40, ('p', 1, 9, 1): 29.48, ('gt', 1, 1, 2): 29.53, ('p', 2, 7, 1): 29.56, ('v', 1, 9): 29.58, ('p', 1, 8, 0): 29.73, ('g3t', 0): 29.79, ('v', 2, 4): 29.87, ('p', 1, 8, 1): 29.90, ('p', 0, 11, 0): 30.06, ('v', 2, 5): 30.16, ('p', 0, 11, 1): 30.23, ('p', 0, 12, 0): 30.40, ('v', 2, 6): 30.46, ('p', 0, 12, 1): 30.56, ('p', 3, 0, 1): 30.73, ('v', 2, 7): 30.75, ('p', 3, 4, 1): 30.90, ('v', 1, 8): 31.04, ('p', 3, 5, 1): 31.06, ('p', 0, 13, 0): 31.23, ('v', 0, 10): 31.34, ('p', 3, 2, 1): 31.40, ('p', 3, 3, 1): 31.56, ('v', 0, 11): 31.63, ('p', 3, 6, 1): 31.73, ('p', 3, 7, 1): 31.90, ('e1', 7): 31.92, ('p', 0, 13, 1): 32.06, ('p', 1, 10, 0): 32.23, ('p', 3, 1, 1): 32.39, ('p', 1, 11, 0): 32.40, ('v', 3, 0): 32.48, ('p', 1, 10, 1): 32.56, ('p', 1, 11, 1): 32.73, ('v', 3, 1): 32.78, ('pe1', 7): 32.89, ('p', 2, 8, 0): 32.90, ('p', 2, 10, 0): 33.06, ('v', 3, 2): 33.07, ('p', 2, 11, 0): 33.23, ('v', 3, 3): 33.36, ('ge', 1, 1, 0): 33.40, ('v', 3, 4): 33.66, ('g3t', 1): 33.77, ('ge', 1, 1, 1): 33.85, ('v', 3, 5): 33.95, ('v', 3, 6): 34.24, ('ge', 1, 1, 2): 34.31, ('gt', 1, 1, 3): 34.35, ('bl', 1): 34.37, ('v', 3, 7): 34.54, ('p', 0, 14, 0): 34.76, ('v', 1, 10): 34.83, ('p', 0, 14, 1): 34.93, ('p', 0, 15, 0): 35.10, ('v', 1, 11): 35.12, ('p', 0, 15, 1): 35.26, ('v', 0, 12): 35.42, ('ge', 1, 1, 3): 35.43, ('v', 0, 13): 35.71, ('p', 2, 8, 1): 35.89, ('p', 2, 9, 0): 36.00, ('p', 2, 10, 1): 36.05, ('p', 2, 9, 1): 36.10, ('v', 2, 9): 36.19, ('p', 2, 11, 1): 36.22, ('p', 1, 12, 0): 36.39, ('v', 0, 14): 36.48, ('p', 1, 12, 1): 36.55, ('p', 1, 13, 0): 36.72, ('v', 2, 8): 36.78, ('p', 1, 13, 1): 36.89, ('p', 4, 0, 0): 37.05, ('v', 2, 10): 37.07, ('p', 4, 2, 0): 37.25, ('v', 2, 11): 37.36, ('p', 1, 14, 0): 37.45, ('p', 1, 15, 0): 37.61, ('v', 1, 12): 37.66, ('p', 4, 3, 0): 37.78, ('v', 1, 13): 37.95, ('p', 4, 4, 0): 37.98, ('p', 4, 5, 0): 38.17, ('v', 0, 15): 38.24, ('p', 4, 6, 0): 38.37, ('p', 4, 1, 0): 38.54, ('p', 4, 7, 0): 38.57, ('p', 4, 9, 0): 38.63, ('p', 3, 9, 0): 38.72, ('p', 4, 8, 0): 38.76, ('g3e', 0): 38.82, ('p', 4, 10, 0): 38.96, ('p', 1, 14, 1): 39.16, ('g3p', 2): 39.28, ('p', 1, 15, 1): 39.32, ('p', 4, 11, 0): 39.49, ('p', 4, 12, 0): 39.69, ('g3e', 1): 39.75, ('p', 4, 13, 0): 39.88, ('p', 4, 14, 0): 40.08, ('v', 1, 14): 40.21, ('g3t', 2): 40.25, ('p', 4, 15, 0): 40.28, ('p', 2, 12, 0): 40.47, ('v', 1, 15): 40.51, ('p', 2, 13, 0): 40.64, ('g3p', 3): 40.80, ('p', 2, 14, 0): 40.81, ('p', 2, 15, 0): 40.97, ('p', 2, 12, 1): 41.14, ('g3e', 2): 41.27, ('p', 2, 13, 1): 41.31, ('p', 2, 14, 1): 41.47, ('p', 2, 15, 1): 41.64, ('g3p', 4): 41.73, ('g3t', 3): 41.77, ('p', 3, 8, 0): 41.81, ('p', 3, 10, 0): 41.97, ('p', 3, 11, 0): 42.14, ('v', 2, 12): 42.20, ('p', 3, 12, 0): 42.31, ('p', 3, 13, 0): 42.47, ('v', 2, 13): 42.49, ('p', 3, 14, 0): 42.64, ('g3t', 4): 42.70, ('v', 2, 14): 42.79, ('p', 3, 15, 0): 42.81, ('p', 3, 8, 1): 42.99, ('v', 2, 15): 43.08, ('p', 3, 12, 1): 43.16, ('p', 3, 13, 1): 43.33, ('p', 3, 9, 1): 43.37, ('v', 3, 9): 43.47, ('p', 3, 10, 1): 43.58, ('p', 3, 14, 1): 43.75, ('v', 3, 8): 43.76, ('p', 3, 11, 1): 43.91, ('v', 3, 12): 44.05, ('p', 3, 15, 1): 44.08, ('v', 3, 10): 44.35, ('p', 4, 0, 1): 44.55, ('v', 3, 11): 44.64, ('p', 4, 8, 1): 44.75, ('v', 3, 13): 44.93, ('p', 4, 4, 1): 44.95, ('p', 4, 2, 1): 45.14, ('v', 3, 14): 45.23, ('p', 4, 10, 1): 45.34, ('v', 3, 15): 45.52, ('p', 4, 3, 1): 45.54, ('p', 4, 5, 1): 45.73, ('p', 4, 1, 1): 45.81, ('p', 4, 9, 1): 45.91, ('p', 4, 11, 1): 45.93, ('v', 4, 0): 46.00, ('p', 4, 6, 1): 46.13, ('v', 4, 1): 46.29, ('p', 4, 7, 1): 46.32, ('p', 4, 12, 1): 46.52, ('v', 4, 2): 46.59, ('p', 4, 13, 1): 46.72, ('v', 4, 3): 46.88, ('p', 4, 14, 1): 46.91, ('p', 4, 15, 1): 47.11, ('v', 4, 4): 47.17, ('v', 4, 5): 47.47, ('gelu', 0): 47.67, ('v', 4, 6): 47.76, ('v', 4, 7): 48.05, ('gelu', 4): 48.13, ('v', 4, 8): 48.35, ('pe2', 0): 48.63, ('v', 4, 9): 48.64, ('gelu', 1): 48.85, ('v', 4, 10): 48.93, ('v', 4, 11): 49.23, ('gelu', 5): 49.30, ('pe2', 4): 49.51, ('v', 4, 12): 49.52, ('v', 4, 13): 49.81, ('gelu', 2): 50.02, ('v', 4, 14): 50.11, ('pe2', 1): 50.40, ('ea', 0): 50.40, ('gelu', 6): 50.48, ('v', 4, 15): 50.86, ('ea', 4): 51.16, ('pe2', 5): 51.28, ('g3e', 3): 51.62, ('gelu', 3): 51.66, ('g3p', 5): 52.09, ('ea', 1): 52.11, ('pe2', 2): 52.16, ('g3e', 4): 52.56, ('gelu', 7): 52.57, ('g3p', 6): 53.02, ('ea', 5): 53.03, ('pe2', 6): 53.04, ('ba',): 53.49, ('pe2', 3): 53.93, ('pe2', 7): 54.81, ('ea', 2): 55.24, ('ea', 3): 55.41, ('g3t', 5): 55.69, ('ea', 6): 55.70, ('g3t', 6): 55.95, ('ea', 7): 56.29, ('g3e', 5): 56.55, ('g3p', 7): 57.02, ('tp', 0, 0): 57.25, ('g3e', 6): 57.49, ('tp', 0, 1): 57.51, ('g3t', 7): 57.99, ('s7', 0, 0): 58.11, ('g3e', 7): 59.28, ('s7', 0, 1): 59.75, ('tp', 1, 0): 59.78, ('s7', 1, 0): 60.92, ('tp', 1, 1): 61.42, ('m8', 0, 0): 61.68, ('s7', 1, 1): 62.28, ('m8', 0, 1): 62.57, ('le', 0, 0): 63.17, ('tp', 2, 0): 63.45, ('tp', 2, 1): 63.96, ('le', 0, 1): 64.05, ('lq', 0, 0): 64.12, ('m8', 1, 0): 64.22, ('s7', 2, 0): 64.31, ('mx2', 0, 0): 65.10, ('lq', 0, 1): 65.48, ('s7', 2, 1): 65.61, ('le', 1, 0): 65.70, ('m8', 1, 1): 66.06, ('lq', 1, 0): 66.78, ('mx2', 0, 1): 67.03, ('le', 1, 1): 67.63, ('mx2', 1, 0): 67.99, ('lq', 1, 1): 68.59, ('tp', 3, 0): 68.87, ('tp', 3, 1): 69.22, ('mx2', 1, 1): 69.48, ('s7', 3, 0): 69.82, ('m8', 2, 0): 70.44, ('s7', 3, 1): 70.99, ('m8', 2, 1): 71.41, ('le', 2, 0): 72.01, ('le', 2, 1): 72.89, ('lq', 2, 0): 72.97, ('m8', 3, 0): 72.97, ('lq', 2, 1): 73.85, ('mx2', 2, 0): 73.85, ('le', 3, 0): 74.45, ('mx2', 2, 1): 74.81, ('lq', 3, 0): 75.40, ('m8', 3, 1): 75.69, ('mx2', 3, 0): 76.66, ('le', 3, 1): 77.26, ('lq', 3, 1): 78.22, ('mx2', 3, 1): 79.04, ('oa', 0): 80.52, ('oa', 1): 80.99, ('oa', 2): 81.45, ('os', 0): 81.49, ('oa', 3): 81.92, ('os', 1): 81.95, ('os', 2): 82.42, ('os', 3): 82.89}
+FLOPS = 2 * 2 * TOK * D_IN * H + 24 * (H // 2) * 6 * TOK
 
 
 def tile_butterflymlp_w_kernel(
     tc, x, W_exp_words, W_exp_scales, b_exp, up_weights, up_bias, down_weights, W_con_words, W_con_scales, b_con, down_bias, out
 ):
     nc = tc.nc
-    plan = []
-
-    def at(key, fn):
-        plan.append((KEYS.get(key, 1000.0 + len(plan)), len(plan), key, fn))
-
-    done = [0]
-
-    def run_plan():
-        items = sorted(plan[done[0] :])
-        done[0] = len(plan)
-        for item in items:
-            item[3]()
-
     with ExitStack() as ctx:
-        ctx.enter_context(tc.manual_schedule())
         const = ctx.enter_context(tc.tile_pool(name="const", bufs=1))
         wpool = ctx.enter_context(tc.tile_pool(name="wpool", bufs=8))
         psum = ctx.enter_context(tc.psum_pool(name="psum", bufs=1))
 
         def bank(i, shape, dtype=F32):
             return psum.tile(shape, dtype, name="bk%d" % i, tag="bk%d" % i)
-
-        def copy_on(eng, o, i):
-            if eng == 0:
-                nc.vector.tensor_copy(out=o, in_=i)
-            else:
-                nc.scalar.copy(out=o, in_=i)
 
         ident_f = const.tile([P, P], F32, name="ident_f")
         make_identity(nc, ident_f[:])
@@ -78,18 +56,17 @@ def tile_butterflymlp_w_kernel(
         buf_c = const.tile([P, NT, TOK], F32, name="buf_c")
         bsum = const.tile([P, D_IN], F32, name="bsum")
         w7f = const.tile([P, 16, 2, 2], F32, name="w7f")
-        bw = (up_weights, down_weights)
-        wc = {}
 
         with tc.tile_pool(name="tmp", bufs=1) as tmp, tc.tile_pool(name="grp", bufs=4) as grp:
+            bw = (up_weights, down_weights)
             raw = [tmp.tile([P, 7, 256], BF16, name="raw_up"), tmp.tile([P, 7, 256], BF16, name="raw_down")]
 
-            def load_raw(b):
+            def load_raw(b, queue):
                 src = bw[b][0:7].rearrange("s (c k) r l -> c s (k r l)", c=NT)
                 for h in range(4):
-                    nc.sync.dma_start(out=raw[b][32 * h : 32 * h + 32, :, :], in_=src)
+                    queue.dma_start(out=raw[b][32 * h : 32 * h + 32, :, :], in_=src)
 
-            load_raw(0)
+            load_raw(0, nc.sync)
             x_sb = grp.tile([P, D_IN], BF16, name="x_sb", tag="gr", align_bytes=64)
             nc.sync.dma_start(out=x_sb[:], in_=x.flatten_outer_dims())
             vb = tmp.tile([P, P], BF16, name="vb")
@@ -114,26 +91,18 @@ def tile_butterflymlp_w_kernel(
                 )
                 wx.append(t)
                 if c8 == 1:
-                    load_raw(1)
+                    load_raw(1, nc.sync)
                     nc.sync.dma_start(out=zh[1][0:80, :], in_=bw[1][7:12].rearrange("s (k p) r l -> (s k) (p r l)", p=P))
                     for h in range(4):
                         nc.sync.dma_start(out=w7raw[:, h, :], in_=w7src[h])
-            sc_view = W_con_scales.rearrange("g (e s) n -> s (g e) n", e=2, s=8)
-            wc_view = W_con_words.rearrange("g (e s l) n t -> s (g e) l (n t)", e=2, s=8, l=8)
-            for h in range(2):
-                for q in range(4):
-                    nc.sync.dma_start(out=pl_con[32 * q : 32 * q + 16, h, :].bitcast(I32), in_=sc_view[4 * h : 4 * h + 4, 4 * q : 4 * q + 4, :].bitcast(I32))
 
-            def load_wc(g):
-                t = wpool.tile([P, D_IN], U32, name="wc%d" % g, tag="w", align_bytes=64)
-                nc.sync.dma_start(out=t[:].bitcast(I32), in_=wc_view[g].bitcast(I32))
-                wc[g] = t
+            def copy_on(eng, o, i):
+                if eng == 0:
+                    nc.vector.tensor_copy(out=o, in_=i)
+                else:
+                    nc.scalar.copy(out=o, in_=i)
 
             fp = tmp.tile([P, 7, 256], BF16, name="fp")
-            xrec = [None, tmp.tile([P, 512], F32, name="xrec1"), tmp.tile([P, 1024], F32, name="xrec2")]
-            yrec = {5: tmp.tile([P, 128], F32, name="yrec5"), 4: tmp.tile([P, 256], F32, name="yrec4"), 3: tmp.tile([P, 512], F32, name="yrec3")}
-            grs = {}
-            pts = {}
 
             def g_copies(b, stages, eng):
                 for s in stages:
@@ -162,11 +131,14 @@ def tile_butterflymlp_w_kernel(
                                 raw[b][q, 6, :].rearrange("p (t b r l) -> p t r b l", t=2, b=32, r=2, l=2)[:, h % 2, h // 2],
                             )
 
-            def g_x():
+            xrec = [None, tmp.tile([P, 512], F32, name="xrec1"), tmp.tile([P, 1024], F32, name="xrec2")]
+            yrec = {5: tmp.tile([P, 128], F32, name="yrec5"), 4: tmp.tile([P, 256], F32, name="yrec4"), 3: tmp.tile([P, 512], F32, name="yrec3")}
+
+            def g_x(ve):
                 prev = fp[:, 0, :]
                 for s in (1, 2):
                     shp = [P, 2, 128, 2**s]
-                    nc.vector.tensor_tensor(
+                    ve.tensor_tensor(
                         out=xrec[s][:].rearrange("p (u m w) -> p u m w", u=2, w=2**s),
                         in0=prev.rearrange("p (m w) -> p m w", w=2**s).unsqueeze(1).to_broadcast(shp),
                         in1=fp[:, s, :].rearrange("p (u m) -> p u m", u=2).unsqueeze(3).to_broadcast(shp),
@@ -174,13 +146,13 @@ def tile_butterflymlp_w_kernel(
                     )
                     prev = xrec[s][:]
 
-            def g_y():
+            def g_y(ve):
                 prev = fp[:, 6, 0:64]
                 for s in (5, 4, 3):
                     u = 2 if s == 3 else 1
                     m = 64 if s == 5 else 128
                     shp = [P, u, m, 2]
-                    nc.vector.tensor_tensor(
+                    ve.tensor_tensor(
                         out=yrec[s][:].rearrange("p (u m w) -> p u m w", u=u, w=2),
                         in0=prev.rearrange("p (u m) -> p u m", u=u).unsqueeze(3).to_broadcast(shp),
                         in1=fp[:, s, 0 : 2 * m].rearrange("p (m w) -> p m w", w=2).unsqueeze(1).to_broadcast(shp),
@@ -188,104 +160,59 @@ def tile_butterflymlp_w_kernel(
                     )
                     prev = yrec[s][:]
 
-            def g_prod(b, u):
+            grs = {}
+
+            def g_prod(u, ve):
                 gr = grp.tile([P, 1024], F32, name="gr", tag="gr", align_bytes=64)
-                nc.vector.tensor_tensor(
+                ve.tensor_tensor(
                     out=gr[:].rearrange("p (m w) -> p m w", w=8),
                     in0=xrec[2][:].rearrange("p (m w) -> p m w", w=8),
                     in1=yrec[3][:, 128 * u : 128 * (u + 1)].unsqueeze(2).to_broadcast([P, 128, 8]),
                     op=ALU.mult,
                 )
-                grs[(b, u)] = gr
+                grs[u] = gr
 
-            def g_tr(b, u, vh, bk):
-                pt = bank(bk, [P, 4, P])
-                for sl in range(4):
-                    v = 4 * vh + sl
-                    nc.tensor.transpose(out=pt[:, sl, :], in_=grs[(b, u)][:, 128 * v : 128 * (v + 1)], identity=ident_f[:])
-                pts[("g", b, u, vh)] = pt
+            def g_out(b, u, banks, eng):
+                for vh in range(2):
+                    pt = bank(banks[vh], [P, 4, P])
+                    for sl in range(4):
+                        v = 4 * vh + sl
+                        nc.tensor.transpose(out=pt[:, sl, :], in_=grs[u][:, 128 * v : 128 * (v + 1)], identity=ident_f[:])
+                    il0 = 8 * u + 4 * vh
+                    copy_on(
+                        eng,
+                        g_mats[b][:].rearrange("p c (h i) -> p c h i", h=4)[:, :, :, il0 : il0 + 4],
+                        pt[:].rearrange("p s (h c) -> p c h s", h=4),
+                    )
 
-            def g_ev(b, u, vh, eng):
-                il0 = 8 * u + 4 * vh
-                copy_on(
-                    eng,
-                    g_mats[b][:].rearrange("p c (h i) -> p c h i", h=4)[:, :, :, il0 : il0 + 4],
-                    pts[("g", b, u, vh)][:].rearrange("p s (h c) -> p c h s", h=4),
-                )
+            def wh_path(b, bk, eng):
+                pz = bank(bk, [P, 2, P])
+                zw = zh[b][:].bitcast(F32)
+                for r in range(2):
+                    nc.tensor.transpose(out=pz[:, r, :], in_=zw[:, r:256:2], identity=ident_f[:])
+                copy_on(eng, wh32[b][:], pz[:].bitcast(BF16).rearrange("p r (w l) -> p w r l", l=2)[:, 0:80, :, :])
 
-            def build_g(b, banks):
-                at(("fpv", b), lambda: g_copies(b, (0, 1, 2), 0))
-                at(("fps", b), lambda: g_copies(b, (6, 5, 4, 3), 1))
-                at(("gx", b), g_x)
-                at(("gy", b), g_y)
-                for u in range(4):
-                    at(("gp", b, u), lambda u=u: g_prod(b, u))
-                    for vh in range(2):
-                        at(("gt", b, u, vh), lambda u=u, vh=vh: g_tr(b, u, vh, banks[(2 * u + vh) % len(banks)]))
-                        at(("ge", b, u, vh), lambda u=u, vh=vh: g_ev(b, u, vh, GE_ENG[b][u]))
-
+            g_copies(0, (0, 1, 2), 0)
+            g_copies(0, (6, 5, 4, 3), 1)
+            g_x(nc.vector)
             xw = x_sb[:].bitcast(F32)
             xg = grp.tile([P, 4, TOK, 4], BF16, name="xg", tag="gr", align_bytes=64)
-
-            def x_tr(h):
+            for h in range(2):
                 px = bank(h, [P, 2, 2, TOK])
                 for g2 in range(2):
                     g = 2 * h + g2
                     for u in range(2):
                         nc.tensor.transpose(out=px[:, g2, u, :], in_=xw[:, 256 * g + u : 256 * (g + 1) : 2], identity=ident_f[:])
-                pts[("x", h)] = px
-
-            for h in range(2):
-                at(("xt", h), lambda h=h: x_tr(h))
-                at(("xe", h), lambda h=h: nc.scalar.copy(out=xg[:, 2 * h : 2 * h + 2, :, :].bitcast(F32), in_=pts[("x", h)][:].rearrange("p g u q -> p g q u")))
-            at(("xq",), lambda: nc.vector.quantize_mx(out=xq[:].bitcast(FP8X4), scales=xs[:], in_=xg[:].rearrange("p g q t -> p (g q t)")))
-
-            def vb_tr():
-                pb = bank(7, [P, P], BF16)
-                nc.tensor.transpose(out=pb[:], in_=vb[:], identity=ident_b[:])
-                pts["vb"] = pb
-
-            at(("vt",), vb_tr)
-            at(("ve",), lambda: nc.scalar.copy(out=bias32[:], in_=pts["vb"][:]))
-
-            def zh_tr(b, bk):
-                pz = bank(bk, [P, 2, P])
-                zw = zh[b][:].bitcast(F32)
-                for r in range(2):
-                    nc.tensor.transpose(out=pz[:, r, :], in_=zw[:, r:256:2], identity=ident_f[:])
-                pts[("z", b)] = pz
-
-            for b in range(2):
-                at(("zt", b), lambda b=b: zh_tr(b, 6 if b == 0 else 7))
-                at(("ze", b), lambda b=b: nc.scalar.copy(out=wh32[b][:], in_=pts[("z", b)][:].bitcast(BF16).rearrange("p r (w l) -> p w r l", l=2)[:, 0:80, :, :]))
-
-            def g_tr2(i4, t, bk):
-                pt = bank(bk, [P, 4, P])
-                for sl in range(4):
-                    v = 4 * (sl % 2) + t
-                    nc.tensor.transpose(out=pt[:, sl, :], in_=grs[(1, 2 * i4 + sl // 2)][:, 128 * v : 128 * (v + 1)], identity=ident_f[:])
-                pts[("g2", i4, t)] = pt
-
-            def g_ev2(i4, t):
-                copy_on(
-                    GE_ENG[1][t],
-                    g_mats[1][:].rearrange("p c (h t z) -> p c h t z", h=4, t=4)[:, :, :, t, 4 * i4 : 4 * i4 + 4],
-                    pts[("g2", i4, t)][:].rearrange("p s (h c) -> p c h s", h=4),
-                )
-
-            def build_g2(banks):
-                at(("fpv", 1), lambda: g_copies(1, (0, 1, 2), 0))
-                at(("fps", 1), lambda: g_copies(1, (6, 5, 4, 3), 1))
-                at(("gx", 1), g_x)
-                at(("gy", 1), g_y)
-                for u in range(4):
-                    at(("gp", 1, u), lambda u=u: g_prod(1, u))
-                for i4 in range(2):
-                    for t in range(4):
-                        at(("gt", 1, i4, t), lambda i4=i4, t=t: g_tr2(i4, t, banks[(4 * i4 + t) % len(banks)]))
-                        at(("ge", 1, i4, t), lambda i4=i4, t=t: g_ev2(i4, t))
+                nc.scalar.copy(out=xg[:, 2 * h : 2 * h + 2, :, :].bitcast(F32), in_=px[:].rearrange("p g u q -> p g q u"))
+            g_y(nc.vector)
+            nc.vector.quantize_mx(out=xq[:].bitcast(FP8X4), scales=xs[:], in_=xg[:].rearrange("p g q t -> p (g q t)"))
+            pb = bank(7, [P, P], BF16)
+            nc.tensor.transpose(out=pb[:], in_=vb[:], identity=ident_b[:])
+            nc.scalar.copy(out=bias32[:], in_=pb[:])
+            wh_path(0, 6, 1)
 
             h0s = {}
+            pms = {}
 
             def mx1(c8):
                 pm = bank(2 + c8 % 2, [P, 4, TOK])
@@ -301,20 +228,22 @@ def tile_butterflymlp_w_kernel(
                             start=(g == 0),
                             stop=(g == 3),
                         )
-                pts[("m", c8)] = pm
+                pms[c8] = pm
 
             def e1(c8):
                 h0 = tmp.tile([P, 4, TOK], F32, name="h0", tag="h0", bufs=3)
                 nc.vector.tensor_tensor(
-                    out=h0[:], in0=pts[("m", c8)][:], in1=bias32[:, 4 * c8 : 4 * c8 + 4].unsqueeze(2).to_broadcast([P, 4, TOK]), op=ALU.add
+                    out=h0[:], in0=pms[c8][:], in1=bias32[:, 4 * c8 : 4 * c8 + 4].unsqueeze(2).to_broadcast([P, 4, TOK]), op=ALU.add
                 )
                 h0s[c8] = h0
+
+            pes = {}
 
             def pe1(c8):
                 pe = bank(4 + c8 % 3, [P, 4, TOK])
                 for cl in range(4):
                     nc.tensor.matmul(out=pe[:, cl, :], lhsT=g_mats[0][:, 4 * c8 + cl, :], rhs=h0s[c8][:, cl, :], start=True, stop=True)
-                pts[("p", c8)] = pe
+                pes[c8] = pe
 
             def pair_tiles(s5, k):
                 lo = k & (2**s5 - 1)
@@ -325,21 +254,23 @@ def tile_butterflymlp_w_kernel(
 
             def ew_src(s5, c):
                 if s5 == 0:
-                    return pts[("p", c // 4)][:, c % 4, :]
+                    return pes[c // 4][:, c % 4, :]
                 return ew_bufs[s5][:, c, :]
 
             def ew_p(s5, k, side):
                 c = pair_tiles(s5, k)[side]
-                w = wh32[0][:, 16 * s5 + k, side, side : side + 1]
                 if k % 8 in V_SHARE:
+                    w = wh32[0][:, 16 * s5 + k, side, side : side + 1]
                     if s5 == 4:
                         nc.vector.tensor_scalar(out=ew_bufs[5][:, c, :], in0=ew_src(4, c), scalar1=w, scalar2=bias32[:, 32 + c : 33 + c], op0=ALU.mult, op1=ALU.add)
                     else:
                         nc.vector.tensor_scalar(out=ew_bufs[s5 + 1][:, c, :], in0=ew_src(s5, c), scalar1=w, scalar2=None, op0=ALU.mult)
                 elif s5 == 4:
-                    nc.scalar.activation(out=ew_bufs[5][:, c, :], in_=ew_src(4, c), func=ACT.Identity, scale=w, bias=bias32[:, 32 + c : 33 + c])
+                    nc.scalar.activation(
+                        out=ew_bufs[5][:, c, :], in_=ew_src(4, c), func=ACT.Identity, scale=wh32[0][:, 64 + k, side, side : side + 1], bias=bias32[:, 32 + c : 33 + c]
+                    )
                 else:
-                    nc.scalar.activation(out=ew_bufs[s5 + 1][:, c, :], in_=ew_src(s5, c), func=ACT.Copy, scale=w)
+                    nc.scalar.activation(out=ew_bufs[s5 + 1][:, c, :], in_=ew_src(s5, c), func=ACT.Copy, scale=wh32[0][:, 16 * s5 + k, side, side : side + 1])
 
             def ew_v(s5, k, side):
                 cs = pair_tiles(s5, k)
@@ -348,49 +279,35 @@ def tile_butterflymlp_w_kernel(
                     out=dst, in0=ew_src(s5, cs[1 - side]), scalar=wh32[0][:, 16 * s5 + k, side, 1 - side : 2 - side], in1=dst, op0=ALU.mult, op1=ALU.add
                 )
 
-            build_g(0, (0, 1, 7))
-            for c8 in range(8):
-                at(("mx1", c8), lambda c8=c8: mx1(c8))
-                at(("wc", c8), lambda c8=c8: load_wc(c8))
-                at(("e1", c8), lambda c8=c8: e1(c8))
-                at(("pe1", c8), lambda c8=c8: pe1(c8))
-            build_g2((0, 1, 7))
-            for s5 in range(5):
-                for k in range(16):
-                    for side in range(2):
-                        at(("p", s5, k, side), lambda s5=s5, k=k, side=side: ew_p(s5, k, side))
-                    at(("v", s5, k), lambda s5=s5, k=k: (ew_v(s5, k, 0), ew_v(s5, k, 1)))
+            def wave(ops, sides=(0, 1)):
+                for s5, k in ops:
+                    for side in sides:
+                        ew_p(s5, k, side)
+                return ops
 
+            def wave_v(ops):
+                for s5, k in ops:
+                    for side in (0, 1):
+                        ew_v(s5, k, side)
 
-            gl = buf_b
-            ta = buf_c
+            g_prod(0, nc.vector)
+            g_prod(1, nc.vector)
+            g_out(0, 0, (0, 1), 1)
+            mx1(0)
+            g_prod(2, nc.vector)
+            g_out(0, 1, (7, 0), 1)
+            mx1(1)
+            g_prod(3, nc.vector)
+            g_out(0, 2, (1, 7), 1)
+            e1(0)
+            g_out(0, 3, (0, 1), 1)
+            e1(1)
 
-            def pe2(g):
-                pe = bank(4 + g % 4, [P, 4, P])
-                for cl in range(4):
-                    c = 4 * g + cl
-                    nc.tensor.matmul(out=pe[:, cl, :], lhsT=gl[:, c, :], rhs=g_mats[1][:, c, :], start=True, stop=True)
-                pts[("q", g)] = pe
-
-            for g in range(8):
-                at(("gelu", g), lambda g=g: nc.scalar.activation(out=gl[:, 4 * g : 4 * g + 4, :], in_=buf_a[:, 4 * g : 4 * g + 4, :], func=ACT.Gelu))
-                at(("pe2", g), lambda g=g: pe2(g))
-                at(
-                    ("ea", g),
-                    lambda g=g: copy_on(
-                        g % 2,
-                        ta[:].rearrange("q b (g e z) -> q b g e z", g=8, e=2)[:, :, g, :, :],
-                        pts[("q", g)][:].rearrange("q (e s) (b z) -> q (s b) e z", e=2, z=8),
-                    ),
-                )
-
-            at(("w7",), lambda: nc.scalar.copy(out=w7f[:].rearrange("p a r l -> p (a r l)"), in_=w7raw[:].rearrange("p h e -> p (h e)")))
             zmask = tmp.tile([P, 8], F32, name="zmask")
             fh = xrec[1][:, 0:256].rearrange("p (s f e) -> p s f e", s=4, f=2)
             hx = yrec[5][:, 0:128].rearrange("p (f e) -> p f e", f=2)
             hy = yrec[4][:, 0:128].rearrange("p (f e) -> p f e", f=2)
             hmat = xrec[2][:, 0:512]
-            exs = {}
 
             def g3_small():
                 nc.vector.tensor_reduce(out=zmask[:], in_=ident_f[:].rearrange("p (h z t) -> p z h t", h=4, z=8), axis=mybir.AxisListType.XY, op=ALU.add)
@@ -413,13 +330,14 @@ def tile_butterflymlp_w_kernel(
                         in1=fh[:, 2, f, :].rearrange("p (m w) -> p m w", w=2).unsqueeze(1).to_broadcast([P, 2, 16, 2]),
                         op=ALU.mult,
                     )
-                for f in range(2):
                     nc.vector.tensor_tensor(
                         out=hmat[:, 256 * f : 256 * (f + 1)].rearrange("p (u m w) -> p u m w", u=4, w=4),
                         in0=hx[:, f, :].rearrange("p (m w) -> p m w", w=4).unsqueeze(1).to_broadcast([P, 4, 16, 4]),
                         in1=hy[:, f, :].rearrange("p (u m) -> p u m", u=4).unsqueeze(3).to_broadcast([P, 4, 16, 4]),
                         op=ALU.mult,
                     )
+
+            exs = {}
 
             def g3_prod(q):
                 ex = tmp.tile([P, 512], F32, name="ex", tag="ex", bufs=2)
@@ -431,105 +349,169 @@ def tile_butterflymlp_w_kernel(
                 )
                 exs[q] = ex
 
-            def g3_tr(q):
-                pt = bank(2 + q % 2, [P, 4, P])
+            def g3_out(q, bk):
+                pt = bank(bk, [P, 4, P])
                 for sl in range(4):
                     nc.tensor.transpose(out=pt[:, sl, :], in_=exs[q][:, 128 * sl : 128 * (sl + 1)], identity=ident_f[:])
-                pts[("h", q)] = pt
-
-            at(("g3s",), g3_small)
-            for q in range(8):
-                at(("g3p", q), lambda q=q: g3_prod(q))
-                at(("g3t", q), lambda q=q: g3_tr(q))
-                at(
-                    ("g3e", q),
-                    lambda q=q: nc.vector.tensor_copy(
-                        out=g3[:].rearrange("p (f h t) (i z) -> p f h t i z", f=2, h=4, z=8)[:, q // 4, :, :, 4 * (q % 4) : 4 * (q % 4) + 4, :],
-                        in_=pts[("h", q)][:].rearrange("p s (h z t) -> p h t s z", h=4, z=8),
-                    ),
+                nc.vector.tensor_copy(
+                    out=g3[:].rearrange("p (f h t) (i z) -> p f h t i z", f=2, h=4, z=8)[:, q // 4, :, :, 4 * (q % 4) : 4 * (q % 4) + 4, :],
+                    in_=pt[:].rearrange("p s (h z t) -> p h t s z", h=4, z=8),
                 )
+
+            def g_out2(i4, t, bk, eng):
+                pt = bank(bk, [P, 4, P])
+                for sl in range(4):
+                    v = 4 * (sl % 2) + t
+                    nc.tensor.transpose(out=pt[:, sl, :], in_=grs[2 * i4 + sl // 2][:, 128 * v : 128 * (v + 1)], identity=ident_f[:])
+                copy_on(
+                    eng,
+                    g_mats[1][:].rearrange("p c (h t z) -> p c h t z", h=4, t=4)[:, :, :, t, 4 * i4 : 4 * i4 + 4],
+                    pt[:].rearrange("p s (h c) -> p c h s", h=4),
+                )
+
+            def ops_in_round(r):
+                ops = []
+                if r in (6, 10):
+                    ops += [(3, k) for k in range(2 * (r - 6), 2 * (r - 6) + 8)]
+                if r in (3, 5, 7, 9):
+                    ops += [(2, k) for k in range(2 * (r - 3), 2 * (r - 3) + 4)]
+                if 1 <= r <= 8:
+                    ops += [(1, 2 * r - 2), (1, 2 * r - 1)]
+                if r <= 7:
+                    ops += [(0, 2 * r), (0, 2 * r + 1)]
+                return ops
+
+            last_ops = [(4, k) for k in range(16)]
+            extra = {
+                0: lambda: g_copies(1, (0, 1, 2, 6, 5, 4, 3), 1),
+                1: lambda: (g_x(nc.vector), g_y(nc.vector), wh_path(1, 0, 1), nc.scalar.copy(out=w7f[:].rearrange("p a r l -> p (a r l)"), in_=w7raw[:].rearrange("p h e -> p (h e)"))),
+                2: lambda: (g_prod(0, nc.vector), g_prod(1, nc.vector), g_prod(2, nc.vector), g_prod(3, nc.vector), g3_small(), g3_prod(0), g3_prod(1)),
+                6: lambda: (g_out2(0, 0, 0, 1), g_out2(0, 1, 1, 1)),
+                7: lambda: (g_out2(0, 2, 7, 1), g_out2(0, 3, 0, 1)),
+                8: lambda: (g_out2(1, 0, 1, 1), g_out2(1, 1, 7, 1), g_out2(1, 2, 0, 1), g_out2(1, 3, 1, 1), wave(last_ops, (0,))),
+                9: lambda: (g3_out(0, 7), g3_prod(2), g3_out(1, 0), g3_prod(3), wave([(3, k) for k in range(8, 16)], (0,))),
+                10: lambda: (g3_out(2, 1), g3_prod(4), g3_out(3, 7), g3_prod(5)),
+            }
+            for r in range(11):
+                if r + 2 < 8:
+                    mx1(r + 2)
+                if r < 8:
+                    pe1(r)
+                ops = ops_in_round(r)
+                wave(ops, (1,) if r == 10 else (0, 1))
+                wave_v(ops)
+                if r + 2 < 8:
+                    e1(r + 2)
+                if r in extra:
+                    extra[r]()
 
             bc_b = g_mats[0][:, 16:24, :].rearrange("p c i -> p (c i)").bitcast(BF16)
             db_b = g_mats[0][:, 24:32, :].rearrange("p c i -> p (c i)").bitcast(BF16)
-            at(("bl", 0), lambda: nc.gpsimd.dma_start(out=bc_b, in_=b_con.partition_broadcast(P)))
-            at(("bl", 1), lambda: nc.gpsimd.dma_start(out=db_b, in_=down_bias.partition_broadcast(P)))
-            at(("ba",), lambda: nc.vector.tensor_tensor(out=bsum[:], in0=bc_b, in1=db_b, op=ALU.add))
-            run_plan()
+            nc.gpsimd.dma_start(out=bc_b, in_=b_con.partition_broadcast(P))
+            nc.gpsimd.dma_start(out=db_b, in_=down_bias.partition_broadcast(P))
+
+            sc_view = W_con_scales.rearrange("g (e s) n -> s (g e) n", e=2, s=8)
+            for h in range(2):
+                for q in range(4):
+                    nc.sync.dma_start(out=pl_con[32 * q : 32 * q + 16, h, :].bitcast(I32), in_=sc_view[4 * h : 4 * h + 4, 4 * q : 4 * q + 4, :].bitcast(I32))
+            wc_view = W_con_words.rearrange("g (e s l) n t -> s (g e) l (n t)", e=2, s=8, l=8)
+            wc = []
+            for s in range(8):
+                t = wpool.tile([P, D_IN], U32, name="wc%d" % s, tag="w", align_bytes=64)
+                nc.sync.dma_start(out=t[:].bitcast(I32), in_=wc_view[s].bitcast(I32))
+                wc.append(t)
+
+            gl = buf_b
+            ta = buf_c
+            wave(last_ops, (1,))
+            for q in range(4):
+                wave_v(last_ops[4 * q : 4 * q + 4])
+                for hi in range(2):
+                    c0 = 4 * q + 16 * hi
+                    g = q + 4 * hi
+                    nc.scalar.activation(out=gl[:, c0 : c0 + 4, :], in_=buf_a[:, c0 : c0 + 4, :], func=ACT.Gelu)
+                    pe = bank(4 + 2 * (q % 2) + hi, [P, 4, P])
+                    for cl in range(4):
+                        nc.tensor.matmul(out=pe[:, cl, :], lhsT=gl[:, c0 + cl, :], rhs=g_mats[1][:, c0 + cl, :], start=True, stop=True)
+                    copy_on(
+                        1,
+                        ta[:].rearrange("q b (g e z) -> q b g e z", g=8, e=2)[:, :, g, :, :],
+                        pe[:].rearrange("q (e s) (b z) -> q (s b) e z", e=2, z=8),
+                    )
+                if q < 2:
+                    g3_out(4 + 2 * q, 2)
+                    if q == 0:
+                        g3_prod(6)
+                        g3_prod(7)
+                    g3_out(5 + 2 * q, 3)
+
+            nc.vector.tensor_tensor(out=bsum[:], in0=bc_b, in1=db_b, op=ALU.add)
 
         with tc.tile_pool(name="lpool", bufs=3) as lpool:
             hq = lpool.tile([P, 8 * TOK], U32, name="hq", bufs=1, align_bytes=64)
             hs = lpool.tile([P, 8 * TOK], U8, name="hs", bufs=1, align_bytes=64)
             acc = [bank(n4, [P, 512]) for n4 in range(4)]
             d2 = buf_a
+            trs = {}
+            outs = {}
             hbs = {}
-            obs = {}
-            out2 = out.flatten_outer_dims()
 
-            def to_pi(h, half):
-                pt = bank(4 + half, [P, 4, TOK])
-                for sl in range(4):
-                    blk = 16 * (sl % 2) + 4 * h + 2 * half + sl // 2
-                    nc.tensor.transpose(out=pt[:, sl, :], in_=ta[:, blk, :], identity=ident_f[:])
-                    pts[("b", blk)] = pt[:, sl, :]
+            def to_pi(h):
+                for half in range(2):
+                    pt = bank(4 + half, [P, 4, TOK])
+                    for sl in range(4):
+                        blk = 16 * (sl % 2) + 4 * h + 2 * half + sl // 2
+                        nc.tensor.transpose(out=pt[:, sl, :], in_=ta[:, blk, :], identity=ident_f[:])
+                        trs[blk] = pt[:, sl, :]
 
-            def stage7(h, half):
-                for t in (2 * half, 2 * half + 1):
-                    for f7 in range(2):
-                        blk = 16 * f7 + 4 * h + t
-                        nc.vector.tensor_scalar(out=d2[:, blk, :], in0=pts[("b", blk)], scalar1=w7f[:, 4 * h + t, f7, f7 : f7 + 1], scalar2=None, op0=ALU.mult)
-                for t in (2 * half, 2 * half + 1):
-                    for f7 in range(2):
-                        blk = 16 * f7 + 4 * h + t
-                        nc.vector.scalar_tensor_tensor(
-                            out=d2[:, blk, :], in0=pts[("b", 16 * (1 - f7) + 4 * h + t)], scalar=w7f[:, 4 * h + t, f7, 1 - f7 : 2 - f7], in1=d2[:, blk, :], op0=ALU.mult, op1=ALU.add
-                        )
-
-            def stages8(h, f7):
-                po = bank(6 + f7, [P, 4, TOK])
+            def stage7(h):
                 for t in range(4):
-                    blk = 16 * f7 + 4 * h + t
-                    nc.tensor.matmul(out=po[:, t, :], lhsT=g3[:, blk, :], rhs=d2[:, blk, :], start=True, stop=True)
-                pts[("o", h, f7)] = po
+                    ba = 4 * h + t
+                    bb = ba + 16
+                    w = w7f[:, 4 * h + t, :, :]
+                    nc.vector.tensor_scalar(out=d2[:, ba, :], in0=trs[ba], scalar1=w[:, 0, 0:1], scalar2=None, op0=ALU.mult)
+                    nc.vector.tensor_scalar(out=d2[:, bb, :], in0=trs[bb], scalar1=w[:, 1, 1:2], scalar2=None, op0=ALU.mult)
+                    nc.vector.scalar_tensor_tensor(out=d2[:, ba, :], in0=trs[bb], scalar=w[:, 0, 1:2], in1=d2[:, ba, :], op0=ALU.mult, op1=ALU.add)
+                    nc.vector.scalar_tensor_tensor(out=d2[:, bb, :], in0=trs[ba], scalar=w[:, 1, 0:1], in1=d2[:, bb, :], op0=ALU.mult, op1=ALU.add)
 
-            def l2_ev(h, f7):
-                hb = lpool.tile([P, TOK, 4], BF16, name="hb", tag="hb", align_bytes=64)
-                nc.scalar.copy(out=hb[:], in_=pts[("o", h, f7)][:].rearrange("m t q -> m q t"))
-                hbs[(h, f7)] = hb
-
-            def quant(h, f7):
-                s = 4 * f7 + h
-                nc.vector.quantize_mx(
-                    out=hq[:, 128 * s : 128 * (s + 1)].bitcast(FP8X4), scales=hs[:, 128 * s : 128 * (s + 1)], in_=hbs[(h, f7)][:].rearrange("m q t -> m (q t)")
-                )
-
-            def mx2(h, f7):
-                s = 4 * f7 + h
-                for n4 in range(4):
-                    nc.tensor.matmul_mx(
-                        out=acc[n4][:],
-                        lhsT=hq[:, 128 * s : 128 * (s + 1)].bitcast(FP8X4),
-                        lhsT_scale=hs[:, 128 * s : 128 * (s + 1)],
-                        rhs=wc[s][:, 512 * n4 : 512 * (n4 + 1)].bitcast(FP8X4),
-                        rhs_scale=pl_con[4 * (s % 4) : 128, s // 4, 512 * n4 : 512 * (n4 + 1)],
-                        start=(h == 0 and f7 == 0),
-                        stop=(h == 3 and f7 == 1),
+            def stages8(h):
+                for f7 in range(2):
+                    po = bank(6 + f7, [P, 4, TOK])
+                    for t in range(4):
+                        blk = 16 * f7 + 4 * h + t
+                        nc.tensor.matmul(out=po[:, t, :], lhsT=g3[:, blk, :], rhs=d2[:, blk, :], start=True, stop=True)
+                    s = 4 * f7 + h
+                    hb = lpool.tile([P, TOK, 4], BF16, name="hb", tag="hb", align_bytes=64)
+                    nc.scalar.copy(out=hb[:], in_=po[:].rearrange("m t q -> m q t"))
+                    nc.vector.quantize_mx(
+                        out=hq[:, 128 * s : 128 * (s + 1)].bitcast(FP8X4), scales=hs[:, 128 * s : 128 * (s + 1)], in_=hb[:].rearrange("m q t -> m (q t)")
                     )
 
-            def out_add(n4):
+            def mx2(h):
+                for f7 in range(2):
+                    s = 4 * f7 + h
+                    for n4 in range(4):
+                        nc.tensor.matmul_mx(
+                            out=acc[n4][:],
+                            lhsT=hq[:, 128 * s : 128 * (s + 1)].bitcast(FP8X4),
+                            lhsT_scale=hs[:, 128 * s : 128 * (s + 1)],
+                            rhs=wc[s][:, 512 * n4 : 512 * (n4 + 1)].bitcast(FP8X4),
+                            rhs_scale=pl_con[4 * (s % 4) : 128, s // 4, 512 * n4 : 512 * (n4 + 1)],
+                            start=(h == 0 and f7 == 0),
+                            stop=(h == 3 and f7 == 1),
+                        )
+
+            to_pi(0)
+            stage7(0)
+            for h in range(4):
+                if h + 1 < 4:
+                    to_pi(h + 1)
+                stages8(h)
+                if h + 1 < 4:
+                    stage7(h + 1)
+                mx2(h)
+            out2 = out.flatten_outer_dims()
+            for n4 in range(4):
                 o_sb = lpool.tile([P, 512], F32, name="o_sb", tag="o_sb", bufs=4)
                 nc.vector.tensor_tensor(out=o_sb[:], in0=acc[n4][:], in1=bsum[:, 512 * n4 : 512 * (n4 + 1)], op=ALU.add)
-                obs[n4] = o_sb
-
-            for h in range(4):
-                for half in range(2):
-                    at(("tp", h, half), lambda h=h, half=half: to_pi(h, half))
-                    at(("s7", h, half), lambda h=h, half=half: stage7(h, half))
-                for f7 in range(2):
-                    at(("m8", h, f7), lambda h=h, f7=f7: stages8(h, f7))
-                    at(("le", h, f7), lambda h=h, f7=f7: l2_ev(h, f7))
-                    at(("lq", h, f7), lambda h=h, f7=f7: quant(h, f7))
-                    at(("mx2", h, f7), lambda h=h, f7=f7: mx2(h, f7))
-            for n4 in range(4):
-                at(("oa", n4), lambda n4=n4: out_add(n4))
-                at(("os", n4), lambda n4=n4: nc.sync.dma_start(out=out2[:, 512 * n4 : 512 * (n4 + 1)], in_=obs[n4][:]))
-            run_plan()
+                nc.sync.dma_start(out=out2[:, 512 * n4 : 512 * (n4 + 1)], in_=o_sb[:])

@@ -19,7 +19,7 @@ TOK = 128
 D_IN = 2048
 H = 4096
 NT = H // P
-V_SHARE = (1,)
+V_SHARE = ()
 FLOPS = 2 * 2 * TOK * D_IN * H + 24 * (H // 2) * 6 * TOK
 
 
@@ -82,6 +82,10 @@ def tile_butterflymlp_w_kernel(
                 nc.sync.dma_start(out=pl_exp[32 * q : 32 * q + 16, :].bitcast(I32), in_=W_exp_scales[:, 4 * q : 4 * q + 4, :].bitcast(I32))
             w7raw = tmp.tile([P, 4, 16], BF16, name="w7raw")
             w7src = bw[1][7].rearrange("(c h z t) r l -> h c z (t r l)", c=16, h=4, z=8)
+            load_raw(1, nc.sync)
+            nc.sync.dma_start(out=zh[1][0:80, :], in_=bw[1][7:12].rearrange("s (k p) r l -> (s k) (p r l)", p=P))
+            for h in range(4):
+                nc.sync.dma_start(out=w7raw[:, h, :], in_=w7src[h])
             wx = []
             for c8 in range(8):
                 t = wpool.tile([P, 4, 512], U32, name="wx%d" % c8, tag="w", align_bytes=64)
@@ -90,11 +94,6 @@ def tile_butterflymlp_w_kernel(
                     in_=W_exp_words[:, :, 512 * c8 : 512 * (c8 + 1), :].rearrange("g p n t -> p g (n t)").bitcast(I32),
                 )
                 wx.append(t)
-                if c8 == 1:
-                    load_raw(1, nc.sync)
-                    nc.sync.dma_start(out=zh[1][0:80, :], in_=bw[1][7:12].rearrange("s (k p) r l -> (s k) (p r l)", p=P))
-                    for h in range(4):
-                        nc.sync.dma_start(out=w7raw[:, h, :], in_=w7src[h])
 
             def copy_on(eng, o, i):
                 if eng == 0:
@@ -232,9 +231,13 @@ def tile_butterflymlp_w_kernel(
 
             def e1(c8):
                 h0 = tmp.tile([P, 4, TOK], F32, name="h0", tag="h0", bufs=3)
-                nc.vector.tensor_tensor(
-                    out=h0[:], in0=pms[c8][:], in1=bias32[:, 4 * c8 : 4 * c8 + 4].unsqueeze(2).to_broadcast([P, 4, TOK]), op=ALU.add
-                )
+                if c8 < 2:
+                    nc.vector.tensor_tensor(
+                        out=h0[:], in0=pms[c8][:], in1=bias32[:, 4 * c8 : 4 * c8 + 4].unsqueeze(2).to_broadcast([P, 4, TOK]), op=ALU.add
+                    )
+                else:
+                    for cl in range(4):
+                        nc.scalar.activation(out=h0[:, cl, :], in_=pms[c8][:, cl, :], func=ACT.Identity, bias=bias32[:, 4 * c8 + cl : 4 * c8 + cl + 1])
                 h0s[c8] = h0
 
             pes = {}
@@ -389,8 +392,7 @@ def tile_butterflymlp_w_kernel(
                 6: lambda: (g_out2(0, 0, 0, 1), g_out2(0, 1, 1, 1)),
                 7: lambda: (g_out2(0, 2, 7, 1), g_out2(0, 3, 0, 1)),
                 8: lambda: (g_out2(1, 0, 1, 1), g_out2(1, 1, 7, 1), g_out2(1, 2, 0, 1), g_out2(1, 3, 1, 1), wave(last_ops, (0,))),
-                9: lambda: (g3_out(0, 7), g3_prod(2), g3_out(1, 0), g3_prod(3), wave([(3, k) for k in range(8, 16)], (0,))),
-                10: lambda: (g3_out(2, 1), g3_prod(4), g3_out(3, 7), g3_prod(5)),
+                9: lambda: (wave([(3, k) for k in range(8, 16)], (0,)),),
             }
             for r in range(11):
                 if r + 2 < 8:
@@ -438,19 +440,17 @@ def tile_butterflymlp_w_kernel(
                         ta[:].rearrange("q b (g e z) -> q b g e z", g=8, e=2)[:, :, g, :, :],
                         pe[:].rearrange("q (e s) (b z) -> q (s b) e z", e=2, z=8),
                     )
-                if q < 2:
-                    g3_out(4 + 2 * q, 2)
-                    if q == 0:
-                        g3_prod(6)
-                        g3_prod(7)
-                    g3_out(5 + 2 * q, 3)
 
+            for q in range(8):
+                g3_out(q, (2, 3, 0, 1)[q % 4])
+                if q + 2 < 8:
+                    g3_prod(q + 2)
             nc.vector.tensor_tensor(out=bsum[:], in0=bc_b, in1=db_b, op=ALU.add)
 
         with tc.tile_pool(name="lpool", bufs=3) as lpool:
             hq = lpool.tile([P, 8 * TOK], U32, name="hq", bufs=1, align_bytes=64)
             hs = lpool.tile([P, 8 * TOK], U8, name="hs", bufs=1, align_bytes=64)
-            acc = [bank(n4, [P, 512]) for n4 in range(4)]
+            acc = {0: bank(0, [P, 512]), 1: bank(1, [P, 512])}
             d2 = buf_a
             trs = {}
             outs = {}
@@ -458,7 +458,7 @@ def tile_butterflymlp_w_kernel(
 
             def to_pi(h):
                 for half in range(2):
-                    pt = bank(4 + half, [P, 4, TOK])
+                    pt = bank((4, 2)[h % 2] + half, [P, 4, TOK])
                     for sl in range(4):
                         blk = 16 * (sl % 2) + 4 * h + 2 * half + sl // 2
                         nc.tensor.transpose(out=pt[:, sl, :], in_=ta[:, blk, :], identity=ident_f[:])
@@ -487,10 +487,10 @@ def tile_butterflymlp_w_kernel(
                         out=hq[:, 128 * s : 128 * (s + 1)].bitcast(FP8X4), scales=hs[:, 128 * s : 128 * (s + 1)], in_=hb[:].rearrange("m q t -> m (q t)")
                     )
 
-            def mx2(h):
+            def mx2(h, cols):
                 for f7 in range(2):
                     s = 4 * f7 + h
-                    for n4 in range(4):
+                    for n4 in cols:
                         nc.tensor.matmul_mx(
                             out=acc[n4][:],
                             lhsT=hq[:, 128 * s : 128 * (s + 1)].bitcast(FP8X4),
@@ -502,14 +502,22 @@ def tile_butterflymlp_w_kernel(
                         )
 
             to_pi(0)
+            to_pi(1)
             stage7(0)
             for h in range(4):
-                if h + 1 < 4:
-                    to_pi(h + 1)
                 stages8(h)
+                if h + 2 < 4:
+                    to_pi(h + 2)
                 if h + 1 < 4:
                     stage7(h + 1)
-                mx2(h)
+                if h < 3:
+                    mx2(h, (0, 1))
+                if h == 2:
+                    acc[2] = bank(4, [P, 512])
+                    acc[3] = bank(5, [P, 512])
+                    for hh in range(3):
+                        mx2(hh, (2, 3))
+            mx2(3, (0, 1, 2, 3))
             out2 = out.flatten_outer_dims()
             for n4 in range(4):
                 o_sb = lpool.tile([P, 512], F32, name="o_sb", tag="o_sb", bufs=4)

@@ -19,7 +19,7 @@ TOK = 128
 D_IN = 2048
 H = 4096
 NT = H // P
-V_SHARE = ()
+V_SHARE = (1,)
 FLOPS = 2 * 2 * TOK * D_IN * H + 24 * (H // 2) * 6 * TOK
 
 

@@ -282,6 +282,39 @@ def tile_butterflymlp_w_kernel(
                     out=dst, in0=ew_src(s5, cs[1 - side]), scalar=wh32[0][:, 16 * s5 + k, side, 1 - side : 2 - side], in1=dst, op0=ALU.mult, op1=ALU.add
                 )
 
+            early = {}
+
+            def ew_p1(s5, k):
+                ca, cb = pair_tiles(s5, k)
+                w = wh32[0][:, 16 * s5 + k, 1, 0:1]
+                o = early[s5][:, k if s5 == 4 else k - 8, :]
+                if k % 8 in V_SHARE:
+                    if s5 == 4:
+                        nc.vector.tensor_scalar(out=o, in0=ew_src(4, ca), scalar1=w, scalar2=bias32[:, 32 + cb : 33 + cb], op0=ALU.mult, op1=ALU.add)
+                    else:
+                        nc.vector.tensor_scalar(out=o, in0=ew_src(s5, ca), scalar1=w, scalar2=None, op0=ALU.mult)
+                elif s5 == 4:
+                    nc.scalar.activation(out=o, in_=ew_src(4, ca), func=ACT.Identity, scale=w, bias=bias32[:, 32 + cb : 33 + cb])
+                else:
+                    nc.scalar.activation(out=o, in_=ew_src(s5, ca), func=ACT.Copy, scale=w)
+
+            def ew_v1(s5, k):
+                ca, cb = pair_tiles(s5, k)
+                nc.vector.scalar_tensor_tensor(
+                    out=ew_bufs[s5 + 1][:, cb, :], in0=ew_src(s5, cb), scalar=wh32[0][:, 16 * s5 + k, 1, 1:2],
+                    in1=early[s5][:, k if s5 == 4 else k - 8, :], op0=ALU.mult, op1=ALU.add
+                )
+
+            def wave_early(ops):
+                for s5, k in ops:
+                    ew_p(s5, k, 0)
+                    ew_p1(s5, k)
+
+            def wave_v_early(ops):
+                for s5, k in ops:
+                    ew_v(s5, k, 0)
+                    ew_v1(s5, k)
+
             def wave(ops, sides=(0, 1)):
                 for s5, k in ops:
                     for side in sides:
@@ -391,16 +424,21 @@ def tile_butterflymlp_w_kernel(
                 2: lambda: (g_prod(0, nc.vector), g_prod(1, nc.vector), g_prod(2, nc.vector), g_prod(3, nc.vector), g3_small(), g3_prod(0), g3_prod(1)),
                 6: lambda: (g_out2(0, 0, 0, 1), g_out2(0, 1, 1, 1)),
                 7: lambda: (g_out2(0, 2, 7, 1), g_out2(0, 3, 0, 1)),
-                8: lambda: (g_out2(1, 0, 1, 1), g_out2(1, 1, 7, 1), g_out2(1, 2, 0, 1), g_out2(1, 3, 1, 1), wave(last_ops, (0,))),
-                9: lambda: (wave([(3, k) for k in range(8, 16)], (0,)),),
+                8: lambda: (g_out2(1, 0, 1, 1), g_out2(1, 1, 7, 1), g_out2(1, 2, 0, 1), g_out2(1, 3, 1, 1), wave_early(last_ops)),
+                9: lambda: (wave_early([(3, k) for k in range(8, 16)]),),
             }
-            for r in range(11):
+            for r in range(10):
                 if r + 2 < 8:
                     mx1(r + 2)
                 if r < 8:
                     pe1(r)
                 ops = ops_in_round(r)
-                wave(ops, (1,) if r == 10 else (0, 1))
+                if r == 8:
+                    early[4] = g_mats[0][:, 0:16, :]
+                if r == 9:
+                    e10 = grp.tile([P, 1024], F32, name="e10", tag="gr", align_bytes=64)
+                    early[3] = e10[:].rearrange("p (k q) -> p k q", k=8)
+                wave(ops)
                 wave_v(ops)
                 if r + 2 < 8:
                     e1(r + 2)
@@ -425,14 +463,15 @@ def tile_butterflymlp_w_kernel(
 
             gl = buf_b
             ta = buf_c
-            wave(last_ops, (1,))
-            for q in range(4):
-                wave_v(last_ops[4 * q : 4 * q + 4])
+            for seq, q in enumerate((0, 2, 1, 3)):
+                if seq % 2 == 0:
+                    wave_v_early([(3, k) for k in range(8 + 2 * seq, 12 + 2 * seq)])
+                wave_v_early(last_ops[4 * q : 4 * q + 4])
                 for hi in range(2):
                     c0 = 4 * q + 16 * hi
                     g = q + 4 * hi
                     nc.scalar.activation(out=gl[:, c0 : c0 + 4, :], in_=buf_a[:, c0 : c0 + 4, :], func=ACT.Gelu)
-                    pe = bank(4 + 2 * (q % 2) + hi, [P, 4, P])
+                    pe = bank(4 + 2 * (seq % 2) + hi, [P, 4, P])
                     for cl in range(4):
                         nc.tensor.matmul(out=pe[:, cl, :], lhsT=gl[:, c0 + cl, :], rhs=g_mats[1][:, c0 + cl, :], start=True, stop=True)
                     copy_on(

@@ -419,7 +419,7 @@ def tile_butterflymlp_w_kernel(
 
             last_ops = [(4, k) for k in range(16)]
             extra = {
-                0: lambda: g_copies(1, (0, 1, 2, 6, 5, 4, 3), 1),
+                0: lambda: (g_copies(1, (0, 1, 2, 3, 4), 0), g_copies(1, (6, 5), 1)),
                 1: lambda: (g_x(nc.vector), g_y(nc.vector), wh_path(1, 0, 1), nc.scalar.copy(out=w7f[:].rearrange("p a r l -> p (a r l)"), in_=w7raw[:].rearrange("p h e -> p (h e)"))),
                 2: lambda: (g_prod(0, nc.vector), g_prod(1, nc.vector), g_prod(2, nc.vector), g_prod(3, nc.vector), g3_small(), g3_prod(0), g3_prod(1)),
                 6: lambda: (g_out2(0, 0, 0, 1), g_out2(0, 1, 1, 1)),
@@ -504,12 +504,18 @@ def tile_butterflymlp_w_kernel(
                         trs[blk] = pt[:, sl, :]
 
             def stage7(h):
+                if h == 0:
+                    for t in range(4):
+                        w = w7f[:, t, :, :]
+                        nc.scalar.activation(out=d2[:, t, :], in_=trs[t], func=ACT.Copy, scale=w[:, 0, 0:1])
+                        nc.scalar.activation(out=d2[:, t + 16, :], in_=trs[t + 16], func=ACT.Copy, scale=w[:, 1, 1:2])
                 for t in range(4):
                     ba = 4 * h + t
                     bb = ba + 16
                     w = w7f[:, 4 * h + t, :, :]
-                    nc.vector.tensor_scalar(out=d2[:, ba, :], in0=trs[ba], scalar1=w[:, 0, 0:1], scalar2=None, op0=ALU.mult)
-                    nc.vector.tensor_scalar(out=d2[:, bb, :], in0=trs[bb], scalar1=w[:, 1, 1:2], scalar2=None, op0=ALU.mult)
+                    if h > 0:
+                        nc.vector.tensor_scalar(out=d2[:, ba, :], in0=trs[ba], scalar1=w[:, 0, 0:1], scalar2=None, op0=ALU.mult)
+                        nc.vector.tensor_scalar(out=d2[:, bb, :], in0=trs[bb], scalar1=w[:, 1, 1:2], scalar2=None, op0=ALU.mult)
                     nc.vector.scalar_tensor_tensor(out=d2[:, ba, :], in0=trs[bb], scalar=w[:, 0, 1:2], in1=d2[:, ba, :], op0=ALU.mult, op1=ALU.add)
                     nc.vector.scalar_tensor_tensor(out=d2[:, bb, :], in0=trs[ba], scalar=w[:, 1, 0:1], in1=d2[:, bb, :], op0=ALU.mult, op1=ALU.add)
 

from contextlib import ExitStack

import concourse.bass as bass
import concourse.mybir as mybir
import concourse.tile as tile
from concourse.masks import make_identity

F32 = mybir.dt.float32
BF16 = mybir.dt.bfloat16
I32 = mybir.dt.int32
U32 = mybir.dt.uint32
U8 = mybir.dt.uint8
FP8X4 = mybir.dt.float8_e4m3fn_x4
ALU = mybir.AluOpType
ACT = mybir.ActivationFunctionType

P = 128
TOK = 128
D_IN = 2048
H = 4096
NT = H // P
V_SHARE = (1,)
FLOPS = 2 * 2 * TOK * D_IN * H + 24 * (H // 2) * 6 * TOK


def tile_butterflymlp_w_kernel(
    tc, x, W_exp_words, W_exp_scales, b_exp, up_weights, up_bias, down_weights, W_con_words, W_con_scales, b_con, down_bias, out
):
    nc = tc.nc
    with ExitStack() as ctx:
        const = ctx.enter_context(tc.tile_pool(name="const", bufs=1))
        wpool = ctx.enter_context(tc.tile_pool(name="wpool", bufs=8))
        psum = ctx.enter_context(tc.psum_pool(name="psum", bufs=1))

        def bank(i, shape, dtype=F32):
            return psum.tile(shape, dtype, name="bk%d" % i, tag="bk%d" % i)

        ident_f = const.tile([P, P], F32, name="ident_f")
        make_identity(nc, ident_f[:])
        ident_b = const.tile([P, P], BF16, name="ident_b")
        make_identity(nc, ident_b[:])
        warm = const.tile([P, 1], F32, name="warm")
        nc.vector.memset(warm[:], 0.0)
        nc.scalar.activation(out=warm[:], in_=warm[:], func=ACT.Gelu)
        pl_exp = const.tile([P, H], U8, name="pl_exp", align_bytes=64)
        nc.vector.memset(pl_exp[:].bitcast(I32), 0)
        pl_con = const.tile([P, 2, D_IN], U8, name="pl_con", align_bytes=64)
        g_mats = [const.tile([P, NT, P], F32, name="g_up"), const.tile([P, NT, P], F32, name="g_down")]
        g3 = const.tile([P, 32, P], F32, name="g3")
        wh32 = [const.tile([P, 80, 2, 2], F32, name="wh_up"), const.tile([P, 80, 2, 2], F32, name="wh_down")]
        bias32 = const.tile([P, P], F32, name="bias32")
        xq = const.tile([P, 4 * TOK], U32, name="xq", align_bytes=64)
        xs = const.tile([P, 4 * TOK], U8, name="xs", align_bytes=64)
        buf_a = const.tile([P, NT, TOK], F32, name="buf_a")
        buf_b = const.tile([P, NT, TOK], F32, name="buf_b")
        buf_c = const.tile([P, NT, TOK], F32, name="buf_c")
        bsum = const.tile([P, D_IN], F32, name="bsum")
        w7f = const.tile([P, 16, 2, 2], F32, name="w7f")

        with tc.tile_pool(name="tmp", bufs=1) as tmp, tc.tile_pool(name="grp", bufs=4) as grp:
            bw = (up_weights, down_weights)
            raw = [tmp.tile([P, 7, 256], BF16, name="raw_up"), tmp.tile([P, 7, 256], BF16, name="raw_down")]

            def load_raw(b, queue):
                src = bw[b][0:7].rearrange("s (c k) r l -> c s (k r l)", c=NT)
                for h in range(4):
                    queue.dma_start(out=raw[b][32 * h : 32 * h + 32, :, :], in_=src)

            load_raw(0, nc.sync)
            x_sb = grp.tile([P, D_IN], BF16, name="x_sb", tag="gr", align_bytes=64)
            nc.sync.dma_start(out=x_sb[:], in_=x.flatten_outer_dims())
            vb = tmp.tile([P, P], BF16, name="vb")
            nc.vector.memset(vb[64:128, :], 0.0)
            zh = [tmp.tile([P, 512], BF16, name="zh_up"), tmp.tile([P, 512], BF16, name="zh_down")]
            for b in range(2):
                nc.vector.memset(zh[b][64:128, :], 0.0)
            nc.vector.memset(pl_con[:].rearrange("p h n -> p (h n)").bitcast(I32), 0)
            nc.sync.dma_start(out=vb[0:32, :], in_=b_exp.rearrange("(c p) -> c p", p=P))
            nc.sync.dma_start(out=vb[32:64, :], in_=up_bias.rearrange("(c p) -> c p", p=P))
            nc.sync.dma_start(out=zh[0][0:80, :], in_=bw[0][7:12].rearrange("s (k p) r l -> (s k) (p r l)", p=P))
            for q in range(4):
                nc.sync.dma_start(out=pl_exp[32 * q : 32 * q + 16, :].bitcast(I32), in_=W_exp_scales[:, 4 * q : 4 * q + 4, :].bitcast(I32))
            w7raw = tmp.tile([P, 4, 16], BF16, name="w7raw")
            w7src = bw[1][7].rearrange("(c h z t) r l -> h c z (t r l)", c=16, h=4, z=8)
            load_raw(1, nc.sync)
            nc.sync.dma_start(out=zh[1][0:80, :], in_=bw[1][7:12].rearrange("s (k p) r l -> (s k) (p r l)", p=P))
            for h in range(4):
                nc.sync.dma_start(out=w7raw[:, h, :], in_=w7src[h])
            wx = []
            for c8 in range(8):
                t = wpool.tile([P, 4, 512], U32, name="wx%d" % c8, tag="w", align_bytes=64)
                nc.sync.dma_start(
                    out=t[:].bitcast(I32),
                    in_=W_exp_words[:, :, 512 * c8 : 512 * (c8 + 1), :].rearrange("g p n t -> p g (n t)").bitcast(I32),
                )
                wx.append(t)

            def copy_on(eng, o, i):
                if eng == 0:
                    nc.vector.tensor_copy(out=o, in_=i)
                else:
                    nc.scalar.copy(out=o, in_=i)

            fp = tmp.tile([P, 7, 256], BF16, name="fp")

            def g_copies(b, stages, eng):
                for s in stages:
                    if s <= 4:
                        o = fp[:, s, :].rearrange("p (r b a l) -> p r b a l", r=2, b=2**s, a=2 ** (6 - s), l=2)
                        i = raw[b][:, s, :].rearrange("p (a b r l) -> p r b a l", a=2 ** (6 - s), b=2**s, r=2, l=2)
                        if eng == 0:
                            nc.vector.tensor_copy(out=o, in_=i)
                        else:
                            for r in range(2):
                                nc.scalar.copy(out=o[:, r], in_=i[:, r])
                    elif s == 5:
                        for h in range(4):
                            q = slice(32 * h, 32 * h + 32)
                            copy_on(
                                eng,
                                fp[q, 5, 0:128].rearrange("p (b a l) -> p b a l", b=32, a=2, l=2),
                                raw[b][q, 5, :].rearrange("p (a b r l) -> p r b a l", a=2, b=32, r=2, l=2)[:, h % 2],
                            )
                    else:
                        for h in range(4):
                            q = slice(32 * h, 32 * h + 32)
                            copy_on(
                                eng,
                                fp[q, 6, 0:64].rearrange("p (b l) -> p b l", l=2),
                                raw[b][q, 6, :].rearrange("p (t b r l) -> p t r b l", t=2, b=32, r=2, l=2)[:, h % 2, h // 2],
                            )

            xrec = [None, tmp.tile([P, 512], F32, name="xrec1"), tmp.tile([P, 1024], F32, name="xrec2")]
            yrec = {5: tmp.tile([P, 128], F32, name="yrec5"), 4: tmp.tile([P, 256], F32, name="yrec4"), 3: tmp.tile([P, 512], F32, name="yrec3")}

            def g_x(ve):
                prev = fp[:, 0, :]
                for s in (1, 2):
                    shp = [P, 2, 128, 2**s]
                    ve.tensor_tensor(
                        out=xrec[s][:].rearrange("p (u m w) -> p u m w", u=2, w=2**s),
                        in0=prev.rearrange("p (m w) -> p m w", w=2**s).unsqueeze(1).to_broadcast(shp),
                        in1=fp[:, s, :].rearrange("p (u m) -> p u m", u=2).unsqueeze(3).to_broadcast(shp),
                        op=ALU.mult,
                    )
                    prev = xrec[s][:]

            def g_y(ve):
                prev = fp[:, 6, 0:64]
                for s in (5, 4, 3):
                    u = 2 if s == 3 else 1
                    m = 64 if s == 5 else 128
                    shp = [P, u, m, 2]
                    ve.tensor_tensor(
                        out=yrec[s][:].rearrange("p (u m w) -> p u m w", u=u, w=2),
                        in0=prev.rearrange("p (u m) -> p u m", u=u).unsqueeze(3).to_broadcast(shp),
                        in1=fp[:, s, 0 : 2 * m].rearrange("p (m w) -> p m w", w=2).unsqueeze(1).to_broadcast(shp),
                        op=ALU.mult,
                    )
                    prev = yrec[s][:]

            grs = {}

            def g_prod(u, ve):
                gr = grp.tile([P, 1024], F32, name="gr", tag="gr", align_bytes=64)
                ve.tensor_tensor(
                    out=gr[:].rearrange("p (m w) -> p m w", w=8),
                    in0=xrec[2][:].rearrange("p (m w) -> p m w", w=8),
                    in1=yrec[3][:, 128 * u : 128 * (u + 1)].unsqueeze(2).to_broadcast([P, 128, 8]),
                    op=ALU.mult,
                )
                grs[u] = gr

            def g_out(b, u, banks, eng):
                for vh in range(2):
                    pt = bank(banks[vh], [P, 4, P])
                    for sl in range(4):
                        v = 4 * vh + sl
                        nc.tensor.transpose(out=pt[:, sl, :], in_=grs[u][:, 128 * v : 128 * (v + 1)], identity=ident_f[:])
                    il0 = 8 * u + 4 * vh
                    copy_on(
                        eng,
                        g_mats[b][:].rearrange("p c (h i) -> p c h i", h=4)[:, :, :, il0 : il0 + 4],
                        pt[:].rearrange("p s (h c) -> p c h s", h=4),
                    )

            def wh_path(b, bk, eng):
                pz = bank(bk, [P, 2, P])
                zw = zh[b][:].bitcast(F32)
                for r in range(2):
                    nc.tensor.transpose(out=pz[:, r, :], in_=zw[:, r:256:2], identity=ident_f[:])
                copy_on(eng, wh32[b][:], pz[:].bitcast(BF16).rearrange("p r (w l) -> p w r l", l=2)[:, 0:80, :, :])

            g_copies(0, (0, 1, 2), 0)
            g_copies(0, (6, 5, 4, 3), 1)
            g_x(nc.vector)
            xw = x_sb[:].bitcast(F32)
            xg = grp.tile([P, 4, TOK, 4], BF16, name="xg", tag="gr", align_bytes=64)
            for h in range(2):
                px = bank(h, [P, 2, 2, TOK])
                for g2 in range(2):
                    g = 2 * h + g2
                    for u in range(2):
                        nc.tensor.transpose(out=px[:, g2, u, :], in_=xw[:, 256 * g + u : 256 * (g + 1) : 2], identity=ident_f[:])
                nc.scalar.copy(out=xg[:, 2 * h : 2 * h + 2, :, :].bitcast(F32), in_=px[:].rearrange("p g u q -> p g q u"))
            g_y(nc.vector)
            nc.vector.quantize_mx(out=xq[:].bitcast(FP8X4), scales=xs[:], in_=xg[:].rearrange("p g q t -> p (g q t)"))
            pb = bank(7, [P, P], BF16)
            nc.tensor.transpose(out=pb[:], in_=vb[:], identity=ident_b[:])
            nc.scalar.copy(out=bias32[:], in_=pb[:])
            wh_path(0, 6, 1)

            h0s = {}
            pms = {}

            def mx1(c8):
                pm = bank(2 + c8 % 2, [P, 4, TOK])
                for cl in range(4):
                    c = 4 * c8 + cl
                    for g in range(4):
                        nc.tensor.matmul_mx(
                            out=pm[:, cl, :],
                            lhsT=wx[c8][:, g, 128 * cl : 128 * (cl + 1)].bitcast(FP8X4),
                            lhsT_scale=pl_exp[4 * g : 128, 128 * c : 128 * (c + 1)],
                            rhs=xq[:, 128 * g : 128 * (g + 1)].bitcast(FP8X4),
                            rhs_scale=xs[:, 128 * g : 128 * (g + 1)],
                            start=(g == 0),
                            stop=(g == 3),
                        )
                pms[c8] = pm

            def e1(c8):
                h0 = tmp.tile([P, 4, TOK], F32, name="h0", tag="h0", bufs=3)
                if c8 < 2:
                    nc.vector.tensor_tensor(
                        out=h0[:], in0=pms[c8][:], in1=bias32[:, 4 * c8 : 4 * c8 + 4].unsqueeze(2).to_broadcast([P, 4, TOK]), op=ALU.add
                    )
                else:
                    for cl in range(4):
                        nc.scalar.activation(out=h0[:, cl, :], in_=pms[c8][:, cl, :], func=ACT.Identity, bias=bias32[:, 4 * c8 + cl : 4 * c8 + cl + 1])
                h0s[c8] = h0

            pes = {}

            def pe1(c8):
                pe = bank(4 + c8 % 3, [P, 4, TOK])
                for cl in range(4):
                    nc.tensor.matmul(out=pe[:, cl, :], lhsT=g_mats[0][:, 4 * c8 + cl, :], rhs=h0s[c8][:, cl, :], start=True, stop=True)
                pes[c8] = pe

            def pair_tiles(s5, k):
                lo = k & (2**s5 - 1)
                ca = ((k >> s5) << (s5 + 1)) + lo
                return ca, ca + 2**s5

            ew_bufs = [None, buf_a, buf_b, buf_a, buf_b, buf_a]

            def ew_src(s5, c):
                if s5 == 0:
                    return pes[c // 4][:, c % 4, :]
                return ew_bufs[s5][:, c, :]

            def ew_p(s5, k, side):
                c = pair_tiles(s5, k)[side]
                if k % 8 in V_SHARE:
                    w = wh32[0][:, 16 * s5 + k, side, side : side + 1]
                    if s5 == 4:
                        nc.vector.tensor_scalar(out=ew_bufs[5][:, c, :], in0=ew_src(4, c), scalar1=w, scalar2=bias32[:, 32 + c : 33 + c], op0=ALU.mult, op1=ALU.add)
                    else:
                        nc.vector.tensor_scalar(out=ew_bufs[s5 + 1][:, c, :], in0=ew_src(s5, c), scalar1=w, scalar2=None, op0=ALU.mult)
                elif s5 == 4:
                    nc.scalar.activation(
                        out=ew_bufs[5][:, c, :], in_=ew_src(4, c), func=ACT.Identity, scale=wh32[0][:, 64 + k, side, side : side + 1], bias=bias32[:, 32 + c : 33 + c]
                    )
                else:
                    nc.scalar.activation(out=ew_bufs[s5 + 1][:, c, :], in_=ew_src(s5, c), func=ACT.Copy, scale=wh32[0][:, 16 * s5 + k, side, side : side + 1])

            def ew_v(s5, k, side):
                cs = pair_tiles(s5, k)
                dst = ew_bufs[s5 + 1][:, cs[side], :]
                nc.vector.scalar_tensor_tensor(
                    out=dst, in0=ew_src(s5, cs[1 - side]), scalar=wh32[0][:, 16 * s5 + k, side, 1 - side : 2 - side], in1=dst, op0=ALU.mult, op1=ALU.add
                )

            early = {}

            def ew_p1(s5, k):
                ca, cb = pair_tiles(s5, k)
                w = wh32[0][:, 16 * s5 + k, 1, 0:1]
                o = early[s5][:, k if s5 == 4 else k - 8, :]
                if k % 8 in V_SHARE:
                    if s5 == 4:
                        nc.vector.tensor_scalar(out=o, in0=ew_src(4, ca), scalar1=w, scalar2=bias32[:, 32 + cb : 33 + cb], op0=ALU.mult, op1=ALU.add)
                    else:
                        nc.vector.tensor_scalar(out=o, in0=ew_src(s5, ca), scalar1=w, scalar2=None, op0=ALU.mult)
                elif s5 == 4:
                    nc.scalar.activation(out=o, in_=ew_src(4, ca), func=ACT.Identity, scale=w, bias=bias32[:, 32 + cb : 33 + cb])
                else:
                    nc.scalar.activation(out=o, in_=ew_src(s5, ca), func=ACT.Copy, scale=w)

            def ew_v1(s5, k):
                ca, cb = pair_tiles(s5, k)
                nc.vector.scalar_tensor_tensor(
                    out=ew_bufs[s5 + 1][:, cb, :], in0=ew_src(s5, cb), scalar=wh32[0][:, 16 * s5 + k, 1, 1:2],
                    in1=early[s5][:, k if s5 == 4 else k - 8, :], op0=ALU.mult, op1=ALU.add
                )

            def wave_early(ops):
                for s5, k in ops:
                    ew_p(s5, k, 0)
                    ew_p1(s5, k)

            def wave_v_early(ops):
                for s5, k in ops:
                    ew_v(s5, k, 0)
                    ew_v1(s5, k)

            def wave(ops, sides=(0, 1)):
                for s5, k in ops:
                    for side in sides:
                        ew_p(s5, k, side)
                return ops

            def wave_v(ops):
                for s5, k in ops:
                    for side in (0, 1):
                        ew_v(s5, k, side)

            g_prod(0, nc.vector)
            g_prod(1, nc.vector)
            g_out(0, 0, (0, 1), 1)
            mx1(0)
            g_prod(2, nc.vector)
            g_out(0, 1, (7, 0), 1)
            mx1(1)
            g_prod(3, nc.vector)
            g_out(0, 2, (1, 7), 1)
            e1(0)
            g_out(0, 3, (0, 1), 1)
            e1(1)

            zmask = tmp.tile([P, 8], F32, name="zmask")
            fh = xrec[1][:, 0:256].rearrange("p (s f e) -> p s f e", s=4, f=2)
            hx = yrec[5][:, 0:128].rearrange("p (f e) -> p f e", f=2)
            hy = yrec[4][:, 0:128].rearrange("p (f e) -> p f e", f=2)
            hmat = xrec[2][:, 0:512]

            def g3_small():
                nc.vector.tensor_reduce(out=zmask[:], in_=ident_f[:].rearrange("p (h z t) -> p z h t", h=4, z=8), axis=mybir.AxisListType.XY, op=ALU.add)
                for s in range(4):
                    for f in range(2):
                        nc.vector.tensor_copy(
                            out=fh[:, s, f, :].rearrange("p (r b a l) -> p r b a l", r=2, b=2**s, a=2 ** (3 - s), l=2),
                            in_=wh32[1][:, 16 * (s + 1) : 16 * (s + 2), :, :].rearrange("p (a b f) r l -> p f r b a l", a=2 ** (3 - s), b=2**s, f=2)[:, f],
                        )
                for f in range(2):
                    nc.vector.tensor_tensor(
                        out=hx[:, f, :].rearrange("p (u m w) -> p u m w", u=2, w=2),
                        in0=fh[:, 0, f, :].rearrange("p (m w) -> p m w", w=2).unsqueeze(1).to_broadcast([P, 2, 16, 2]),
                        in1=fh[:, 1, f, :].rearrange("p (u m) -> p u m", u=2).unsqueeze(3).to_broadcast([P, 2, 16, 2]),
                        op=ALU.mult,
                    )
                    nc.vector.tensor_tensor(
                        out=hy[:, f, :].rearrange("p (u m w) -> p u m w", u=2, w=2),
                        in0=fh[:, 3, f, :].rearrange("p (u m) -> p u m", u=2).unsqueeze(3).to_broadcast([P, 2, 16, 2]),
                        in1=fh[:, 2, f, :].rearrange("p (m w) -> p m w", w=2).unsqueeze(1).to_broadcast([P, 2, 16, 2]),
                        op=ALU.mult,
                    )
                    nc.vector.tensor_tensor(
                        out=hmat[:, 256 * f : 256 * (f + 1)].rearrange("p (u m w) -> p u m w", u=4, w=4),
                        in0=hx[:, f, :].rearrange("p (m w) -> p m w", w=4).unsqueeze(1).to_broadcast([P, 4, 16, 4]),
                        in1=hy[:, f, :].rearrange("p (u m) -> p u m", u=4).unsqueeze(3).to_broadcast([P, 4, 16, 4]),
                        op=ALU.mult,
                    )

            exs = {}

            def g3_prod(q):
                ex = tmp.tile([P, 512], F32, name="ex", tag="ex", bufs=2)
                nc.vector.tensor_tensor(
                    out=ex[:].rearrange("p (a z) -> p a z", z=8),
                    in0=hmat[:, 64 * q : 64 * (q + 1)].unsqueeze(2).to_broadcast([P, 64, 8]),
                    in1=zmask[:].unsqueeze(1).to_broadcast([P, 64, 8]),
                    op=ALU.mult,
                )
                exs[q] = ex

            def g3_out(q, bk):
                pt = bank(bk, [P, 4, P])
                for sl in range(4):
                    nc.tensor.transpose(out=pt[:, sl, :], in_=exs[q][:, 128 * sl : 128 * (sl + 1)], identity=ident_f[:])
                nc.vector.tensor_copy(
                    out=g3[:].rearrange("p (f h t) (i z) -> p f h t i z", f=2, h=4, z=8)[:, q // 4, :, :, 4 * (q % 4) : 4 * (q % 4) + 4, :],
                    in_=pt[:].rearrange("p s (h z t) -> p h t s z", h=4, z=8),
                )

            def g_out2(i4, t, bk, eng):
                pt = bank(bk, [P, 4, P])
                for sl in range(4):
                    v = 4 * (sl % 2) + t
                    nc.tensor.transpose(out=pt[:, sl, :], in_=grs[2 * i4 + sl // 2][:, 128 * v : 128 * (v + 1)], identity=ident_f[:])
                copy_on(
                    eng,
                    g_mats[1][:].rearrange("p c (h t z) -> p c h t z", h=4, t=4)[:, :, :, t, 4 * i4 : 4 * i4 + 4],
                    pt[:].rearrange("p s (h c) -> p c h s", h=4),
                )

            def ops_in_round(r):
                ops = []
                if r in (6, 10):
                    ops += [(3, k) for k in range(2 * (r - 6), 2 * (r - 6) + 8)]
                if r in (3, 5, 7, 9):
                    ops += [(2, k) for k in range(2 * (r - 3), 2 * (r - 3) + 4)]
                if 1 <= r <= 8:
                    ops += [(1, 2 * r - 2), (1, 2 * r - 1)]
                if r <= 7:
                    ops += [(0, 2 * r), (0, 2 * r + 1)]
                return ops

            last_ops = [(4, k) for k in range(16)]
            extra = {
                0: lambda: (g_copies(1, (0, 1, 2, 3, 4), 0), g_copies(1, (6, 5), 1)),
                1: lambda: (g_x(nc.vector), g_y(nc.vector), wh_path(1, 0, 1), nc.scalar.copy(out=w7f[:].rearrange("p a r l -> p (a r l)"), in_=w7raw[:].rearrange("p h e -> p (h e)"))),
                2: lambda: (g_prod(0, nc.vector), g_prod(1, nc.vector), g_prod(2, nc.vector), g_prod(3, nc.vector), g3_small(), g3_prod(0), g3_prod(1)),
                6: lambda: (g_out2(0, 0, 0, 1), g_out2(0, 1, 1, 1)),
                7: lambda: (g_out2(0, 2, 7, 1), g_out2(0, 3, 0, 1)),
                8: lambda: (g_out2(1, 0, 1, 1), g_out2(1, 1, 7, 1), g_out2(1, 2, 0, 1), g_out2(1, 3, 1, 1), wave_early(last_ops)),
                9: lambda: (wave_early([(3, k) for k in range(8, 16)]),),
            }
            for r in range(10):
                if r + 2 < 8:
                    mx1(r + 2)
                if r < 8:
                    pe1(r)
                ops = ops_in_round(r)
                if r == 8:
                    early[4] = g_mats[0][:, 0:16, :]
                if r == 9:
                    e10 = grp.tile([P, 1024], F32, name="e10", tag="gr", align_bytes=64)
                    early[3] = e10[:].rearrange("p (k q) -> p k q", k=8)
                wave(ops)
                wave_v(ops)
                if r + 2 < 8:
                    e1(r + 2)
                if r in extra:
                    extra[r]()

            bc_b = g_mats[0][:, 16:24, :].rearrange("p c i -> p (c i)").bitcast(BF16)
            db_b = g_mats[0][:, 24:32, :].rearrange("p c i -> p (c i)").bitcast(BF16)
            nc.gpsimd.dma_start(out=bc_b, in_=b_con.partition_broadcast(P))
            nc.gpsimd.dma_start(out=db_b, in_=down_bias.partition_broadcast(P))

            sc_view = W_con_scales.rearrange("g (e s) n -> s (g e) n", e=2, s=8)
            for h in range(2):
                for q in range(4):
                    nc.sync.dma_start(out=pl_con[32 * q : 32 * q + 16, h, :].bitcast(I32), in_=sc_view[4 * h : 4 * h + 4, 4 * q : 4 * q + 4, :].bitcast(I32))
            wc_view = W_con_words.rearrange("g (e s l) n t -> s (g e) l (n t)", e=2, s=8, l=8)
            wc = []
            for s in range(8):
                t = wpool.tile([P, D_IN], U32, name="wc%d" % s, tag="w", align_bytes=64)
                nc.sync.dma_start(out=t[:].bitcast(I32), in_=wc_view[s].bitcast(I32))
                wc.append(t)

            gl = buf_b
            ta = buf_c
            for seq, q in enumerate((0, 2, 1, 3)):
                if seq % 2 == 0:
                    wave_v_early([(3, k) for k in range(8 + 2 * seq, 12 + 2 * seq)])
                wave_v_early(last_ops[4 * q : 4 * q + 4])
                for hi in range(2):
                    c0 = 4 * q + 16 * hi
                    g = q + 4 * hi
                    nc.scalar.activation(out=gl[:, c0 : c0 + 4, :], in_=buf_a[:, c0 : c0 + 4, :], func=ACT.Gelu)
                    pe = bank(4 + 2 * (seq % 2) + hi, [P, 4, P])
                    for cl in range(4):
                        nc.tensor.matmul(out=pe[:, cl, :], lhsT=gl[:, c0 + cl, :], rhs=g_mats[1][:, c0 + cl, :], start=True, stop=True)
                    copy_on(
                        1,
                        ta[:].rearrange("q b (g e z) -> q b g e z", g=8, e=2)[:, :, g, :, :],
                        pe[:].rearrange("q (e s) (b z) -> q (s b) e z", e=2, z=8),
                    )

            for q in range(8):
                g3_out(q, (2, 3, 0, 1)[q % 4])
                if q + 2 < 8:
                    g3_prod(q + 2)
            nc.vector.tensor_tensor(out=bsum[:], in0=bc_b, in1=db_b, op=ALU.add)

        with tc.tile_pool(name="lpool", bufs=3) as lpool:
            hq = lpool.tile([P, 8 * TOK], U32, name="hq", bufs=1, align_bytes=64)
            hs = lpool.tile([P, 8 * TOK], U8, name="hs", bufs=1, align_bytes=64)
            acc = {0: bank(0, [P, 512]), 1: bank(1, [P, 512])}
            d2 = buf_a
            trs = {}
            outs = {}
            hbs = {}

            def to_pi(h):
                for half in range(2):
                    pt = bank((4, 2)[h % 2] + half, [P, 4, TOK])
                    for sl in range(4):
                        blk = 16 * (sl % 2) + 4 * h + 2 * half + sl // 2
                        nc.tensor.transpose(out=pt[:, sl, :], in_=ta[:, blk, :], identity=ident_f[:])
                        trs[blk] = pt[:, sl, :]

            def stage7(h):
                if h == 0:
                    for t in range(4):
                        w = w7f[:, t, :, :]
                        nc.scalar.activation(out=d2[:, t, :], in_=trs[t], func=ACT.Copy, scale=w[:, 0, 0:1])
                        nc.scalar.activation(out=d2[:, t + 16, :], in_=trs[t + 16], func=ACT.Copy, scale=w[:, 1, 1:2])
                for t in range(4):
                    ba = 4 * h + t
                    bb = ba + 16
                    w = w7f[:, 4 * h + t, :, :]
                    if h > 0:
                        nc.vector.tensor_scalar(out=d2[:, ba, :], in0=trs[ba], scalar1=w[:, 0, 0:1], scalar2=None, op0=ALU.mult)
                        nc.vector.tensor_scalar(out=d2[:, bb, :], in0=trs[bb], scalar1=w[:, 1, 1:2], scalar2=None, op0=ALU.mult)
                    nc.vector.scalar_tensor_tensor(out=d2[:, ba, :], in0=trs[bb], scalar=w[:, 0, 1:2], in1=d2[:, ba, :], op0=ALU.mult, op1=ALU.add)
                    nc.vector.scalar_tensor_tensor(out=d2[:, bb, :], in0=trs[ba], scalar=w[:, 1, 0:1], in1=d2[:, bb, :], op0=ALU.mult, op1=ALU.add)

            def stages8(h):
                for f7 in range(2):
                    po = bank(6 + f7, [P, 4, TOK])
                    for t in range(4):
                        blk = 16 * f7 + 4 * h + t
                        nc.tensor.matmul(out=po[:, t, :], lhsT=g3[:, blk, :], rhs=d2[:, blk, :], start=True, stop=True)
                    s = 4 * f7 + h
                    hb = lpool.tile([P, TOK, 4], BF16, name="hb", tag="hb", align_bytes=64)
                    nc.scalar.copy(out=hb[:], in_=po[:].rearrange("m t q -> m q t"))
                    nc.vector.quantize_mx(
                        out=hq[:, 128 * s : 128 * (s + 1)].bitcast(FP8X4), scales=hs[:, 128 * s : 128 * (s + 1)], in_=hb[:].rearrange("m q t -> m (q t)")
                    )

            def mx2(h, cols):
                for f7 in range(2):
                    s = 4 * f7 + h
                    for n4 in cols:
                        nc.tensor.matmul_mx(
                            out=acc[n4][:],
                            lhsT=hq[:, 128 * s : 128 * (s + 1)].bitcast(FP8X4),
                            lhsT_scale=hs[:, 128 * s : 128 * (s + 1)],
                            rhs=wc[s][:, 512 * n4 : 512 * (n4 + 1)].bitcast(FP8X4),
                            rhs_scale=pl_con[4 * (s % 4) : 128, s // 4, 512 * n4 : 512 * (n4 + 1)],
                            start=(h == 0 and f7 == 0),
                            stop=(h == 3 and f7 == 1),
                        )

            to_pi(0)
            to_pi(1)
            stage7(0)
            for h in range(4):
                stages8(h)
                if h + 2 < 4:
                    to_pi(h + 2)
                if h + 1 < 4:
                    stage7(h + 1)
                if h < 3:
                    mx2(h, (0, 1))
                if h == 2:
                    acc[2] = bank(4, [P, 512])
                    acc[3] = bank(5, [P, 512])
                    for hh in range(3):
                        mx2(hh, (2, 3))
            mx2(3, (0, 1, 2, 3))
            out2 = out.flatten_outer_dims()
            for n4 in range(4):
                o_sb = lpool.tile([P, 512], F32, name="o_sb", tag="o_sb", bufs=4)
                nc.vector.tensor_tensor(out=o_sb[:], in0=acc[n4][:], in1=bsum[:, 512 * n4 : 512 * (n4 + 1)], op=ALU.add)
                nc.sync.dma_start(out=out2[:, 512 * n4 : 512 * (n4 + 1)], in_=o_sb[:])
